import numpy as np
import ml_dtypes


def mxq(x, axis, fmt="e4m3"):
    dtype, down = {"e4m3": (ml_dtypes.float8_e4m3fn, 7), "e5m2": (ml_dtypes.float8_e5m2, 14)}[fmt]
    v = np.moveaxis(np.asarray(x, np.float32).astype(ml_dtypes.bfloat16).astype(np.float64), axis, -1)
    blocks = v.reshape(v.shape[:-1] + (-1, 32))
    amax = np.abs(blocks).max(-1, keepdims=True)
    byte = np.maximum(np.where(amax > 0, np.frexp(amax)[1] - 1 + 127, 0) - down, 1)
    scale = np.exp2(byte - 127.0)
    codes = (blocks / scale).astype(np.float32).astype(dtype).astype(np.float64)
    return np.moveaxis((codes * scale).reshape(v.shape), -1, axis)


WIDE = False


def mx_kscale(k):
    if not WIDE:
        return np.ones(k)
    levels = np.array([10, -10, 5, -5, 0])
    a = np.random.permutation(np.resize(levels, k // 512 * 4)).reshape(k // 512, 4)
    idx = np.arange(k)
    return np.exp2(a[idx // 512, idx % 128 // 32])


BF16 = ml_dtypes.bfloat16


def bf(x):
    return np.asarray(x, np.float32).astype(BF16)


def f64(x):
    return np.asarray(x).astype(np.float64)


B, C, H, W, K, M = 2, 16384, 16, 16, 16, 8
D = C
LOG2PI = float(np.log(2.0 * np.pi))


def setup_inputs():
    t = mx_kscale(D)
    a = D ** -0.25
    feats = np.random.standard_normal((B, C, H, W)) * 1.5 * a * t[None, :, None, None]
    means = np.random.standard_normal((K, M, D)) * a * t
    r = np.random.standard_normal((K, M, D)) * 0.5
    log_vars = r - r.mean(-1, keepdims=True) + np.random.standard_normal((K, M, 1)) / D + 2.0 * np.log(t)
    u = np.random.uniform(size=(K, M))
    log_weights = u - np.log(np.exp(u).sum(-1, keepdims=True))
    return {"feats": bf(feats), "means": bf(means), "log_vars": bf(log_vars), "log_weights": bf(log_weights)}


def reference(feats, means, log_vars, log_weights):
    feats, means, log_vars, log_weights = f64(feats), f64(means), f64(log_vars), f64(log_weights)
    x = feats.transpose(0, 2, 3, 1).reshape(-1, C)
    inv_var = np.exp(-log_vars)
    xsq_iv = (mxq(x * x, 1, "e4m3") @ mxq(inv_var.reshape(K * M, D), 1, "e4m3").T).reshape(-1, K, M)
    x_mu_iv = (mxq(x, 1, "e4m3") @ mxq((means * inv_var).reshape(K * M, D), 1, "e4m3").T).reshape(-1, K, M)
    mu_sq_iv = np.sum(means * means * inv_var, axis=-1)
    maha = xsq_iv - 2.0 * x_mu_iv + mu_sq_iv[None]
    log_det = np.sum(log_vars, axis=-1)
    log_prob = -0.5 * (D * LOG2PI + log_det[None] + maha)
    z = log_prob + log_weights[None]
    zm = z.max(-1, keepdims=True)
    log_lik = np.log(np.exp(z - zm).sum(-1)) + zm[..., 0]
    e = np.exp(log_lik - log_lik.max(-1, keepdims=True))
    probs = e / e.sum(-1, keepdims=True)
    anomaly = 1.0 - probs.max(axis=1)
    return anomaly.reshape(B, H, W)

@@ -1,0 +1,257 @@
+from contextlib import ExitStack
+
+import concourse.mybir as mybir
+from concourse.masks import make_identity
+
+F32 = mybir.dt.float32
+BF16 = mybir.dt.bfloat16
+U32 = mybir.dt.uint32
+U8 = mybir.dt.uint8
+FP8X4 = mybir.dt.float8_e4m3fn_x4
+ALU = mybir.AluOpType
+ACT = mybir.ActivationFunctionType
+AXIS_X = mybir.AxisListType.X
+
+P = 128
+PACK = 4
+K_PASS = P * PACK
+
+BATCH = 2
+CHANNELS = 16384
+PIXELS = 256
+ROWS = BATCH * PIXELS
+CLASSES = 16
+PER_CLASS = 8
+COMPONENTS = CLASSES * PER_CLASS
+ROW_TILES = ROWS // P
+
+PASSES_PER_CHUNK = 4
+CHUNK = PASSES_PER_CHUNK * K_PASS
+CHUNKS = CHANNELS // CHUNK
+SLABS_PER_CHUNK = CHUNK // P
+
+LD_GROUP = 32
+LD_GROUPS_PER_CHUNK = CHUNK // LD_GROUP
+LD_BLOCKS = CHANNELS // LD_GROUP // P
+SUM_BLOCKS = LD_BLOCKS + 1
+BIAS_BLOCKS = SUM_BLOCKS + 1
+
+RUN = 4
+
+FLOPS = 2 * 2 * ROWS * COMPONENTS * CHANNELS
+
+
+def prepare_weights(nc, pools, ident, log_var, mean, chunk, sums):
+    inv_var = pools["natural"].tile([P, CHUNK], F32, name="inv_var")
+    nc.scalar.activation(out=inv_var[:], in_=log_var[:], func=ACT.Exp, scale=-1.0)
+    mean_iv = pools["natural"].tile([P, CHUNK], F32, name="mean_iv")
+    nc.vector.tensor_tensor(out=mean_iv[:], in0=mean[:], in1=inv_var[:], op=ALU.mult)
+
+    products = pools["scratch"].tile([P, CHUNK], F32, name="products")
+    nc.vector.scalar_tensor_tensor(
+        out=products[:],
+        in0=mean[:],
+        scalar=1.0,
+        in1=mean_iv[:],
+        op0=ALU.mult,
+        op1=ALU.mult,
+        accum_out=sums[:, LD_BLOCKS, chunk : chunk + 1],
+    )
+    first = chunk * LD_GROUPS_PER_CHUNK
+    nc.vector.tensor_reduce(
+        out=sums[:].rearrange("p j g -> p (j g)")[:, first : first + LD_GROUPS_PER_CHUNK],
+        in_=log_var[:].rearrange("p (g k) -> p g k", k=LD_GROUP),
+        axis=AXIS_X,
+        op=ALU.add,
+    )
+
+    grouped = pools["weights"].tile(
+        [P, 2, PASSES_PER_CHUNK, COMPONENTS * PACK], BF16, name="w_grouped", align_bytes=64
+    )
+    for pair, natural in enumerate((inv_var, mean_iv)):
+        for g in range(PASSES_PER_CHUNK):
+            flipped = pools["bank"].tile([P, PACK, COMPONENTS], F32, name="flipped", tag="bank")
+            for t in range(PACK):
+                k0 = g * K_PASS + t * P
+                nc.tensor.transpose(flipped[:, t, :], natural[:, k0 : k0 + P], ident[:])
+            nc.scalar.copy(
+                out=grouped[:, pair, g, :].rearrange("p (m t) -> p m t", t=PACK),
+                in_=flipped[:].rearrange("p t m -> p m t"),
+            )
+    codes = pools["weights"].tile(
+        [P, 2, PASSES_PER_CHUNK, COMPONENTS], U32, name="w_codes", align_bytes=64
+    )
+    scales = pools["weights"].tile(
+        [P, 2, PASSES_PER_CHUNK, COMPONENTS], U8, name="w_scales", align_bytes=64
+    )
+    nc.vector.quantize_mx(
+        out=codes[:].rearrange("p a g m -> p (a g m)").bitcast(FP8X4),
+        scales=scales[:].rearrange("p a g m -> p (a g m)"),
+        in_=grouped[:].rearrange("p a g w -> p (a g w)"),
+    )
+    return codes, scales
+
+
+def quantise_x_pass(nc, pools, raw_pass):
+    grouped = pools["x"].tile([P, 2, ROWS * PACK], BF16, name="x_grouped", align_bytes=64)
+    source = raw_pass.rearrange("p t (c i) -> p c t i", i=RUN)
+    nc.scalar.activation(
+        out=grouped[:, 0, :].rearrange("p (c i t) -> p c t i", i=RUN, t=PACK),
+        in_=source,
+        func=ACT.Square,
+    )
+    nc.vector.tensor_copy(
+        out=grouped[:, 1, :].rearrange("p (c i t) -> p c t i", i=RUN, t=PACK),
+        in_=source,
+    )
+    codes = pools["x"].tile([P, 2, ROWS], U32, name="x_codes", align_bytes=64)
+    scales = pools["x"].tile([P, 2, ROWS], U8, name="x_scales", align_bytes=64)
+    nc.vector.quantize_mx(
+        out=codes[:].rearrange("p a n -> p (a n)").bitcast(FP8X4),
+        scales=scales[:].rearrange("p a n -> p (a n)"),
+        in_=grouped[:].rearrange("p a w -> p (a w)"),
+    )
+    return codes, scales
+
+
+def tile_gmmoutlierdetector_k_kernel(tc, feats, means, log_vars, log_weights, out):
+    nc = tc.nc
+    x_slabs = feats.rearrange("b (s p) h w -> b p s (h w)", p=P)
+    mean_rows = means.rearrange("k m d -> (k m) d")
+    log_var_rows = log_vars.rearrange("k m d -> (k m) d")
+
+    with ExitStack() as stack:
+        pools = {
+            "const": stack.enter_context(tc.tile_pool(name="const", bufs=1)),
+            "load": stack.enter_context(tc.tile_pool(name="load", bufs=3)),
+            "natural": stack.enter_context(tc.tile_pool(name="natural", bufs=2)),
+            "scratch": stack.enter_context(tc.tile_pool(name="scratch", bufs=1)),
+            "weights": stack.enter_context(tc.tile_pool(name="weights", bufs=2)),
+            "x": stack.enter_context(tc.tile_pool(name="x", bufs=3)),
+            "acc": stack.enter_context(tc.psum_pool(name="acc", bufs=1)),
+            "bank": stack.enter_context(tc.psum_pool(name="bank", bufs=6)),
+        }
+        const = pools["const"]
+
+        ident = const.tile([P, P], F32, name="ident")
+        make_identity(nc, ident[:])
+        minus_half = const.tile([P, P], F32, name="minus_half")
+        nc.vector.memset(minus_half[:], -0.5)
+        sums = const.tile([P, SUM_BLOCKS, P], F32, name="sums")
+        nc.vector.memset(sums[:, LD_BLOCKS, :], 0.0)
+        log_weight_rows = const.tile([P, COMPONENTS], BF16, name="log_weight_rows")
+        nc.vector.memset(log_weight_rows[:], 0.0)
+        score = const.tile([P, P], F32, name="score")
+        nc.vector.memset(score[:], 0.0)
+
+        acc = [
+            pools["acc"].tile([P, ROWS], F32, name="p_acc"),
+            pools["acc"].tile([P, ROWS], F32, name="q_acc"),
+        ]
+
+        for chunk in range(CHUNKS):
+            k0 = chunk * CHUNK
+            log_var = pools["load"].tile([P, CHUNK], BF16, name="log_var")
+            nc.sync.dma_start(out=log_var[:], in_=log_var_rows[:, k0 : k0 + CHUNK])
+            mean = pools["load"].tile([P, CHUNK], BF16, name="mean")
+            nc.sync.dma_start(out=mean[:], in_=mean_rows[:, k0 : k0 + CHUNK])
+            raw = pools["load"].tile([P, SLABS_PER_CHUNK, ROWS], BF16, name="raw")
+            s0 = chunk * SLABS_PER_CHUNK
+            for b in range(BATCH):
+                nc.sync.dma_start(
+                    out=raw[:, :, b * PIXELS : (b + 1) * PIXELS],
+                    in_=x_slabs[b, :, s0 : s0 + SLABS_PER_CHUNK, :],
+                )
+
+            w_codes, w_scales = prepare_weights(nc, pools, ident, log_var, mean, chunk, sums)
+            for g in range(PASSES_PER_CHUNK):
+                x_codes, x_scales = quantise_x_pass(
+                    nc, pools, raw[:, g * PACK : (g + 1) * PACK, :]
+                )
+                for pair in range(2):
+                    nc.tensor.matmul_mx(
+                        out=acc[pair][:],
+                        lhsT=w_codes[:, pair, g, :].bitcast(FP8X4),
+                        lhsT_scale=w_scales[:, pair, g, :],
+                        rhs=x_codes[:, pair, :].bitcast(FP8X4),
+                        rhs_scale=x_scales[:, pair, :],
+                        start=(chunk == 0 and g == 0),
+                        stop=(chunk == CHUNKS - 1 and g == PASSES_PER_CHUNK - 1),
+                    )
+
+        nc.sync.dma_start(
+            out=log_weight_rows[0:1, :], in_=log_weights.rearrange("(o k) m -> o (k m)", o=1)
+        )
+        shifted = const.tile([P, BIAS_BLOCKS, COMPONENTS], F32, name="shifted")
+        for j in range(SUM_BLOCKS):
+            rows = pools["bank"].tile([P, PACK, COMPONENTS], F32, name="rows", tag="bank")
+            nc.tensor.transpose(rows[:, 0, :], sums[:, j, :], ident[:])
+            top = const.tile([P, 1], F32, name="top%d" % j)
+            nc.vector.tensor_reduce(out=top[:], in_=rows[:, 0, :], axis=AXIS_X, op=ALU.max)
+            nc.vector.tensor_scalar_sub(out=shifted[:, j, :], in0=rows[:, 0, :], scalar1=top[:, 0:1])
+        nc.vector.tensor_scalar_mul(
+            out=shifted[:, SUM_BLOCKS, :], in0=log_weight_rows[:], scalar1=-2.0
+        )
+        bias_bank = pools["bank"].tile([P, PACK, COMPONENTS], F32, name="bias_bank", tag="bank")
+        for j in range(BIAS_BLOCKS):
+            nc.tensor.matmul(
+                out=bias_bank[:, 0, :],
+                lhsT=minus_half[:],
+                rhs=shifted[:, j, :],
+                start=(j == 0),
+                stop=(j == BIAS_BLOCKS - 1),
+            )
+        bias = const.tile([P, COMPONENTS], F32, name="bias")
+        nc.vector.tensor_copy(out=bias[:], in_=bias_bank[:, 0, :])
+
+        minus_2q = const.tile([P, ROWS], F32, name="minus_2q")
+        nc.scalar.mul(out=minus_2q[:], in_=acc[1][:], mul=-2.0)
+        p_minus_2q = const.tile([P, ROWS], F32, name="p_minus_2q")
+        nc.vector.tensor_tensor(out=p_minus_2q[:], in0=acc[0][:], in1=minus_2q[:], op=ALU.add)
+        by_row = pools["bank"].tile([P, ROW_TILES, COMPONENTS], F32, name="by_row", tag="bank")
+        for j in range(ROW_TILES):
+            nc.tensor.transpose(by_row[:, j, :], p_minus_2q[:, j * P : (j + 1) * P], ident[:])
+        z = const.tile([P, ROW_TILES, COMPONENTS], F32, name="z")
+        nc.vector.scalar_tensor_tensor(
+            out=z[:],
+            in0=by_row[:],
+            scalar=-0.5,
+            in1=bias[:].unsqueeze(1).to_broadcast([P, ROW_TILES, COMPONENTS]),
+            op0=ALU.mult,
+            op1=ALU.add,
+        )
+
+        minus_top = const.tile([P, ROW_TILES], F32, name="minus_top")
+        nc.vector.tensor_reduce(out=minus_top[:], in_=z[:], axis=AXIS_X, op=ALU.max, negate=True)
+        weight = const.tile([P, ROW_TILES, COMPONENTS], F32, name="weight")
+        for j in range(ROW_TILES):
+            nc.scalar.activation(
+                out=weight[:, j, :], in_=z[:, j, :], func=ACT.Exp, bias=minus_top[:, j : j + 1]
+            )
+        class_sum = const.tile([P, ROW_TILES, CLASSES], F32, name="class_sum")
+        nc.vector.tensor_reduce(
+            out=class_sum[:].rearrange("p j k -> p (j k)"),
+            in_=weight[:].rearrange("p j (k m) -> p (j k) m", m=PER_CLASS),
+            axis=AXIS_X,
+            op=ALU.add,
+        )
+        largest = const.tile([P, ROW_TILES], F32, name="largest")
+        nc.vector.tensor_reduce(out=largest[:], in_=class_sum[:], axis=AXIS_X, op=ALU.max)
+        total = const.tile([P, ROW_TILES], F32, name="total")
+        nc.vector.tensor_reduce(out=total[:], in_=class_sum[:], axis=AXIS_X, op=ALU.add)
+        others = const.tile([P, ROW_TILES], F32, name="others")
+        nc.vector.tensor_tensor(out=others[:], in0=total[:], in1=largest[:], op=ALU.subtract)
+        inv_total = const.tile([P, ROW_TILES], F32, name="inv_total")
+        nc.vector.reciprocal(out=inv_total[:], in_=total[:])
+        nc.vector.tensor_tensor(
+            out=score[:, 0:ROW_TILES], in0=others[:], in1=inv_total[:], op=ALU.mult
+        )
+
+        score_bank = pools["bank"].tile([P, PACK, P], F32, name="score_bank", tag="bank")
+        nc.tensor.transpose(score_bank[:, 0, :], score[:], ident[:])
+        score_rows = const.tile([P, P], F32, name="score_rows")
+        nc.vector.tensor_copy(out=score_rows[:], in_=score_bank[:, 0, :])
+        nc.sync.dma_start(
+            out=out.rearrange("b (a h) w -> (b a) (h w)", a=ROW_TILES // BATCH),
+            in_=score_rows[0:ROW_TILES, :],
+        )

@@ -31,7 +31,10 @@ CHUNKS = CHANNELS // CHUNK
 SLABS_PER_CHUNK = CHUNK // P
 
 LD_GROUP = 32
-LD_GROUPS_PER_CHUNK = CHUNK // LD_GROUP
+GROUPS_PER_SLAB = P // LD_GROUP
+LD_SLABS = 8
+LD_COLUMNS = LD_SLABS * GROUPS_PER_SLAB
+LD_BANKS_PER_CHUNK = SLABS_PER_CHUNK // LD_SLABS
 LD_BLOCKS = CHANNELS // LD_GROUP // P
 SUM_BLOCKS = LD_BLOCKS + 1
 BIAS_BLOCKS = SUM_BLOCKS + 1
@@ -41,7 +44,31 @@ RUN = 4
 FLOPS = 2 * 2 * ROWS * COMPONENTS * CHANNELS
 
 
-def prepare_weights(nc, pools, ident, log_var, mean, chunk, sums):
+def add_up_log_vars(nc, pools, consts, log_var, chunk, ld_acc):
+    for h in range(LD_BANKS_PER_CHUNK):
+        flipped = pools["bank"].tile([P, LD_SLABS, COMPONENTS], BF16, name="lv_flipped", tag="bank")
+        for s in range(LD_SLABS):
+            k0 = (h * LD_SLABS + s) * P
+            nc.tensor.transpose(flipped[:, s, :], log_var[:, k0 : k0 + P], consts["ident_bf"][:])
+        by_channel = pools["weights"].tile([P, LD_SLABS, COMPONENTS], BF16, name="lv_by_channel")
+        if h % 2 == 0:
+            nc.scalar.copy(out=by_channel[:], in_=flipped[:])
+        else:
+            nc.vector.tensor_copy(out=by_channel[:], in_=flipped[:])
+        first = (chunk * LD_BANKS_PER_CHUNK + h) * LD_COLUMNS
+        for s in range(LD_SLABS):
+            window = LD_COLUMNS - GROUPS_PER_SLAB * (s + 1)
+            nc.tensor.matmul(
+                out=ld_acc[:, first : first + LD_COLUMNS],
+                lhsT=by_channel[:, s, :],
+                rhs=consts["quarter"][:, window : window + LD_COLUMNS],
+                start=(s == 0),
+                stop=(s == LD_SLABS - 1),
+            )
+
+
+def prepare_weights(nc, pools, consts, log_var, mean, chunk, sums):
+    ident = consts["ident"]
     inv_var = pools["natural"].tile([P, CHUNK], F32, name="inv_var")
     nc.scalar.activation(out=inv_var[:], in_=log_var[:], func=ACT.Exp, scale=-1.0)
     mean_iv = pools["natural"].tile([P, CHUNK], F32, name="mean_iv")
@@ -56,13 +83,6 @@ def prepare_weights(nc, pools, ident, log_var, mean, chunk, sums):
         op0=ALU.mult,
         op1=ALU.mult,
         accum_out=sums[:, LD_BLOCKS, chunk : chunk + 1],
-    )
-    first = chunk * LD_GROUPS_PER_CHUNK
-    nc.vector.tensor_reduce(
-        out=sums[:].rearrange("p j g -> p (j g)")[:, first : first + LD_GROUPS_PER_CHUNK],
-        in_=log_var[:].rearrange("p (g k) -> p g k", k=LD_GROUP),
-        axis=AXIS_X,
-        op=ALU.add,
     )
 
     grouped = pools["weights"].tile(
@@ -114,6 +134,98 @@ def quantise_x_pass(nc, pools, raw_pass):
     return codes, scales
 
 
+def component_bias(nc, pools, consts, sums, ld_acc, log_weights):
+    const = pools["const"]
+    nc.vector.tensor_copy(
+        out=sums[:, 0:LD_BLOCKS, :].rearrange("p j g -> p (j g)"), in_=ld_acc[:]
+    )
+    shifted = const.tile([P, BIAS_BLOCKS, COMPONENTS], F32, name="shifted")
+    for j in range(SUM_BLOCKS):
+        rows = pools["bank"].tile([P, PACK, COMPONENTS], F32, name="rows", tag="bank")
+        nc.tensor.transpose(rows[:, 0, :], sums[:, j, :], consts["ident"][:])
+        top = const.tile([P, 1], F32, name="top%d" % j)
+        nc.vector.tensor_reduce(out=top[:], in_=rows[:, 0, :], axis=AXIS_X, op=ALU.max)
+        nc.vector.tensor_scalar_sub(out=shifted[:, j, :], in0=rows[:, 0, :], scalar1=top[:, 0:1])
+    log_weight_rows = const.tile([P, COMPONENTS], BF16, name="log_weight_rows")
+    nc.vector.memset(log_weight_rows[:], 0.0)
+    nc.sync.dma_start(
+        out=log_weight_rows[0:1, :], in_=log_weights.rearrange("(o k) m -> o (k m)", o=1)
+    )
+    nc.vector.tensor_scalar_mul(
+        out=shifted[:, SUM_BLOCKS, :], in0=log_weight_rows[:], scalar1=-2.0
+    )
+    minus_half = const.tile([P, P], F32, name="minus_half")
+    nc.vector.memset(minus_half[:], -0.5)
+    bias_bank = pools["bank"].tile([P, PACK, COMPONENTS], F32, name="bias_bank", tag="bank")
+    for j in range(BIAS_BLOCKS):
+        nc.tensor.matmul(
+            out=bias_bank[:, 0, :],
+            lhsT=minus_half[:],
+            rhs=shifted[:, j, :],
+            start=(j == 0),
+            stop=(j == BIAS_BLOCKS - 1),
+        )
+    bias = const.tile([P, COMPONENTS], F32, name="bias")
+    nc.vector.tensor_copy(out=bias[:], in_=bias_bank[:, 0, :])
+    return bias
+
+
+def anomaly_scores(nc, pools, consts, p_acc, q_acc, bias, out):
+    const = pools["const"]
+    ident = consts["ident"]
+    minus_2q = const.tile([P, ROWS], F32, name="minus_2q")
+    nc.scalar.mul(out=minus_2q[:], in_=q_acc[:], mul=-2.0)
+    p_minus_2q = const.tile([P, ROWS], F32, name="p_minus_2q")
+    nc.vector.tensor_tensor(out=p_minus_2q[:], in0=p_acc[:], in1=minus_2q[:], op=ALU.add)
+    by_row = pools["bank"].tile([P, ROW_TILES, COMPONENTS], F32, name="by_row", tag="bank")
+    for j in range(ROW_TILES):
+        nc.tensor.transpose(by_row[:, j, :], p_minus_2q[:, j * P : (j + 1) * P], ident[:])
+    z = const.tile([P, ROW_TILES, COMPONENTS], F32, name="z")
+    nc.vector.scalar_tensor_tensor(
+        out=z[:],
+        in0=by_row[:],
+        scalar=-0.5,
+        in1=bias[:].unsqueeze(1).to_broadcast([P, ROW_TILES, COMPONENTS]),
+        op0=ALU.mult,
+        op1=ALU.add,
+    )
+
+    minus_top = const.tile([P, ROW_TILES], F32, name="minus_top")
+    nc.vector.tensor_reduce(out=minus_top[:], in_=z[:], axis=AXIS_X, op=ALU.max, negate=True)
+    weight = const.tile([P, ROW_TILES, COMPONENTS], F32, name="weight")
+    for j in range(ROW_TILES):
+        nc.scalar.activation(
+            out=weight[:, j, :], in_=z[:, j, :], func=ACT.Exp, bias=minus_top[:, j : j + 1]
+        )
+    class_sum = const.tile([P, ROW_TILES, CLASSES], F32, name="class_sum")
+    nc.vector.tensor_reduce(
+        out=class_sum[:].rearrange("p j k -> p (j k)"),
+        in_=weight[:].rearrange("p j (k m) -> p (j k) m", m=PER_CLASS),
+        axis=AXIS_X,
+        op=ALU.add,
+    )
+    largest = const.tile([P, ROW_TILES], F32, name="largest")
+    nc.vector.tensor_reduce(out=largest[:], in_=class_sum[:], axis=AXIS_X, op=ALU.max)
+    total = const.tile([P, ROW_TILES], F32, name="total")
+    nc.vector.tensor_reduce(out=total[:], in_=class_sum[:], axis=AXIS_X, op=ALU.add)
+    others = const.tile([P, ROW_TILES], F32, name="others")
+    nc.vector.tensor_tensor(out=others[:], in0=total[:], in1=largest[:], op=ALU.subtract)
+    inv_total = const.tile([P, ROW_TILES], F32, name="inv_total")
+    nc.vector.reciprocal(out=inv_total[:], in_=total[:])
+    score = consts["score"]
+    nc.vector.tensor_tensor(
+        out=score[:, 0:ROW_TILES], in0=others[:], in1=inv_total[:], op=ALU.mult
+    )
+    score_bank = pools["bank"].tile([P, PACK, P], F32, name="score_bank", tag="bank")
+    nc.tensor.transpose(score_bank[:, 0, :], score[:], ident[:])
+    score_rows = const.tile([P, P], F32, name="score_rows")
+    nc.vector.tensor_copy(out=score_rows[:], in_=score_bank[:, 0, :])
+    nc.sync.dma_start(
+        out=out.rearrange("b (a h) w -> (b a) (h w)", a=ROW_TILES // BATCH),
+        in_=score_rows[0:ROW_TILES, :],
+    )
+
+
 def tile_gmmoutlierdetector_k_kernel(tc, feats, means, log_vars, log_weights, out):
     nc = tc.nc
     x_slabs = feats.rearrange("b (s p) h w -> b p s (h w)", p=P)
@@ -129,32 +241,51 @@ def tile_gmmoutlierdetector_k_kernel(tc, feats, means, log_vars, log_weights, ou
             "weights": stack.enter_context(tc.tile_pool(name="weights", bufs=2)),
             "x": stack.enter_context(tc.tile_pool(name="x", bufs=3)),
             "acc": stack.enter_context(tc.psum_pool(name="acc", bufs=1)),
-            "bank": stack.enter_context(tc.psum_pool(name="bank", bufs=6)),
+            "bank": stack.enter_context(tc.psum_pool(name="bank", bufs=5)),
         }
         const = pools["const"]
 
         ident = const.tile([P, P], F32, name="ident")
         make_identity(nc, ident[:])
-        minus_half = const.tile([P, P], F32, name="minus_half")
-        nc.vector.memset(minus_half[:], -0.5)
-        sums = const.tile([P, SUM_BLOCKS, P], F32, name="sums")
-        nc.vector.memset(sums[:, LD_BLOCKS, :], 0.0)
-        log_weight_rows = const.tile([P, COMPONENTS], BF16, name="log_weight_rows")
-        nc.vector.memset(log_weight_rows[:], 0.0)
+        ident_bf = const.tile([P, P], BF16, name="ident_bf")
+        make_identity(nc, ident_bf[:])
+        in_quarter = const.tile([P, GROUPS_PER_SLAB], F32, name="in_quarter")
+        nc.vector.tensor_reduce(
+            out=in_quarter[:],
+            in_=ident[:].rearrange("p (q i) -> p q i", i=LD_GROUP),
+            axis=AXIS_X,
+            op=ALU.add,
+        )
+        quarter = const.tile([P, 2 * LD_COLUMNS - GROUPS_PER_SLAB], BF16, name="quarter")
+        nc.vector.memset(quarter[:], 0.0)
+        nc.vector.tensor_copy(
+            out=quarter[:, LD_COLUMNS - GROUPS_PER_SLAB : LD_COLUMNS], in_=in_quarter[:]
+        )
         score = const.tile([P, P], F32, name="score")
         nc.vector.memset(score[:], 0.0)
+        consts = {"ident": ident, "ident_bf": ident_bf, "quarter": quarter, "score": score}
 
-        acc = [
-            pools["acc"].tile([P, ROWS], F32, name="p_acc"),
-            pools["acc"].tile([P, ROWS], F32, name="q_acc"),
-        ]
+        sums = const.tile([P, SUM_BLOCKS, P], F32, name="sums")
+        nc.vector.memset(sums[:, LD_BLOCKS, :], 0.0)
 
-        for chunk in range(CHUNKS):
+        p_acc = pools["acc"].tile([P, ROWS], F32, name="p_acc")
+        q_acc = pools["acc"].tile([P, ROWS], F32, name="q_acc")
+        ld_acc = pools["acc"].tile([P, LD_BLOCKS * P], F32, name="ld_acc")
+        acc = [p_acc, q_acc]
+
+        def weights_of(chunk):
             k0 = chunk * CHUNK
             log_var = pools["load"].tile([P, CHUNK], BF16, name="log_var")
             nc.sync.dma_start(out=log_var[:], in_=log_var_rows[:, k0 : k0 + CHUNK])
             mean = pools["load"].tile([P, CHUNK], BF16, name="mean")
             nc.sync.dma_start(out=mean[:], in_=mean_rows[:, k0 : k0 + CHUNK])
+            quantised = prepare_weights(nc, pools, consts, log_var, mean, chunk, sums)
+            add_up_log_vars(nc, pools, consts, log_var, chunk, ld_acc)
+            return quantised
+
+        ahead = weights_of(0)
+        for chunk in range(CHUNKS):
+            w_codes, w_scales = ahead
             raw = pools["load"].tile([P, SLABS_PER_CHUNK, ROWS], BF16, name="raw")
             s0 = chunk * SLABS_PER_CHUNK
             for b in range(BATCH):
@@ -162,8 +293,10 @@ def tile_gmmoutlierdetector_k_kernel(tc, feats, means, log_vars, log_weights, ou
                     out=raw[:, :, b * PIXELS : (b + 1) * PIXELS],
                     in_=x_slabs[b, :, s0 : s0 + SLABS_PER_CHUNK, :],
                 )
-
-            w_codes, w_scales = prepare_weights(nc, pools, ident, log_var, mean, chunk, sums)
+            if chunk + 1 < CHUNKS:
+                ahead = weights_of(chunk + 1)
+            else:
+                bias = component_bias(nc, pools, consts, sums, ld_acc, log_weights)
             for g in range(PASSES_PER_CHUNK):
                 x_codes, x_scales = quantise_x_pass(
                     nc, pools, raw[:, g * PACK : (g + 1) * PACK, :]
@@ -179,79 +312,4 @@ def tile_gmmoutlierdetector_k_kernel(tc, feats, means, log_vars, log_weights, ou
                         stop=(chunk == CHUNKS - 1 and g == PASSES_PER_CHUNK - 1),
                     )
 
-        nc.sync.dma_start(
-            out=log_weight_rows[0:1, :], in_=log_weights.rearrange("(o k) m -> o (k m)", o=1)
-        )
-        shifted = const.tile([P, BIAS_BLOCKS, COMPONENTS], F32, name="shifted")
-        for j in range(SUM_BLOCKS):
-            rows = pools["bank"].tile([P, PACK, COMPONENTS], F32, name="rows", tag="bank")
-            nc.tensor.transpose(rows[:, 0, :], sums[:, j, :], ident[:])
-            top = const.tile([P, 1], F32, name="top%d" % j)
-            nc.vector.tensor_reduce(out=top[:], in_=rows[:, 0, :], axis=AXIS_X, op=ALU.max)
-            nc.vector.tensor_scalar_sub(out=shifted[:, j, :], in0=rows[:, 0, :], scalar1=top[:, 0:1])
-        nc.vector.tensor_scalar_mul(
-            out=shifted[:, SUM_BLOCKS, :], in0=log_weight_rows[:], scalar1=-2.0
-        )
-        bias_bank = pools["bank"].tile([P, PACK, COMPONENTS], F32, name="bias_bank", tag="bank")
-        for j in range(BIAS_BLOCKS):
-            nc.tensor.matmul(
-                out=bias_bank[:, 0, :],
-                lhsT=minus_half[:],
-                rhs=shifted[:, j, :],
-                start=(j == 0),
-                stop=(j == BIAS_BLOCKS - 1),
-            )
-        bias = const.tile([P, COMPONENTS], F32, name="bias")
-        nc.vector.tensor_copy(out=bias[:], in_=bias_bank[:, 0, :])
-
-        minus_2q = const.tile([P, ROWS], F32, name="minus_2q")
-        nc.scalar.mul(out=minus_2q[:], in_=acc[1][:], mul=-2.0)
-        p_minus_2q = const.tile([P, ROWS], F32, name="p_minus_2q")
-        nc.vector.tensor_tensor(out=p_minus_2q[:], in0=acc[0][:], in1=minus_2q[:], op=ALU.add)
-        by_row = pools["bank"].tile([P, ROW_TILES, COMPONENTS], F32, name="by_row", tag="bank")
-        for j in range(ROW_TILES):
-            nc.tensor.transpose(by_row[:, j, :], p_minus_2q[:, j * P : (j + 1) * P], ident[:])
-        z = const.tile([P, ROW_TILES, COMPONENTS], F32, name="z")
-        nc.vector.scalar_tensor_tensor(
-            out=z[:],
-            in0=by_row[:],
-            scalar=-0.5,
-            in1=bias[:].unsqueeze(1).to_broadcast([P, ROW_TILES, COMPONENTS]),
-            op0=ALU.mult,
-            op1=ALU.add,
-        )
-
-        minus_top = const.tile([P, ROW_TILES], F32, name="minus_top")
-        nc.vector.tensor_reduce(out=minus_top[:], in_=z[:], axis=AXIS_X, op=ALU.max, negate=True)
-        weight = const.tile([P, ROW_TILES, COMPONENTS], F32, name="weight")
-        for j in range(ROW_TILES):
-            nc.scalar.activation(
-                out=weight[:, j, :], in_=z[:, j, :], func=ACT.Exp, bias=minus_top[:, j : j + 1]
-            )
-        class_sum = const.tile([P, ROW_TILES, CLASSES], F32, name="class_sum")
-        nc.vector.tensor_reduce(
-            out=class_sum[:].rearrange("p j k -> p (j k)"),
-            in_=weight[:].rearrange("p j (k m) -> p (j k) m", m=PER_CLASS),
-            axis=AXIS_X,
-            op=ALU.add,
-        )
-        largest = const.tile([P, ROW_TILES], F32, name="largest")
-        nc.vector.tensor_reduce(out=largest[:], in_=class_sum[:], axis=AXIS_X, op=ALU.max)
-        total = const.tile([P, ROW_TILES], F32, name="total")
-        nc.vector.tensor_reduce(out=total[:], in_=class_sum[:], axis=AXIS_X, op=ALU.add)
-        others = const.tile([P, ROW_TILES], F32, name="others")
-        nc.vector.tensor_tensor(out=others[:], in0=total[:], in1=largest[:], op=ALU.subtract)
-        inv_total = const.tile([P, ROW_TILES], F32, name="inv_total")
-        nc.vector.reciprocal(out=inv_total[:], in_=total[:])
-        nc.vector.tensor_tensor(
-            out=score[:, 0:ROW_TILES], in0=others[:], in1=inv_total[:], op=ALU.mult
-        )
-
-        score_bank = pools["bank"].tile([P, PACK, P], F32, name="score_bank", tag="bank")
-        nc.tensor.transpose(score_bank[:, 0, :], score[:], ident[:])
-        score_rows = const.tile([P, P], F32, name="score_rows")
-        nc.vector.tensor_copy(out=score_rows[:], in_=score_bank[:, 0, :])
-        nc.sync.dma_start(
-            out=out.rearrange("b (a h) w -> (b a) (h w)", a=ROW_TILES // BATCH),
-            in_=score_rows[0:ROW_TILES, :],
-        )
+        anomaly_scores(nc, pools, consts, p_acc, q_acc, bias, out)

@@ -28,6 +28,7 @@ ROW_TILES = ROWS // P
 PASSES_PER_CHUNK = 4
 CHUNK = PASSES_PER_CHUNK * K_PASS
 CHUNKS = CHANNELS // CHUNK
+PASSES = CHANNELS // K_PASS
 SLABS_PER_CHUNK = CHUNK // P
 
 LD_GROUP = 32
@@ -44,12 +45,40 @@ RUN = 4
 FLOPS = 2 * 2 * ROWS * COMPONENTS * CHANNELS
 
 
-def add_up_log_vars(nc, pools, consts, log_var, chunk, ld_acc):
+def prepare_weights(nc, pools, consts, log_var, mean, chunk, sums, ld_acc):
+    grouped = pools["weights"].tile(
+        [P, 2, PASSES_PER_CHUNK, COMPONENTS * PACK], BF16, name="w_grouped", align_bytes=64
+    )
+
+    inv_var = pools["natural"].tile([P, CHUNK], F32, name="inv_var")
+    nc.scalar.activation(out=inv_var[:], in_=log_var[:], func=ACT.Exp, scale=-1.0)
+    mean_iv = pools["natural"].tile([P, CHUNK], F32, name="mean_iv")
+    nc.vector.tensor_tensor(out=mean_iv[:], in0=mean[:], in1=inv_var[:], op=ALU.mult)
+    products = pools["scratch"].tile([P, CHUNK], F32, name="products")
+    nc.vector.scalar_tensor_tensor(
+        out=products[:],
+        in0=mean[:],
+        scalar=1.0,
+        in1=mean_iv[:],
+        op0=ALU.mult,
+        op1=ALU.mult,
+        accum_out=sums[:, LD_BLOCKS, chunk : chunk + 1],
+    )
+
     for h in range(LD_BANKS_PER_CHUNK):
         flipped = pools["bank"].tile([P, LD_SLABS, COMPONENTS], BF16, name="lv_flipped", tag="bank")
         for s in range(LD_SLABS):
             k0 = (h * LD_SLABS + s) * P
             nc.tensor.transpose(flipped[:, s, :], log_var[:, k0 : k0 + P], consts["ident_bf"][:])
+        for half in range(LD_SLABS // PACK):
+            nc.scalar.activation(
+                out=grouped[:, 0, h * (LD_SLABS // PACK) + half, :].rearrange(
+                    "p (m t) -> p m t", t=PACK
+                ),
+                in_=flipped[:, half * PACK : (half + 1) * PACK, :].rearrange("p t m -> p m t"),
+                func=ACT.Exp,
+                scale=-1.0,
+            )
         by_channel = pools["weights"].tile([P, LD_SLABS, COMPONENTS], BF16, name="lv_by_channel")
         if h % 2 == 0:
             nc.scalar.copy(out=by_channel[:], in_=flipped[:])
@@ -66,38 +95,16 @@ def add_up_log_vars(nc, pools, consts, log_var, chunk, ld_acc):
                 stop=(s == LD_SLABS - 1),
             )
 
+    for g in range(PASSES_PER_CHUNK):
+        flipped = pools["bank"].tile([P, PACK, COMPONENTS], F32, name="miv_flipped", tag="bank")
+        for t in range(PACK):
+            k0 = g * K_PASS + t * P
+            nc.tensor.transpose(flipped[:, t, :], mean_iv[:, k0 : k0 + P], consts["ident"][:])
+        nc.scalar.copy(
+            out=grouped[:, 1, g, :].rearrange("p (m t) -> p m t", t=PACK),
+            in_=flipped[:].rearrange("p t m -> p m t"),
+        )
 
-def prepare_weights(nc, pools, consts, log_var, mean, chunk, sums):
-    ident = consts["ident"]
-    inv_var = pools["natural"].tile([P, CHUNK], F32, name="inv_var")
-    nc.scalar.activation(out=inv_var[:], in_=log_var[:], func=ACT.Exp, scale=-1.0)
-    mean_iv = pools["natural"].tile([P, CHUNK], F32, name="mean_iv")
-    nc.vector.tensor_tensor(out=mean_iv[:], in0=mean[:], in1=inv_var[:], op=ALU.mult)
-
-    products = pools["scratch"].tile([P, CHUNK], F32, name="products")
-    nc.vector.scalar_tensor_tensor(
-        out=products[:],
-        in0=mean[:],
-        scalar=1.0,
-        in1=mean_iv[:],
-        op0=ALU.mult,
-        op1=ALU.mult,
-        accum_out=sums[:, LD_BLOCKS, chunk : chunk + 1],
-    )
-
-    grouped = pools["weights"].tile(
-        [P, 2, PASSES_PER_CHUNK, COMPONENTS * PACK], BF16, name="w_grouped", align_bytes=64
-    )
-    for pair, natural in enumerate((inv_var, mean_iv)):
-        for g in range(PASSES_PER_CHUNK):
-            flipped = pools["bank"].tile([P, PACK, COMPONENTS], F32, name="flipped", tag="bank")
-            for t in range(PACK):
-                k0 = g * K_PASS + t * P
-                nc.tensor.transpose(flipped[:, t, :], natural[:, k0 : k0 + P], ident[:])
-            nc.scalar.copy(
-                out=grouped[:, pair, g, :].rearrange("p (m t) -> p m t", t=PACK),
-                in_=flipped[:].rearrange("p t m -> p m t"),
-            )
     codes = pools["weights"].tile(
         [P, 2, PASSES_PER_CHUNK, COMPONENTS], U32, name="w_codes", align_bytes=64
     )
@@ -112,26 +119,28 @@ def prepare_weights(nc, pools, consts, log_var, mean, chunk, sums):
     return codes, scales
 
 
-def quantise_x_pass(nc, pools, raw_pass):
-    grouped = pools["x"].tile([P, 2, ROWS * PACK], BF16, name="x_grouped", align_bytes=64)
-    source = raw_pass.rearrange("p t (c i) -> p c t i", i=RUN)
-    nc.scalar.activation(
-        out=grouped[:, 0, :].rearrange("p (c i t) -> p c t i", i=RUN, t=PACK),
-        in_=source,
-        func=ACT.Square,
-    )
+def quantise_x_pass(nc, pools, raw, squares_on_vector):
+    source = raw.rearrange("p t (c i) -> p c t i", i=RUN)
+    plain = pools["x"].tile([P, ROWS * PACK], BF16, name="x_grouped", align_bytes=64)
     nc.vector.tensor_copy(
-        out=grouped[:, 1, :].rearrange("p (c i t) -> p c t i", i=RUN, t=PACK),
-        in_=source,
+        out=plain[:].rearrange("p (c i t) -> p c t i", i=RUN, t=PACK), in_=source
     )
-    codes = pools["x"].tile([P, 2, ROWS], U32, name="x_codes", align_bytes=64)
-    scales = pools["x"].tile([P, 2, ROWS], U8, name="x_scales", align_bytes=64)
-    nc.vector.quantize_mx(
-        out=codes[:].rearrange("p a n -> p (a n)").bitcast(FP8X4),
-        scales=scales[:].rearrange("p a n -> p (a n)"),
-        in_=grouped[:].rearrange("p a w -> p (a w)"),
-    )
-    return codes, scales
+    squares = pools["x"].tile([P, ROWS * PACK], BF16, name="x2_grouped", align_bytes=64)
+    if squares_on_vector:
+        nc.vector.tensor_tensor(out=squares[:], in0=plain[:], in1=plain[:], op=ALU.mult)
+    else:
+        nc.scalar.activation(
+            out=squares[:].rearrange("p (c i t) -> p c t i", i=RUN, t=PACK),
+            in_=source,
+            func=ACT.Square,
+        )
+    quantised = []
+    for pair, grouped in enumerate((squares, plain)):
+        codes = pools["x"].tile([P, ROWS], U32, name="x_codes%d" % pair, align_bytes=64)
+        scales = pools["x"].tile([P, ROWS], U8, name="x_scales%d" % pair, align_bytes=64)
+        nc.vector.quantize_mx(out=codes[:].bitcast(FP8X4), scales=scales[:], in_=grouped[:])
+        quantised.append((codes, scales))
+    return quantised
 
 
 def component_bias(nc, pools, consts, sums, ld_acc, log_weights):
@@ -156,47 +165,51 @@ def component_bias(nc, pools, consts, sums, ld_acc, log_weights):
     )
     minus_half = const.tile([P, P], F32, name="minus_half")
     nc.vector.memset(minus_half[:], -0.5)
-    bias_bank = pools["bank"].tile([P, PACK, COMPONENTS], F32, name="bias_bank", tag="bank")
+    bias_bank = pools["bank"].tile([P, PACK, P], F32, name="bias_bank", tag="bank")
     for j in range(BIAS_BLOCKS):
         nc.tensor.matmul(
             out=bias_bank[:, 0, :],
-            lhsT=minus_half[:],
-            rhs=shifted[:, j, :],
+            lhsT=shifted[:, j, :],
+            rhs=minus_half[:],
             start=(j == 0),
             stop=(j == BIAS_BLOCKS - 1),
         )
-    bias = const.tile([P, COMPONENTS], F32, name="bias")
-    nc.vector.tensor_copy(out=bias[:], in_=bias_bank[:, 0, :])
+    bias = const.tile([P, 1], F32, name="bias")
+    nc.vector.tensor_copy(out=bias[:], in_=bias_bank[:, 0, 0:1])
     return bias
 
 
 def anomaly_scores(nc, pools, consts, p_acc, q_acc, bias, out):
     const = pools["const"]
-    ident = consts["ident"]
-    minus_2q = const.tile([P, ROWS], F32, name="minus_2q")
-    nc.scalar.mul(out=minus_2q[:], in_=q_acc[:], mul=-2.0)
-    p_minus_2q = const.tile([P, ROWS], F32, name="p_minus_2q")
-    nc.vector.tensor_tensor(out=p_minus_2q[:], in0=p_acc[:], in1=minus_2q[:], op=ALU.add)
-    by_row = pools["bank"].tile([P, ROW_TILES, COMPONENTS], F32, name="by_row", tag="bank")
-    for j in range(ROW_TILES):
-        nc.tensor.transpose(by_row[:, j, :], p_minus_2q[:, j * P : (j + 1) * P], ident[:])
-    z = const.tile([P, ROW_TILES, COMPONENTS], F32, name="z")
+    q_plus_bias = const.tile([P, ROWS], F32, name="q_plus_bias")
+    nc.scalar.activation(out=q_plus_bias[:], in_=q_acc[:], func=ACT.Identity, bias=bias[:, 0:1])
+    z_by_component = const.tile([P, ROWS], F32, name="z_by_component")
     nc.vector.scalar_tensor_tensor(
-        out=z[:],
-        in0=by_row[:],
+        out=z_by_component[:],
+        in0=p_acc[:],
         scalar=-0.5,
-        in1=bias[:].unsqueeze(1).to_broadcast([P, ROW_TILES, COMPONENTS]),
+        in1=q_plus_bias[:],
         op0=ALU.mult,
         op1=ALU.add,
     )
+    z = pools["bank"].tile([P, ROW_TILES, COMPONENTS], F32, name="z", tag="bank")
+    for j in range(ROW_TILES):
+        nc.tensor.transpose(z[:, j, :], z_by_component[:, j * P : (j + 1) * P], consts["ident"][:])
 
     minus_top = const.tile([P, ROW_TILES], F32, name="minus_top")
     nc.vector.tensor_reduce(out=minus_top[:], in_=z[:], axis=AXIS_X, op=ALU.max, negate=True)
     weight = const.tile([P, ROW_TILES, COMPONENTS], F32, name="weight")
+    total = const.tile([P, ROW_TILES], F32, name="total")
     for j in range(ROW_TILES):
         nc.scalar.activation(
-            out=weight[:, j, :], in_=z[:, j, :], func=ACT.Exp, bias=minus_top[:, j : j + 1]
+            out=weight[:, j, :],
+            in_=z[:, j, :],
+            func=ACT.Exp,
+            bias=minus_top[:, j : j + 1],
+            accum_out=total[:, j : j + 1],
         )
+    inv_total = const.tile([P, ROW_TILES], F32, name="inv_total")
+    nc.vector.reciprocal(out=inv_total[:], in_=total[:])
     class_sum = const.tile([P, ROW_TILES, CLASSES], F32, name="class_sum")
     nc.vector.tensor_reduce(
         out=class_sum[:].rearrange("p j k -> p (j k)"),
@@ -206,18 +219,14 @@ def anomaly_scores(nc, pools, consts, p_acc, q_acc, bias, out):
     )
     largest = const.tile([P, ROW_TILES], F32, name="largest")
     nc.vector.tensor_reduce(out=largest[:], in_=class_sum[:], axis=AXIS_X, op=ALU.max)
-    total = const.tile([P, ROW_TILES], F32, name="total")
-    nc.vector.tensor_reduce(out=total[:], in_=class_sum[:], axis=AXIS_X, op=ALU.add)
     others = const.tile([P, ROW_TILES], F32, name="others")
     nc.vector.tensor_tensor(out=others[:], in0=total[:], in1=largest[:], op=ALU.subtract)
-    inv_total = const.tile([P, ROW_TILES], F32, name="inv_total")
-    nc.vector.reciprocal(out=inv_total[:], in_=total[:])
     score = consts["score"]
     nc.vector.tensor_tensor(
         out=score[:, 0:ROW_TILES], in0=others[:], in1=inv_total[:], op=ALU.mult
     )
     score_bank = pools["bank"].tile([P, PACK, P], F32, name="score_bank", tag="bank")
-    nc.tensor.transpose(score_bank[:, 0, :], score[:], ident[:])
+    nc.tensor.transpose(score_bank[:, 0, :], score[:], consts["ident"][:])
     score_rows = const.tile([P, P], F32, name="score_rows")
     nc.vector.tensor_copy(out=score_rows[:], in_=score_bank[:, 0, :])
     nc.sync.dma_start(
@@ -236,6 +245,7 @@ def tile_gmmoutlierdetector_k_kernel(tc, feats, means, log_vars, log_weights, ou
         pools = {
             "const": stack.enter_context(tc.tile_pool(name="const", bufs=1)),
             "load": stack.enter_context(tc.tile_pool(name="load", bufs=3)),
+            "raw": stack.enter_context(tc.tile_pool(name="raw", bufs=8)),
             "natural": stack.enter_context(tc.tile_pool(name="natural", bufs=2)),
             "scratch": stack.enter_context(tc.tile_pool(name="scratch", bufs=1)),
             "weights": stack.enter_context(tc.tile_pool(name="weights", bufs=2)),
@@ -279,37 +289,40 @@ def tile_gmmoutlierdetector_k_kernel(tc, feats, means, log_vars, log_weights, ou
             nc.sync.dma_start(out=log_var[:], in_=log_var_rows[:, k0 : k0 + CHUNK])
             mean = pools["load"].tile([P, CHUNK], BF16, name="mean")
             nc.sync.dma_start(out=mean[:], in_=mean_rows[:, k0 : k0 + CHUNK])
-            quantised = prepare_weights(nc, pools, consts, log_var, mean, chunk, sums)
-            add_up_log_vars(nc, pools, consts, log_var, chunk, ld_acc)
-            return quantised
+            return prepare_weights(nc, pools, consts, log_var, mean, chunk, sums, ld_acc)
 
-        ahead = weights_of(0)
-        for chunk in range(CHUNKS):
-            w_codes, w_scales = ahead
-            raw = pools["load"].tile([P, SLABS_PER_CHUNK, ROWS], BF16, name="raw")
-            s0 = chunk * SLABS_PER_CHUNK
+        def load_x_pass(i):
+            raw = pools["raw"].tile([P, PACK, ROWS], BF16, name="raw")
             for b in range(BATCH):
                 nc.sync.dma_start(
                     out=raw[:, :, b * PIXELS : (b + 1) * PIXELS],
-                    in_=x_slabs[b, :, s0 : s0 + SLABS_PER_CHUNK, :],
+                    in_=x_slabs[b, :, i * PACK : (i + 1) * PACK, :],
                 )
-            if chunk + 1 < CHUNKS:
-                ahead = weights_of(chunk + 1)
-            else:
-                bias = component_bias(nc, pools, consts, sums, ld_acc, log_weights)
-            for g in range(PASSES_PER_CHUNK):
-                x_codes, x_scales = quantise_x_pass(
-                    nc, pools, raw[:, g * PACK : (g + 1) * PACK, :]
+            return raw
+
+        raw_ahead = load_x_pass(0)
+        weights_ahead = weights_of(0)
+        for i in range(PASSES):
+            chunk, g = divmod(i, PASSES_PER_CHUNK)
+            raw = raw_ahead
+            if i + 1 < PASSES:
+                raw_ahead = load_x_pass(i + 1)
+            if g == 0:
+                w_codes, w_scales = weights_ahead
+                if chunk + 1 < CHUNKS:
+                    weights_ahead = weights_of(chunk + 1)
+                else:
+                    bias = component_bias(nc, pools, consts, sums, ld_acc, log_weights)
+            quantised = quantise_x_pass(nc, pools, raw[:], squares_on_vector=(i == PASSES - 1))
+            for pair, (x_codes, x_scales) in enumerate(quantised):
+                nc.tensor.matmul_mx(
+                    out=acc[pair][:],
+                    lhsT=w_codes[:, pair, g, :].bitcast(FP8X4),
+                    lhsT_scale=w_scales[:, pair, g, :],
+                    rhs=x_codes[:].bitcast(FP8X4),
+                    rhs_scale=x_scales[:],
+                    start=(i == 0),
+                    stop=(i == PASSES - 1),
                 )
-                for pair in range(2):
-                    nc.tensor.matmul_mx(
-                        out=acc[pair][:],
-                        lhsT=w_codes[:, pair, g, :].bitcast(FP8X4),
-                        lhsT_scale=w_scales[:, pair, g, :],
-                        rhs=x_codes[:, pair, :].bitcast(FP8X4),
-                        rhs_scale=x_scales[:, pair, :],
-                        start=(chunk == 0 and g == 0),
-                        stop=(chunk == CHUNKS - 1 and g == PASSES_PER_CHUNK - 1),
-                    )
 
         anomaly_scores(nc, pools, consts, p_acc, q_acc, bias, out)

@@ -29,81 +29,100 @@ PASSES_PER_CHUNK = 4
 CHUNK = PASSES_PER_CHUNK * K_PASS
 CHUNKS = CHANNELS // CHUNK
 PASSES = CHANNELS // K_PASS
-SLABS_PER_CHUNK = CHUNK // P
+PAIR = 2
+HALVES = 2
+WORDS = PACK // HALVES
 
-LD_GROUP = 32
-GROUPS_PER_SLAB = P // LD_GROUP
-LD_SLABS = 8
-LD_COLUMNS = LD_SLABS * GROUPS_PER_SLAB
-LD_BANKS_PER_CHUNK = SLABS_PER_CHUNK // LD_SLABS
-LD_BLOCKS = CHANNELS // LD_GROUP // P
-SUM_BLOCKS = LD_BLOCKS + 1
-BIAS_BLOCKS = SUM_BLOCKS + 1
-
+SLABS = PASSES * PACK
 RUN = 4
 
 FLOPS = 2 * 2 * ROWS * COMPONENTS * CHANNELS
 
 
-def prepare_weights(nc, pools, consts, log_var, mean, chunk, sums, ld_acc):
+def c_on_tensor(i):
+    return i % PASSES_PER_CHUNK != PASSES_PER_CHUNK - 1
+
+
+def prepare_weights(nc, pools, consts, log_var, mean, chunk, sums):
     grouped = pools["weights"].tile(
         [P, 2, PASSES_PER_CHUNK, COMPONENTS * PACK], BF16, name="w_grouped", align_bytes=64
     )
+    log_var_words = log_var[:].bitcast(F32)
+    mean_words = mean[:].bitcast(F32)
 
-    inv_var = pools["natural"].tile([P, CHUNK], F32, name="inv_var")
-    nc.scalar.activation(out=inv_var[:], in_=log_var[:], func=ACT.Exp, scale=-1.0)
-    mean_iv = pools["natural"].tile([P, CHUNK], F32, name="mean_iv")
-    nc.vector.tensor_tensor(out=mean_iv[:], in0=mean[:], in1=inv_var[:], op=ALU.mult)
-    products = pools["scratch"].tile([P, CHUNK], F32, name="products")
-    nc.vector.scalar_tensor_tensor(
-        out=products[:],
-        in0=mean[:],
-        scalar=1.0,
-        in1=mean_iv[:],
-        op0=ALU.mult,
-        op1=ALU.mult,
-        accum_out=sums[:, LD_BLOCKS, chunk : chunk + 1],
-    )
+    for h in range(PASSES_PER_CHUNK // PAIR):
+        flipped = []
+        for words, name in ((log_var_words, "lv_flipped"), (mean_words, "mean_flipped")):
+            bank = pools["bank"].tile([P, WORDS, PAIR, COMPONENTS], F32, name=name, tag="bank")
+            for g in range(PAIR):
+                first = (h * PAIR + g) * K_PASS // HALVES
+                for u in range(WORDS):
+                    nc.tensor.transpose(
+                        bank[:, u, g, :],
+                        words[:, first + u : first + K_PASS // HALVES : WORDS],
+                        consts["ident"][:],
+                    )
+            flipped.append(bank)
+        lv_bank, mean_bank = flipped
 
-    for h in range(LD_BANKS_PER_CHUNK):
-        flipped = pools["bank"].tile([P, LD_SLABS, COMPONENTS], BF16, name="lv_flipped", tag="bank")
-        for s in range(LD_SLABS):
-            k0 = (h * LD_SLABS + s) * P
-            nc.tensor.transpose(flipped[:, s, :], log_var[:, k0 : k0 + P], consts["ident_bf"][:])
-        for half in range(LD_SLABS // PACK):
-            nc.scalar.activation(
-                out=grouped[:, 0, h * (LD_SLABS // PACK) + half, :].rearrange(
-                    "p (m t) -> p m t", t=PACK
-                ),
-                in_=flipped[:, half * PACK : (half + 1) * PACK, :].rearrange("p t m -> p m t"),
-                func=ACT.Exp,
-                scale=-1.0,
+        lv, mu = [
+            bank[:].rearrange("p u g m -> p u (g m)").bitcast(BF16).rearrange(
+                "p u (m e) -> p m u e", e=HALVES
             )
-        by_channel = pools["weights"].tile([P, LD_SLABS, COMPONENTS], BF16, name="lv_by_channel")
-        if h % 2 == 0:
-            nc.scalar.copy(out=by_channel[:], in_=flipped[:])
-        else:
-            nc.vector.tensor_copy(out=by_channel[:], in_=flipped[:])
-        first = (chunk * LD_BANKS_PER_CHUNK + h) * LD_COLUMNS
-        for s in range(LD_SLABS):
-            window = LD_COLUMNS - GROUPS_PER_SLAB * (s + 1)
-            nc.tensor.matmul(
-                out=ld_acc[:, first : first + LD_COLUMNS],
-                lhsT=by_channel[:, s, :],
-                rhs=consts["quarter"][:, window : window + LD_COLUMNS],
-                start=(s == 0),
-                stop=(s == LD_SLABS - 1),
-            )
+            for bank in (lv_bank, mean_bank)
+        ]
+        inv_var = pools["turned"].tile([P, PAIR, COMPONENTS * PACK], F32, name="inv_var")
+        mean_sq = pools["turned"].tile([P, PAIR, COMPONENTS * PACK], F32, name="mean_sq")
 
-    for g in range(PASSES_PER_CHUNK):
-        flipped = pools["bank"].tile([P, PACK, COMPONENTS], F32, name="miv_flipped", tag="bank")
-        for t in range(PACK):
-            k0 = g * K_PASS + t * P
-            nc.tensor.transpose(flipped[:, t, :], mean_iv[:, k0 : k0 + P], consts["ident"][:])
-        nc.scalar.copy(
-            out=grouped[:, 1, g, :].rearrange("p (m t) -> p m t", t=PACK),
-            in_=flipped[:].rearrange("p t m -> p m t"),
+        def by_word(tile_view):
+            return tile_view.rearrange("p g (m u e) -> p (g m) u e", u=WORDS, e=HALVES)
+
+        pair = slice(h * PAIR, (h + 1) * PAIR)
+        nc.scalar.activation(out=by_word(inv_var[:]), in_=lv, func=ACT.Exp, scale=-1.0)
+        nc.scalar.activation(out=by_word(grouped[:, 0, pair, :]), in_=lv, func=ACT.Exp, scale=-1.0)
+        nc.vector.tensor_tensor(
+            out=by_word(grouped[:, 1, pair, :]), in0=mu, in1=by_word(inv_var[:]), op=ALU.mult
         )
+        nc.scalar.activation(out=by_word(mean_sq[:]), in_=mu, func=ACT.Square)
+        by_channel = pools["turned"].tile([P, WORDS, PAIR, COMPONENTS], F32, name="lv_by_channel")
+        nc.scalar.copy(out=by_channel[:], in_=lv_bank[:])
+
+        for g in range(PAIR):
+            i = chunk * PASSES_PER_CHUNK + h * PAIR + g
+            if c_on_tensor(i):
+                for t in range(PACK):
+                    nc.tensor.matmul(
+                        out=sums["diagonal"][:],
+                        lhsT=mean_sq[:, g, t::PACK],
+                        rhs=inv_var[:, g, t::PACK],
+                        start=(i == 0 and t == 0),
+                        stop=(i == PASSES - 2 and t == PACK - 1),
+                    )
+            else:
+                products = pools["turned"].tile([P, COMPONENTS * PACK], F32, name="products")
+                nc.vector.tensor_tensor(
+                    out=products[:], in0=mean_sq[:, g, :], in1=inv_var[:, g, :], op=ALU.mult
+                )
+                for t in range(PACK):
+                    column = SLABS + chunk * PACK + t
+                    nc.tensor.matmul(
+                        out=sums["columns"][:, column : column + 1],
+                        lhsT=products[:, t::PACK],
+                        rhs=consts["ones"][:],
+                        start=True,
+                        stop=True,
+                    )
+            lv_values = by_channel[:].bitcast(BF16)
+            for u in range(WORDS):
+                for e in range(HALVES):
+                    slab = i * PACK + u * HALVES + e
+                    nc.tensor.matmul(
+                        out=sums["columns"][:, slab : slab + 1],
+                        lhsT=lv_values[:, u, g, e::HALVES],
+                        rhs=consts["ones_bf"][:],
+                        start=True,
+                        stop=True,
+                    )
 
     codes = pools["weights"].tile(
         [P, 2, PASSES_PER_CHUNK, COMPONENTS], U32, name="w_codes", align_bytes=64
@@ -120,20 +139,16 @@ def prepare_weights(nc, pools, consts, log_var, mean, chunk, sums, ld_acc):
 
 
 def quantise_x_pass(nc, pools, raw, squares_on_vector):
-    source = raw.rearrange("p t (c i) -> p c t i", i=RUN)
     plain = pools["x"].tile([P, ROWS * PACK], BF16, name="x_grouped", align_bytes=64)
     nc.vector.tensor_copy(
-        out=plain[:].rearrange("p (c i t) -> p c t i", i=RUN, t=PACK), in_=source
+        out=plain[:].rearrange("p (c i t) -> p c t i", i=RUN, t=PACK),
+        in_=raw.rearrange("p t (c i) -> p c t i", i=RUN),
     )
     squares = pools["x"].tile([P, ROWS * PACK], BF16, name="x2_grouped", align_bytes=64)
     if squares_on_vector:
         nc.vector.tensor_tensor(out=squares[:], in0=plain[:], in1=plain[:], op=ALU.mult)
     else:
-        nc.scalar.activation(
-            out=squares[:].rearrange("p (c i t) -> p c t i", i=RUN, t=PACK),
-            in_=source,
-            func=ACT.Square,
-        )
+        nc.scalar.activation(out=squares[:], in_=plain[:], func=ACT.Square)
     quantised = []
     for pair, grouped in enumerate((squares, plain)):
         codes = pools["x"].tile([P, ROWS], U32, name="x_codes%d" % pair, align_bytes=64)
@@ -143,39 +158,38 @@ def quantise_x_pass(nc, pools, raw, squares_on_vector):
     return quantised
 
 
-def component_bias(nc, pools, consts, sums, ld_acc, log_weights):
+def component_bias(nc, pools, consts, sums):
     const = pools["const"]
-    nc.vector.tensor_copy(
-        out=sums[:, 0:LD_BLOCKS, :].rearrange("p j g -> p (j g)"), in_=ld_acc[:]
+    columns = const.tile([P, SLABS + CHUNKS * PACK], F32, name="columns_sb")
+    nc.vector.tensor_copy(out=columns[:], in_=sums["columns"][:])
+    shifted = pools["bank"].tile([P, SLABS + CHUNKS * PACK], F32, name="shifted", tag="bank")
+    nc.tensor.matmul(
+        out=shifted[:], lhsT=consts["minus_first"][:], rhs=columns[:], start=True, stop=True
     )
-    shifted = const.tile([P, BIAS_BLOCKS, COMPONENTS], F32, name="shifted")
-    for j in range(SUM_BLOCKS):
-        rows = pools["bank"].tile([P, PACK, COMPONENTS], F32, name="rows", tag="bank")
-        nc.tensor.transpose(rows[:, 0, :], sums[:, j, :], consts["ident"][:])
-        top = const.tile([P, 1], F32, name="top%d" % j)
-        nc.vector.tensor_reduce(out=top[:], in_=rows[:, 0, :], axis=AXIS_X, op=ALU.max)
-        nc.vector.tensor_scalar_sub(out=shifted[:, j, :], in0=rows[:, 0, :], scalar1=top[:, 0:1])
-    log_weight_rows = const.tile([P, COMPONENTS], BF16, name="log_weight_rows")
-    nc.vector.memset(log_weight_rows[:], 0.0)
-    nc.sync.dma_start(
-        out=log_weight_rows[0:1, :], in_=log_weights.rearrange("(o k) m -> o (k m)", o=1)
+    total = const.tile([P, 1], F32, name="bias_total")
+    nc.vector.tensor_reduce(out=total[:], in_=shifted[:], axis=AXIS_X, op=ALU.add)
+    on_diagonal = const.tile([P, COMPONENTS], F32, name="on_diagonal")
+    diagonal = const.tile([P, 1], F32, name="diagonal_sum")
+    nc.vector.scalar_tensor_tensor(
+        out=on_diagonal[:],
+        in0=sums["diagonal"][:],
+        scalar=1.0,
+        in1=consts["ident"][:],
+        op0=ALU.mult,
+        op1=ALU.mult,
+        accum_out=diagonal[:],
     )
-    nc.vector.tensor_scalar_mul(
-        out=shifted[:, SUM_BLOCKS, :], in0=log_weight_rows[:], scalar1=-2.0
-    )
-    minus_half = const.tile([P, P], F32, name="minus_half")
-    nc.vector.memset(minus_half[:], -0.5)
-    bias_bank = pools["bank"].tile([P, PACK, P], F32, name="bias_bank", tag="bank")
-    for j in range(BIAS_BLOCKS):
-        nc.tensor.matmul(
-            out=bias_bank[:, 0, :],
-            lhsT=shifted[:, j, :],
-            rhs=minus_half[:],
-            start=(j == 0),
-            stop=(j == BIAS_BLOCKS - 1),
-        )
+    both = const.tile([P, 1], F32, name="bias_both")
+    nc.vector.tensor_tensor(out=both[:], in0=total[:], in1=diagonal[:], op=ALU.add)
     bias = const.tile([P, 1], F32, name="bias")
-    nc.vector.tensor_copy(out=bias[:], in_=bias_bank[:, 0, 0:1])
+    nc.vector.scalar_tensor_tensor(
+        out=bias[:],
+        in0=both[:],
+        scalar=-0.5,
+        in1=consts["log_weight"][:],
+        op0=ALU.mult,
+        op1=ALU.add,
+    )
     return bias
 
 
@@ -237,7 +251,7 @@ def anomaly_scores(nc, pools, consts, p_acc, q_acc, bias, out):
 
 def tile_gmmoutlierdetector_k_kernel(tc, feats, means, log_vars, log_weights, out):
     nc = tc.nc
-    x_slabs = feats.rearrange("b (s p) h w -> b p s (h w)", p=P)
+    x_passes = feats.rearrange("b (g p t) h w -> b g p t (h w)", p=P, t=PACK)
     mean_rows = means.rearrange("k m d -> (k m) d")
     log_var_rows = log_vars.rearrange("k m d -> (k m) d")
 
@@ -246,41 +260,41 @@ def tile_gmmoutlierdetector_k_kernel(tc, feats, means, log_vars, log_weights, ou
             "const": stack.enter_context(tc.tile_pool(name="const", bufs=1)),
             "load": stack.enter_context(tc.tile_pool(name="load", bufs=3)),
             "raw": stack.enter_context(tc.tile_pool(name="raw", bufs=8)),
-            "natural": stack.enter_context(tc.tile_pool(name="natural", bufs=2)),
-            "scratch": stack.enter_context(tc.tile_pool(name="scratch", bufs=1)),
+            "turned": stack.enter_context(tc.tile_pool(name="turned", bufs=3)),
             "weights": stack.enter_context(tc.tile_pool(name="weights", bufs=2)),
             "x": stack.enter_context(tc.tile_pool(name="x", bufs=3)),
             "acc": stack.enter_context(tc.psum_pool(name="acc", bufs=1)),
-            "bank": stack.enter_context(tc.psum_pool(name="bank", bufs=5)),
+            "bank": stack.enter_context(tc.psum_pool(name="bank", bufs=4)),
         }
         const = pools["const"]
 
         ident = const.tile([P, P], F32, name="ident")
         make_identity(nc, ident[:])
-        ident_bf = const.tile([P, P], BF16, name="ident_bf")
-        make_identity(nc, ident_bf[:])
-        in_quarter = const.tile([P, GROUPS_PER_SLAB], F32, name="in_quarter")
-        nc.vector.tensor_reduce(
-            out=in_quarter[:],
-            in_=ident[:].rearrange("p (q i) -> p q i", i=LD_GROUP),
-            axis=AXIS_X,
-            op=ALU.add,
-        )
-        quarter = const.tile([P, 2 * LD_COLUMNS - GROUPS_PER_SLAB], BF16, name="quarter")
-        nc.vector.memset(quarter[:], 0.0)
-        nc.vector.tensor_copy(
-            out=quarter[:, LD_COLUMNS - GROUPS_PER_SLAB : LD_COLUMNS], in_=in_quarter[:]
-        )
+        minus_first = const.tile([P, P], F32, name="minus_first")
+        nc.vector.tensor_copy(out=minus_first[:], in_=ident[:])
+        nc.vector.tensor_scalar_sub(out=minus_first[0:1, :], in0=ident[0:1, :], scalar1=1.0)
+        ones = const.tile([P, 1], F32, name="ones")
+        nc.vector.memset(ones[:], 1.0)
+        ones_bf = const.tile([P, 1], BF16, name="ones_bf")
+        nc.vector.memset(ones_bf[:], 1.0)
         score = const.tile([P, P], F32, name="score")
         nc.vector.memset(score[:], 0.0)
-        consts = {"ident": ident, "ident_bf": ident_bf, "quarter": quarter, "score": score}
-
-        sums = const.tile([P, SUM_BLOCKS, P], F32, name="sums")
-        nc.vector.memset(sums[:, LD_BLOCKS, :], 0.0)
+        log_weight = const.tile([P, 1], BF16, name="log_weight")
+        consts = {
+            "ident": ident,
+            "minus_first": minus_first,
+            "ones": ones,
+            "ones_bf": ones_bf,
+            "score": score,
+            "log_weight": log_weight,
+        }
 
         p_acc = pools["acc"].tile([P, ROWS], F32, name="p_acc")
         q_acc = pools["acc"].tile([P, ROWS], F32, name="q_acc")
-        ld_acc = pools["acc"].tile([P, LD_BLOCKS * P], F32, name="ld_acc")
+        sums = {
+            "diagonal": pools["acc"].tile([P, COMPONENTS], F32, name="c_diagonal"),
+            "columns": pools["acc"].tile([P, SLABS + CHUNKS * PACK], F32, name="columns"),
+        }
         acc = [p_acc, q_acc]
 
         def weights_of(chunk):
@@ -289,19 +303,19 @@ def tile_gmmoutlierdetector_k_kernel(tc, feats, means, log_vars, log_weights, ou
             nc.sync.dma_start(out=log_var[:], in_=log_var_rows[:, k0 : k0 + CHUNK])
             mean = pools["load"].tile([P, CHUNK], BF16, name="mean")
             nc.sync.dma_start(out=mean[:], in_=mean_rows[:, k0 : k0 + CHUNK])
-            return prepare_weights(nc, pools, consts, log_var, mean, chunk, sums, ld_acc)
+            return prepare_weights(nc, pools, consts, log_var, mean, chunk, sums)
 
         def load_x_pass(i):
             raw = pools["raw"].tile([P, PACK, ROWS], BF16, name="raw")
             for b in range(BATCH):
                 nc.sync.dma_start(
-                    out=raw[:, :, b * PIXELS : (b + 1) * PIXELS],
-                    in_=x_slabs[b, :, i * PACK : (i + 1) * PACK, :],
+                    out=raw[:, :, b * PIXELS : (b + 1) * PIXELS], in_=x_passes[b, i, :, :, :]
                 )
             return raw
 
         raw_ahead = load_x_pass(0)
         weights_ahead = weights_of(0)
+        nc.sync.dma_start(out=log_weight[:], in_=log_weights.rearrange("k (m o) -> (k m) o", o=1))
         for i in range(PASSES):
             chunk, g = divmod(i, PASSES_PER_CHUNK)
             raw = raw_ahead
@@ -312,8 +326,8 @@ def tile_gmmoutlierdetector_k_kernel(tc, feats, means, log_vars, log_weights, ou
                 if chunk + 1 < CHUNKS:
                     weights_ahead = weights_of(chunk + 1)
                 else:
-                    bias = component_bias(nc, pools, consts, sums, ld_acc, log_weights)
-            quantised = quantise_x_pass(nc, pools, raw[:], squares_on_vector=(i == PASSES - 1))
+                    bias = component_bias(nc, pools, consts, sums)
+            quantised = quantise_x_pass(nc, pools, raw[:], squares_on_vector=(g == PASSES_PER_CHUNK - 1))
             for pair, (x_codes, x_scales) in enumerate(quantised):
                 nc.tensor.matmul_mx(
                     out=acc[pair][:],

@@ -55,12 +55,10 @@ def prepare_weights(nc, pools, consts, log_var, mean, chunk, sums):
         for words, name in ((log_var_words, "lv_flipped"), (mean_words, "mean_flipped")):
             bank = pools["bank"].tile([P, WORDS, PAIR, COMPONENTS], F32, name=name, tag="bank")
             for g in range(PAIR):
-                first = (h * PAIR + g) * K_PASS // HALVES
                 for u in range(WORDS):
+                    first = ((h * PAIR + g) * WORDS + u) * P
                     nc.tensor.transpose(
-                        bank[:, u, g, :],
-                        words[:, first + u : first + K_PASS // HALVES : WORDS],
-                        consts["ident"][:],
+                        bank[:, u, g, :], words[:, first : first + P], consts["ident"][:]
                     )
             flipped.append(bank)
         lv_bank, mean_bank = flipped
@@ -72,7 +70,6 @@ def prepare_weights(nc, pools, consts, log_var, mean, chunk, sums):
             for bank in (lv_bank, mean_bank)
         ]
         inv_var = pools["turned"].tile([P, PAIR, COMPONENTS * PACK], F32, name="inv_var")
-        mean_sq = pools["turned"].tile([P, PAIR, COMPONENTS * PACK], F32, name="mean_sq")
 
         def by_word(tile_view):
             return tile_view.rearrange("p g (m u e) -> p (g m) u e", u=WORDS, e=HALVES)
@@ -83,7 +80,15 @@ def prepare_weights(nc, pools, consts, log_var, mean, chunk, sums):
         nc.vector.tensor_tensor(
             out=by_word(grouped[:, 1, pair, :]), in0=mu, in1=by_word(inv_var[:]), op=ALU.mult
         )
-        nc.scalar.activation(out=by_word(mean_sq[:]), in_=mu, func=ACT.Square)
+        first_pass = chunk * PASSES_PER_CHUNK + h * PAIR
+        on_tensor = [g for g in range(PAIR) if c_on_tensor(first_pass + g)]
+        mean_sq = pools["turned"].tile([P, WORDS, HALVES, PAIR * COMPONENTS], F32, name="mean_sq")
+        turned = len(on_tensor) * COMPONENTS
+        nc.scalar.activation(
+            out=mean_sq[:, :, :, 0:turned],
+            in_=mu[:, 0:turned, :, :].rearrange("p m u e -> p u e m"),
+            func=ACT.Square,
+        )
         by_channel = pools["turned"].tile([P, WORDS, PAIR, COMPONENTS], F32, name="lv_by_channel")
         nc.scalar.copy(out=by_channel[:], in_=lv_bank[:])
 
@@ -93,15 +98,21 @@ def prepare_weights(nc, pools, consts, log_var, mean, chunk, sums):
                 for t in range(PACK):
                     nc.tensor.matmul(
                         out=sums["diagonal"][:],
-                        lhsT=mean_sq[:, g, t::PACK],
+                        lhsT=mean_sq[:, t // HALVES, t % HALVES, g * COMPONENTS : (g + 1) * COMPONENTS],
                         rhs=inv_var[:, g, t::PACK],
                         start=(i == 0 and t == 0),
                         stop=(i == PASSES - 2 and t == PACK - 1),
                     )
             else:
+                last_sq = pools["turned"].tile([P, COMPONENTS * PACK], F32, name="last_sq")
+                nc.scalar.activation(
+                    out=last_sq[:].rearrange("p (m u e) -> p m u e", u=WORDS, e=HALVES),
+                    in_=mu[:, g * COMPONENTS : (g + 1) * COMPONENTS, :, :],
+                    func=ACT.Square,
+                )
                 products = pools["turned"].tile([P, COMPONENTS * PACK], F32, name="products")
                 nc.vector.tensor_tensor(
-                    out=products[:], in0=mean_sq[:, g, :], in1=inv_var[:, g, :], op=ALU.mult
+                    out=products[:], in0=last_sq[:], in1=inv_var[:, g, :], op=ALU.mult
                 )
                 for t in range(PACK):
                     column = SLABS + chunk * PACK + t
@@ -139,16 +150,20 @@ def prepare_weights(nc, pools, consts, log_var, mean, chunk, sums):
 
 
 def quantise_x_pass(nc, pools, raw, squares_on_vector):
+    source = raw.rearrange("p t (c i) -> p c t i", i=RUN)
     plain = pools["x"].tile([P, ROWS * PACK], BF16, name="x_grouped", align_bytes=64)
     nc.vector.tensor_copy(
-        out=plain[:].rearrange("p (c i t) -> p c t i", i=RUN, t=PACK),
-        in_=raw.rearrange("p t (c i) -> p c t i", i=RUN),
+        out=plain[:].rearrange("p (c i t) -> p c t i", i=RUN, t=PACK), in_=source
     )
     squares = pools["x"].tile([P, ROWS * PACK], BF16, name="x2_grouped", align_bytes=64)
     if squares_on_vector:
         nc.vector.tensor_tensor(out=squares[:], in0=plain[:], in1=plain[:], op=ALU.mult)
     else:
-        nc.scalar.activation(out=squares[:], in_=plain[:], func=ACT.Square)
+        nc.scalar.activation(
+            out=squares[:].rearrange("p (c i t) -> p c t i", i=RUN, t=PACK),
+            in_=source,
+            func=ACT.Square,
+        )
     quantised = []
     for pair, grouped in enumerate((squares, plain)):
         codes = pools["x"].tile([P, ROWS], U32, name="x_codes%d" % pair, align_bytes=64)
@@ -251,7 +266,7 @@ def anomaly_scores(nc, pools, consts, p_acc, q_acc, bias, out):
 
 def tile_gmmoutlierdetector_k_kernel(tc, feats, means, log_vars, log_weights, out):
     nc = tc.nc
-    x_passes = feats.rearrange("b (g p t) h w -> b g p t (h w)", p=P, t=PACK)
+    x_passes = feats.rearrange("b (g u p e) h w -> b g u p e (h w)", u=WORDS, p=P, e=HALVES)
     mean_rows = means.rearrange("k m d -> (k m) d")
     log_var_rows = log_vars.rearrange("k m d -> (k m) d")
 
@@ -308,9 +323,11 @@ def tile_gmmoutlierdetector_k_kernel(tc, feats, means, log_vars, log_weights, ou
         def load_x_pass(i):
             raw = pools["raw"].tile([P, PACK, ROWS], BF16, name="raw")
             for b in range(BATCH):
-                nc.sync.dma_start(
-                    out=raw[:, :, b * PIXELS : (b + 1) * PIXELS], in_=x_passes[b, i, :, :, :]
-                )
+                for u in range(WORDS):
+                    nc.sync.dma_start(
+                        out=raw[:, u * HALVES : (u + 1) * HALVES, b * PIXELS : (b + 1) * PIXELS],
+                        in_=x_passes[b, i, u, :, :, :],
+                    )
             return raw
 
         raw_ahead = load_x_pass(0)

@@ -39,101 +39,105 @@ RUN = 4
 FLOPS = 2 * 2 * ROWS * COMPONENTS * CHANNELS
 
 
-def c_on_tensor(i):
-    return i % PASSES_PER_CHUNK != PASSES_PER_CHUNK - 1
+def flip_words(nc, pools, consts, tile_in, h, name):
+    words = tile_in[:].bitcast(F32)
+    bank = pools["bank"].tile([P, WORDS, PAIR, COMPONENTS], F32, name=name, tag="bank")
+    for g in range(PAIR):
+        for u in range(WORDS):
+            first = ((h * PAIR + g) * WORDS + u) * P
+            nc.tensor.transpose(bank[:, u, g, :], words[:, first : first + P], consts["ident"][:])
+    values = bank[:].rearrange("p u g m -> p u (g m)").bitcast(BF16).rearrange(
+        "p u (m e) -> p m u e", e=HALVES
+    )
+    return bank, values
+
+
+def by_word(tile_view):
+    return tile_view.rearrange("p g (m u e) -> p (g m) u e", u=WORDS, e=HALVES)
+
+
+def mean_operand_turned(nc, pools, consts, mean, lv, operand, chunk, h, sums):
+    mean_bank, mu = flip_words(nc, pools, consts, mean, h, "mean_flipped")
+    inv_var = pools["turned"].tile([P, PAIR, COMPONENTS * PACK], F32, name="inv_var")
+    nc.scalar.activation(out=by_word(inv_var[:]), in_=lv, func=ACT.Exp, scale=-1.0)
+    nc.vector.tensor_tensor(out=by_word(operand), in0=mu, in1=by_word(inv_var[:]), op=ALU.mult)
+    mean_sq = pools["turned"].tile([P, PACK, PAIR * COMPONENTS], F32, name="mean_sq")
+    nc.scalar.activation(
+        out=mean_sq[:].rearrange("p (u e) m -> p u e m", u=WORDS),
+        in_=mu.rearrange("p m u e -> p u e m"),
+        func=ACT.Square,
+    )
+    for g in range(PAIR):
+        for t in range(PACK):
+            nc.tensor.matmul(
+                out=sums["diagonal"][:],
+                lhsT=mean_sq[:, t, g * COMPONENTS : (g + 1) * COMPONENTS],
+                rhs=inv_var[:, g, t::PACK],
+                start=(chunk == 0 and g == 0 and t == 0),
+                stop=(chunk == CHUNKS - 1 and g == PAIR - 1 and t == PACK - 1),
+            )
+
+
+def mean_operand_natural(nc, pools, consts, log_var, mean, operand, chunk, h, sums):
+    span = PAIR * K_PASS
+    channels = slice(h * span, (h + 1) * span)
+    inv_var = pools["natural"].tile([P, span], F32, name="nat_inv_var")
+    nc.scalar.activation(out=inv_var[:], in_=log_var[:, channels], func=ACT.Exp, scale=-1.0)
+    mean_iv = pools["natural"].tile([P, span], F32, name="nat_mean_iv")
+    nc.vector.tensor_tensor(out=mean_iv[:], in0=mean[:, channels], in1=inv_var[:], op=ALU.mult)
+    products = pools["scratch"].tile([P, span], F32, name="products")
+    column = SLABS + chunk
+    nc.vector.scalar_tensor_tensor(
+        out=products[:],
+        in0=mean[:, channels],
+        scalar=1.0,
+        in1=mean_iv[:],
+        op0=ALU.mult,
+        op1=ALU.mult,
+        accum_out=sums["columns_sb"][:, column : column + 1],
+    )
+    for g in range(PAIR):
+        flipped = pools["bank"].tile([P, PACK, COMPONENTS], F32, name="miv_flipped", tag="bank")
+        for t in range(PACK):
+            u, e = divmod(t, HALVES)
+            first = (g * WORDS + u) * HALVES * P
+            nc.tensor.transpose(
+                flipped[:, t, :],
+                mean_iv[:, first + e : first + HALVES * P : HALVES],
+                consts["ident"][:],
+            )
+        nc.scalar.copy(
+            out=operand[:, g, :].rearrange("p (m t) -> p m t", t=PACK),
+            in_=flipped[:].rearrange("p t m -> p m t"),
+        )
 
 
 def prepare_weights(nc, pools, consts, log_var, mean, chunk, sums):
     grouped = pools["weights"].tile(
         [P, 2, PASSES_PER_CHUNK, COMPONENTS * PACK], BF16, name="w_grouped", align_bytes=64
     )
-    log_var_words = log_var[:].bitcast(F32)
-    mean_words = mean[:].bitcast(F32)
-
     for h in range(PASSES_PER_CHUNK // PAIR):
-        flipped = []
-        for words, name in ((log_var_words, "lv_flipped"), (mean_words, "mean_flipped")):
-            bank = pools["bank"].tile([P, WORDS, PAIR, COMPONENTS], F32, name=name, tag="bank")
-            for g in range(PAIR):
-                for u in range(WORDS):
-                    first = ((h * PAIR + g) * WORDS + u) * P
-                    nc.tensor.transpose(
-                        bank[:, u, g, :], words[:, first : first + P], consts["ident"][:]
-                    )
-            flipped.append(bank)
-        lv_bank, mean_bank = flipped
-
-        lv, mu = [
-            bank[:].rearrange("p u g m -> p u (g m)").bitcast(BF16).rearrange(
-                "p u (m e) -> p m u e", e=HALVES
-            )
-            for bank in (lv_bank, mean_bank)
-        ]
-        inv_var = pools["turned"].tile([P, PAIR, COMPONENTS * PACK], F32, name="inv_var")
-
-        def by_word(tile_view):
-            return tile_view.rearrange("p g (m u e) -> p (g m) u e", u=WORDS, e=HALVES)
-
         pair = slice(h * PAIR, (h + 1) * PAIR)
-        nc.scalar.activation(out=by_word(inv_var[:]), in_=lv, func=ACT.Exp, scale=-1.0)
+        lv_bank, lv = flip_words(nc, pools, consts, log_var, h, "lv_flipped")
         nc.scalar.activation(out=by_word(grouped[:, 0, pair, :]), in_=lv, func=ACT.Exp, scale=-1.0)
-        nc.vector.tensor_tensor(
-            out=by_word(grouped[:, 1, pair, :]), in0=mu, in1=by_word(inv_var[:]), op=ALU.mult
-        )
-        first_pass = chunk * PASSES_PER_CHUNK + h * PAIR
-        on_tensor = [g for g in range(PAIR) if c_on_tensor(first_pass + g)]
-        mean_sq = pools["turned"].tile([P, WORDS, HALVES, PAIR * COMPONENTS], F32, name="mean_sq")
-        turned = len(on_tensor) * COMPONENTS
-        nc.scalar.activation(
-            out=mean_sq[:, :, :, 0:turned],
-            in_=mu[:, 0:turned, :, :].rearrange("p m u e -> p u e m"),
-            func=ACT.Square,
-        )
+        operand = grouped[:, 1, pair, :]
+        if h == 0:
+            mean_operand_turned(nc, pools, consts, mean, lv, operand, chunk, h, sums)
+        else:
+            mean_operand_natural(nc, pools, consts, log_var, mean, operand, chunk, h, sums)
         by_channel = pools["turned"].tile([P, WORDS, PAIR, COMPONENTS], F32, name="lv_by_channel")
         nc.scalar.copy(out=by_channel[:], in_=lv_bank[:])
-
+        lv_values = by_channel[:].bitcast(BF16)
         for g in range(PAIR):
-            i = chunk * PASSES_PER_CHUNK + h * PAIR + g
-            if c_on_tensor(i):
-                for t in range(PACK):
-                    nc.tensor.matmul(
-                        out=sums["diagonal"][:],
-                        lhsT=mean_sq[:, t // HALVES, t % HALVES, g * COMPONENTS : (g + 1) * COMPONENTS],
-                        rhs=inv_var[:, g, t::PACK],
-                        start=(i == 0 and t == 0),
-                        stop=(i == PASSES - 2 and t == PACK - 1),
-                    )
-            else:
-                last_sq = pools["turned"].tile([P, COMPONENTS * PACK], F32, name="last_sq")
-                nc.scalar.activation(
-                    out=last_sq[:].rearrange("p (m u e) -> p m u e", u=WORDS, e=HALVES),
-                    in_=mu[:, g * COMPONENTS : (g + 1) * COMPONENTS, :, :],
-                    func=ACT.Square,
+            for t in range(PACK):
+                slab = (chunk * PASSES_PER_CHUNK + h * PAIR + g) * PACK + t
+                nc.tensor.matmul(
+                    out=sums["columns"][:, slab : slab + 1],
+                    lhsT=lv_values[:, t // HALVES, g, t % HALVES :: HALVES],
+                    rhs=consts["ones_bf"][:],
+                    start=True,
+                    stop=True,
                 )
-                products = pools["turned"].tile([P, COMPONENTS * PACK], F32, name="products")
-                nc.vector.tensor_tensor(
-                    out=products[:], in0=last_sq[:], in1=inv_var[:, g, :], op=ALU.mult
-                )
-                for t in range(PACK):
-                    column = SLABS + chunk * PACK + t
-                    nc.tensor.matmul(
-                        out=sums["columns"][:, column : column + 1],
-                        lhsT=products[:, t::PACK],
-                        rhs=consts["ones"][:],
-                        start=True,
-                        stop=True,
-                    )
-            lv_values = by_channel[:].bitcast(BF16)
-            for u in range(WORDS):
-                for e in range(HALVES):
-                    slab = i * PACK + u * HALVES + e
-                    nc.tensor.matmul(
-                        out=sums["columns"][:, slab : slab + 1],
-                        lhsT=lv_values[:, u, g, e::HALVES],
-                        rhs=consts["ones_bf"][:],
-                        start=True,
-                        stop=True,
-                    )
 
     codes = pools["weights"].tile(
         [P, 2, PASSES_PER_CHUNK, COMPONENTS], U32, name="w_codes", align_bytes=64
@@ -175,9 +179,9 @@ def quantise_x_pass(nc, pools, raw, squares_on_vector):
 
 def component_bias(nc, pools, consts, sums):
     const = pools["const"]
-    columns = const.tile([P, SLABS + CHUNKS * PACK], F32, name="columns_sb")
-    nc.vector.tensor_copy(out=columns[:], in_=sums["columns"][:])
-    shifted = pools["bank"].tile([P, SLABS + CHUNKS * PACK], F32, name="shifted", tag="bank")
+    columns = sums["columns_sb"]
+    nc.vector.tensor_copy(out=columns[:, 0:SLABS], in_=sums["columns"][:])
+    shifted = pools["bank"].tile([P, SLABS + CHUNKS], F32, name="shifted", tag="bank")
     nc.tensor.matmul(
         out=shifted[:], lhsT=consts["minus_first"][:], rhs=columns[:], start=True, stop=True
     )
@@ -275,7 +279,9 @@ def tile_gmmoutlierdetector_k_kernel(tc, feats, means, log_vars, log_weights, ou
             "const": stack.enter_context(tc.tile_pool(name="const", bufs=1)),
             "load": stack.enter_context(tc.tile_pool(name="load", bufs=3)),
             "raw": stack.enter_context(tc.tile_pool(name="raw", bufs=8)),
-            "turned": stack.enter_context(tc.tile_pool(name="turned", bufs=3)),
+            "turned": stack.enter_context(tc.tile_pool(name="turned", bufs=2)),
+            "natural": stack.enter_context(tc.tile_pool(name="natural", bufs=2)),
+            "scratch": stack.enter_context(tc.tile_pool(name="scratch", bufs=1)),
             "weights": stack.enter_context(tc.tile_pool(name="weights", bufs=2)),
             "x": stack.enter_context(tc.tile_pool(name="x", bufs=3)),
             "acc": stack.enter_context(tc.psum_pool(name="acc", bufs=1)),
@@ -288,8 +294,6 @@ def tile_gmmoutlierdetector_k_kernel(tc, feats, means, log_vars, log_weights, ou
         minus_first = const.tile([P, P], F32, name="minus_first")
         nc.vector.tensor_copy(out=minus_first[:], in_=ident[:])
         nc.vector.tensor_scalar_sub(out=minus_first[0:1, :], in0=ident[0:1, :], scalar1=1.0)
-        ones = const.tile([P, 1], F32, name="ones")
-        nc.vector.memset(ones[:], 1.0)
         ones_bf = const.tile([P, 1], BF16, name="ones_bf")
         nc.vector.memset(ones_bf[:], 1.0)
         score = const.tile([P, P], F32, name="score")
@@ -298,7 +302,6 @@ def tile_gmmoutlierdetector_k_kernel(tc, feats, means, log_vars, log_weights, ou
         consts = {
             "ident": ident,
             "minus_first": minus_first,
-            "ones": ones,
             "ones_bf": ones_bf,
             "score": score,
             "log_weight": log_weight,
@@ -308,7 +311,8 @@ def tile_gmmoutlierdetector_k_kernel(tc, feats, means, log_vars, log_weights, ou
         q_acc = pools["acc"].tile([P, ROWS], F32, name="q_acc")
         sums = {
             "diagonal": pools["acc"].tile([P, COMPONENTS], F32, name="c_diagonal"),
-            "columns": pools["acc"].tile([P, SLABS + CHUNKS * PACK], F32, name="columns"),
+            "columns": pools["acc"].tile([P, SLABS], F32, name="columns"),
+            "columns_sb": const.tile([P, SLABS + CHUNKS], F32, name="columns_sb"),
         }
         acc = [p_acc, q_acc]
 

@@ -36,180 +36,28 @@ WORDS = PACK // HALVES
 SLABS = PASSES * PACK
 RUN = 4
 
+
+NATURAL, TURNED = 0, 1
+SLOTS = PASSES
+X_OF_SLOTS = 7
+FILL = 6
+
 FLOPS = 2 * 2 * ROWS * COMPONENTS * CHANNELS
 
 
-def flip_words(nc, pools, consts, tile_in, h, name):
-    words = tile_in[:].bitcast(F32)
-    bank = pools["bank"].tile([P, WORDS, PAIR, COMPONENTS], F32, name=name, tag="bank")
-    for g in range(PAIR):
-        for u in range(WORDS):
-            first = ((h * PAIR + g) * WORDS + u) * P
-            nc.tensor.transpose(bank[:, u, g, :], words[:, first : first + P], consts["ident"][:])
-    values = bank[:].rearrange("p u g m -> p u (g m)").bitcast(BF16).rearrange(
+def turned_words(values):
+    return values.rearrange("p g (m u e) -> p (g m) u e", u=WORDS, e=HALVES)
+
+
+def bank_values(bank):
+    return bank[:].rearrange("p u g m -> p u (g m)").bitcast(BF16).rearrange(
         "p u (m e) -> p m u e", e=HALVES
     )
-    return bank, values
 
 
-def by_word(tile_view):
-    return tile_view.rearrange("p g (m u e) -> p (g m) u e", u=WORDS, e=HALVES)
-
-
-def mean_operand_turned(nc, pools, consts, mean, lv, operand, chunk, h, sums):
-    mean_bank, mu = flip_words(nc, pools, consts, mean, h, "mean_flipped")
-    inv_var = pools["turned"].tile([P, PAIR, COMPONENTS * PACK], F32, name="inv_var")
-    nc.scalar.activation(out=by_word(inv_var[:]), in_=lv, func=ACT.Exp, scale=-1.0)
-    nc.vector.tensor_tensor(out=by_word(operand), in0=mu, in1=by_word(inv_var[:]), op=ALU.mult)
-    mean_sq = pools["turned"].tile([P, PACK, PAIR * COMPONENTS], F32, name="mean_sq")
-    nc.scalar.activation(
-        out=mean_sq[:].rearrange("p (u e) m -> p u e m", u=WORDS),
-        in_=mu.rearrange("p m u e -> p u e m"),
-        func=ACT.Square,
-    )
-    for g in range(PAIR):
-        for t in range(PACK):
-            nc.tensor.matmul(
-                out=sums["diagonal"][:],
-                lhsT=mean_sq[:, t, g * COMPONENTS : (g + 1) * COMPONENTS],
-                rhs=inv_var[:, g, t::PACK],
-                start=(chunk == 0 and g == 0 and t == 0),
-                stop=(chunk == CHUNKS - 1 and g == PAIR - 1 and t == PACK - 1),
-            )
-
-
-def mean_operand_natural(nc, pools, consts, log_var, mean, operand, chunk, h, sums):
-    span = PAIR * K_PASS
-    channels = slice(h * span, (h + 1) * span)
-    inv_var = pools["natural"].tile([P, span], F32, name="nat_inv_var")
-    nc.scalar.activation(out=inv_var[:], in_=log_var[:, channels], func=ACT.Exp, scale=-1.0)
-    mean_iv = pools["natural"].tile([P, span], F32, name="nat_mean_iv")
-    nc.vector.tensor_tensor(out=mean_iv[:], in0=mean[:, channels], in1=inv_var[:], op=ALU.mult)
-    products = pools["scratch"].tile([P, span], F32, name="products")
-    column = SLABS + chunk
-    nc.vector.scalar_tensor_tensor(
-        out=products[:],
-        in0=mean[:, channels],
-        scalar=1.0,
-        in1=mean_iv[:],
-        op0=ALU.mult,
-        op1=ALU.mult,
-        accum_out=sums["columns_sb"][:, column : column + 1],
-    )
-    for g in range(PAIR):
-        flipped = pools["bank"].tile([P, PACK, COMPONENTS], F32, name="miv_flipped", tag="bank")
-        for t in range(PACK):
-            u, e = divmod(t, HALVES)
-            first = (g * WORDS + u) * HALVES * P
-            nc.tensor.transpose(
-                flipped[:, t, :],
-                mean_iv[:, first + e : first + HALVES * P : HALVES],
-                consts["ident"][:],
-            )
-        nc.scalar.copy(
-            out=operand[:, g, :].rearrange("p (m t) -> p m t", t=PACK),
-            in_=flipped[:].rearrange("p t m -> p m t"),
-        )
-
-
-def prepare_weights(nc, pools, consts, log_var, mean, chunk, sums):
-    grouped = pools["weights"].tile(
-        [P, 2, PASSES_PER_CHUNK, COMPONENTS * PACK], BF16, name="w_grouped", align_bytes=64
-    )
-    for h in range(PASSES_PER_CHUNK // PAIR):
-        pair = slice(h * PAIR, (h + 1) * PAIR)
-        lv_bank, lv = flip_words(nc, pools, consts, log_var, h, "lv_flipped")
-        nc.scalar.activation(out=by_word(grouped[:, 0, pair, :]), in_=lv, func=ACT.Exp, scale=-1.0)
-        operand = grouped[:, 1, pair, :]
-        if h == 0:
-            mean_operand_turned(nc, pools, consts, mean, lv, operand, chunk, h, sums)
-        else:
-            mean_operand_natural(nc, pools, consts, log_var, mean, operand, chunk, h, sums)
-        by_channel = pools["turned"].tile([P, WORDS, PAIR, COMPONENTS], F32, name="lv_by_channel")
-        nc.scalar.copy(out=by_channel[:], in_=lv_bank[:])
-        lv_values = by_channel[:].bitcast(BF16)
-        for g in range(PAIR):
-            for t in range(PACK):
-                slab = (chunk * PASSES_PER_CHUNK + h * PAIR + g) * PACK + t
-                nc.tensor.matmul(
-                    out=sums["columns"][:, slab : slab + 1],
-                    lhsT=lv_values[:, t // HALVES, g, t % HALVES :: HALVES],
-                    rhs=consts["ones_bf"][:],
-                    start=True,
-                    stop=True,
-                )
-
-    codes = pools["weights"].tile(
-        [P, 2, PASSES_PER_CHUNK, COMPONENTS], U32, name="w_codes", align_bytes=64
-    )
-    scales = pools["weights"].tile(
-        [P, 2, PASSES_PER_CHUNK, COMPONENTS], U8, name="w_scales", align_bytes=64
-    )
-    nc.vector.quantize_mx(
-        out=codes[:].rearrange("p a g m -> p (a g m)").bitcast(FP8X4),
-        scales=scales[:].rearrange("p a g m -> p (a g m)"),
-        in_=grouped[:].rearrange("p a g w -> p (a g w)"),
-    )
-    return codes, scales
-
-
-def quantise_x_pass(nc, pools, raw, squares_on_vector):
-    source = raw.rearrange("p t (c i) -> p c t i", i=RUN)
-    plain = pools["x"].tile([P, ROWS * PACK], BF16, name="x_grouped", align_bytes=64)
-    nc.vector.tensor_copy(
-        out=plain[:].rearrange("p (c i t) -> p c t i", i=RUN, t=PACK), in_=source
-    )
-    squares = pools["x"].tile([P, ROWS * PACK], BF16, name="x2_grouped", align_bytes=64)
-    if squares_on_vector:
-        nc.vector.tensor_tensor(out=squares[:], in0=plain[:], in1=plain[:], op=ALU.mult)
-    else:
-        nc.scalar.activation(
-            out=squares[:].rearrange("p (c i t) -> p c t i", i=RUN, t=PACK),
-            in_=source,
-            func=ACT.Square,
-        )
-    quantised = []
-    for pair, grouped in enumerate((squares, plain)):
-        codes = pools["x"].tile([P, ROWS], U32, name="x_codes%d" % pair, align_bytes=64)
-        scales = pools["x"].tile([P, ROWS], U8, name="x_scales%d" % pair, align_bytes=64)
-        nc.vector.quantize_mx(out=codes[:].bitcast(FP8X4), scales=scales[:], in_=grouped[:])
-        quantised.append((codes, scales))
-    return quantised
-
-
-def component_bias(nc, pools, consts, sums):
-    const = pools["const"]
-    columns = sums["columns_sb"]
-    nc.vector.tensor_copy(out=columns[:, 0:SLABS], in_=sums["columns"][:])
-    shifted = pools["bank"].tile([P, SLABS + CHUNKS], F32, name="shifted", tag="bank")
-    nc.tensor.matmul(
-        out=shifted[:], lhsT=consts["minus_first"][:], rhs=columns[:], start=True, stop=True
-    )
-    total = const.tile([P, 1], F32, name="bias_total")
-    nc.vector.tensor_reduce(out=total[:], in_=shifted[:], axis=AXIS_X, op=ALU.add)
-    on_diagonal = const.tile([P, COMPONENTS], F32, name="on_diagonal")
-    diagonal = const.tile([P, 1], F32, name="diagonal_sum")
-    nc.vector.scalar_tensor_tensor(
-        out=on_diagonal[:],
-        in0=sums["diagonal"][:],
-        scalar=1.0,
-        in1=consts["ident"][:],
-        op0=ALU.mult,
-        op1=ALU.mult,
-        accum_out=diagonal[:],
-    )
-    both = const.tile([P, 1], F32, name="bias_both")
-    nc.vector.tensor_tensor(out=both[:], in0=total[:], in1=diagonal[:], op=ALU.add)
-    bias = const.tile([P, 1], F32, name="bias")
-    nc.vector.scalar_tensor_tensor(
-        out=bias[:],
-        in0=both[:],
-        scalar=-0.5,
-        in1=consts["log_weight"][:],
-        op0=ALU.mult,
-        op1=ALU.add,
-    )
-    return bias
+def x_slot(j):
+    spread = SLOTS // (X_OF_SLOTS + 1) * X_OF_SLOTS
+    return j + j // X_OF_SLOTS if j < spread else SLOTS + j - spread
 
 
 def anomaly_scores(nc, pools, consts, p_acc, q_acc, bias, out):
@@ -268,6 +116,46 @@ def anomaly_scores(nc, pools, consts, p_acc, q_acc, bias, out):
     )
 
 
+def centred_sums(nc, pools, consts, sums):
+    const = pools["const"]
+    columns = sums["columns_sb"]
+    nc.vector.tensor_copy(out=columns[:, 0:SLABS], in_=sums["columns"][:])
+    shifted = pools["bank"].tile([P, SLABS + CHUNKS], F32, name="shifted", tag="bank")
+    nc.tensor.matmul(
+        out=shifted[:], lhsT=consts["minus_first"][:], rhs=columns[:], start=True, stop=True
+    )
+    on_diagonal = const.tile([P, COMPONENTS], F32, name="on_diagonal")
+    diagonal = const.tile([P, 1], F32, name="diagonal_sum")
+    nc.vector.scalar_tensor_tensor(
+        out=on_diagonal[:],
+        in0=sums["diagonal"][:],
+        scalar=1.0,
+        in1=consts["ident"][:],
+        op0=ALU.mult,
+        op1=ALU.mult,
+        accum_out=diagonal[:],
+    )
+    return shifted, diagonal
+
+
+def component_bias(nc, pools, consts, shifted, diagonal):
+    const = pools["const"]
+    total = const.tile([P, 1], F32, name="bias_total")
+    nc.vector.tensor_reduce(out=total[:], in_=shifted[:], axis=AXIS_X, op=ALU.add)
+    both = const.tile([P, 1], F32, name="bias_both")
+    nc.vector.tensor_tensor(out=both[:], in0=total[:], in1=diagonal[:], op=ALU.add)
+    bias = const.tile([P, 1], F32, name="bias")
+    nc.vector.scalar_tensor_tensor(
+        out=bias[:],
+        in0=both[:],
+        scalar=-0.5,
+        in1=consts["log_weight"][:],
+        op0=ALU.mult,
+        op1=ALU.add,
+    )
+    return bias
+
+
 def tile_gmmoutlierdetector_k_kernel(tc, feats, means, log_vars, log_weights, out):
     nc = tc.nc
     x_passes = feats.rearrange("b (g u p e) h w -> b g u p e (h w)", u=WORDS, p=P, e=HALVES)
@@ -277,15 +165,17 @@ def tile_gmmoutlierdetector_k_kernel(tc, feats, means, log_vars, log_weights, ou
     with ExitStack() as stack:
         pools = {
             "const": stack.enter_context(tc.tile_pool(name="const", bufs=1)),
-            "load": stack.enter_context(tc.tile_pool(name="load", bufs=3)),
-            "raw": stack.enter_context(tc.tile_pool(name="raw", bufs=8)),
-            "turned": stack.enter_context(tc.tile_pool(name="turned", bufs=2)),
-            "natural": stack.enter_context(tc.tile_pool(name="natural", bufs=2)),
-            "scratch": stack.enter_context(tc.tile_pool(name="scratch", bufs=1)),
+            "load": stack.enter_context(tc.tile_pool(name="load", bufs=2)),
+            "raw": stack.enter_context(tc.tile_pool(name="raw", bufs=6)),
             "weights": stack.enter_context(tc.tile_pool(name="weights", bufs=2)),
-            "x": stack.enter_context(tc.tile_pool(name="x", bufs=3)),
+            "scratch": stack.enter_context(tc.tile_pool(name="scratch", bufs=1)),
+            "w_codes": stack.enter_context(tc.tile_pool(name="w_codes", bufs=3)),
+            "x": stack.enter_context(tc.tile_pool(name="x", bufs=5)),
+            "x_codes": stack.enter_context(tc.tile_pool(name="x_codes", bufs=8)),
             "acc": stack.enter_context(tc.psum_pool(name="acc", bufs=1)),
-            "bank": stack.enter_context(tc.psum_pool(name="bank", bufs=4)),
+            "lv": stack.enter_context(tc.psum_pool(name="lv", bufs=1)),
+            "mean": stack.enter_context(tc.psum_pool(name="mean", bufs=1)),
+            "bank": stack.enter_context(tc.psum_pool(name="bank", bufs=2)),
         }
         const = pools["const"]
 
@@ -302,62 +192,343 @@ def tile_gmmoutlierdetector_k_kernel(tc, feats, means, log_vars, log_weights, ou
         consts = {
             "ident": ident,
             "minus_first": minus_first,
-            "ones_bf": ones_bf,
             "score": score,
             "log_weight": log_weight,
         }
 
         p_acc = pools["acc"].tile([P, ROWS], F32, name="p_acc")
         q_acc = pools["acc"].tile([P, ROWS], F32, name="q_acc")
+        acc = [p_acc, q_acc]
         sums = {
             "diagonal": pools["acc"].tile([P, COMPONENTS], F32, name="c_diagonal"),
             "columns": pools["acc"].tile([P, SLABS], F32, name="columns"),
             "columns_sb": const.tile([P, SLABS + CHUNKS], F32, name="columns_sb"),
         }
-        acc = [p_acc, q_acc]
 
-        def weights_of(chunk):
-            k0 = chunk * CHUNK
-            log_var = pools["load"].tile([P, CHUNK], BF16, name="log_var")
-            nc.sync.dma_start(out=log_var[:], in_=log_var_rows[:, k0 : k0 + CHUNK])
-            mean = pools["load"].tile([P, CHUNK], BF16, name="mean")
-            nc.sync.dma_start(out=mean[:], in_=mean_rows[:, k0 : k0 + CHUNK])
-            return prepare_weights(nc, pools, consts, log_var, mean, chunk, sums)
+        stack.enter_context(tc.manual_schedule())
 
-        def load_x_pass(i):
-            raw = pools["raw"].tile([P, PACK, ROWS], BF16, name="raw")
+        loaded = {}
+        w = {}
+        weights = {}
+        raw, plain, squares = {}, {}, {}
+        x_codes = {}
+        quantised_at, weights_at = {}, {}
+
+        def load_weights(k):
+            loaded[k] = (
+                pools["load"].tile([P, CHUNK], BF16, name="log_var"),
+                pools["load"].tile([P, CHUNK], BF16, name="mean"),
+            )
+
+        def load_pair(k, pair, which):
+            rows = (log_var_rows, mean_rows)[which]
+            span = PAIR * K_PASS
+            nc.sync.dma_start(
+                out=loaded[k][which][:, pair * span : (pair + 1) * span],
+                in_=rows[:, k * CHUNK + pair * span : k * CHUNK + (pair + 1) * span],
+            )
+
+        def load_x(j):
+            raw[j] = pools["raw"].tile([P, PACK, ROWS], BF16, name="raw")
             for b in range(BATCH):
                 for u in range(WORDS):
                     nc.sync.dma_start(
-                        out=raw[:, u * HALVES : (u + 1) * HALVES, b * PIXELS : (b + 1) * PIXELS],
-                        in_=x_passes[b, i, u, :, :, :],
+                        out=raw[j][:, u * HALVES : (u + 1) * HALVES, b * PIXELS : (b + 1) * PIXELS],
+                        in_=x_passes[b, j, u, :, :, :],
                     )
-            return raw
 
-        raw_ahead = load_x_pass(0)
-        weights_ahead = weights_of(0)
-        nc.sync.dma_start(out=log_weight[:], in_=log_weights.rearrange("k (m o) -> (k m) o", o=1))
-        for i in range(PASSES):
-            chunk, g = divmod(i, PASSES_PER_CHUNK)
-            raw = raw_ahead
-            if i + 1 < PASSES:
-                raw_ahead = load_x_pass(i + 1)
-            if g == 0:
-                w_codes, w_scales = weights_ahead
-                if chunk + 1 < CHUNKS:
-                    weights_ahead = weights_of(chunk + 1)
-                else:
-                    bias = component_bias(nc, pools, consts, sums)
-            quantised = quantise_x_pass(nc, pools, raw[:], squares_on_vector=(g == PASSES_PER_CHUNK - 1))
-            for pair, (x_codes, x_scales) in enumerate(quantised):
+
+        def flip(k, pair, which, pool):
+            words = loaded[k][which][:].bitcast(F32)
+            bank = pools[pool].tile([P, WORDS, PAIR, COMPONENTS], F32, name=pool + "_bank")
+            for g in range(PAIR):
+                for u in range(WORDS):
+                    first = ((pair * PAIR + g) * WORDS + u) * P
+                    nc.tensor.transpose(bank[:, u, g, :], words[:, first : first + P], ident[:])
+            w[pool, k, pair] = bank
+
+        def group_tile(k, pair):
+            w["grouped", k, pair] = pools["weights"].tile(
+                [P, 2, PAIR, COMPONENTS * PACK], BF16, name="w_grouped%d" % pair, align_bytes=64
+            )
+
+        def inv_var_operand(k, pair):
+            nc.scalar.activation(
+                out=turned_words(w["grouped", k, pair][:, 0, :, :]),
+                in_=bank_values(w["lv", k, pair]),
+                func=ACT.Exp,
+                scale=-1.0,
+            )
+
+        def log_var_copy(k, pair):
+            by_channel = pools["weights"].tile(
+                [P, WORDS, PAIR, COMPONENTS], F32, name="by_channel%d" % pair
+            )
+            nc.scalar.copy(out=by_channel[:], in_=w["lv", k, pair][:])
+            w["by_channel", k, pair] = by_channel
+
+        def log_det_sums(k, pair, n):
+            values = w["by_channel", k, pair][:].bitcast(BF16)
+            g, t = divmod(n, PACK)
+            slab = (k * PASSES_PER_CHUNK + pair * PAIR + g) * PACK + t
+            nc.tensor.matmul(
+                out=sums["columns"][:, slab : slab + 1],
+                lhsT=values[:, t // HALVES, g, t % HALVES :: HALVES],
+                rhs=ones_bf[:],
+                start=True,
+                stop=True,
+            )
+
+        def quantise_weights(k, pair, slot):
+            codes = pools["w_codes"].tile(
+                [P, 2, PAIR, COMPONENTS], U32, name="w_codes%d" % pair, align_bytes=64
+            )
+            scales = pools["w_codes"].tile(
+                [P, 2, PAIR, COMPONENTS], U8, name="w_scales%d" % pair, align_bytes=64
+            )
+            nc.vector.quantize_mx(
+                out=codes[:].rearrange("p a g m -> p (a g m)").bitcast(FP8X4),
+                scales=scales[:].rearrange("p a g m -> p (a g m)"),
+                in_=w["grouped", k, pair][:].rearrange("p a g v -> p (a g v)"),
+            )
+            weights[k, pair] = (codes, scales)
+            weights_at[k, pair] = slot
+
+
+        span_natural = slice(NATURAL * PAIR * K_PASS, (NATURAL + 1) * PAIR * K_PASS)
+
+        def natural_inv_var(k):
+            inv_var = pools["weights"].tile([P, PAIR * K_PASS], F32, name="natural_inv_var")
+            nc.scalar.activation(
+                out=inv_var[:], in_=loaded[k][0][:, span_natural], func=ACT.Exp, scale=-1.0
+            )
+            w["natural_inv_var", k] = inv_var
+
+        def natural_mean_iv(k):
+            mean_iv = pools["weights"].tile([P, PAIR * K_PASS], F32, name="natural_mean_iv")
+            nc.vector.tensor_tensor(
+                out=mean_iv[:],
+                in0=loaded[k][1][:, span_natural],
+                in1=w["natural_inv_var", k][:],
+                op=ALU.mult,
+            )
+            w["natural_mean_iv", k] = mean_iv
+
+        def natural_c(k):
+            products = pools["scratch"].tile([P, PAIR * K_PASS], F32, name="products")
+            nc.vector.scalar_tensor_tensor(
+                out=products[:],
+                in0=loaded[k][1][:, span_natural],
+                scalar=1.0,
+                in1=w["natural_mean_iv", k][:],
+                op0=ALU.mult,
+                op1=ALU.mult,
+                accum_out=sums["columns_sb"][:, SLABS + k : SLABS + k + 1],
+            )
+
+        def natural_flip(k, g):
+            bank = pools["bank"].tile([P, PACK, COMPONENTS], F32, name="mean_iv_bank", tag="bank")
+            for t in range(PACK):
+                u, e = divmod(t, HALVES)
+                first = (g * WORDS + u) * HALVES * P
+                nc.tensor.transpose(
+                    bank[:, t, :],
+                    w["natural_mean_iv", k][:, first + e : first + HALVES * P : HALVES],
+                    ident[:],
+                )
+            w["mean_iv_bank", k, g] = bank
+
+        def natural_operand(k, g):
+            nc.scalar.copy(
+                out=w["grouped", k, NATURAL][:, 1, g, :].rearrange("p (m t) -> p m t", t=PACK),
+                in_=w["mean_iv_bank", k, g][:].rearrange("p t m -> p m t"),
+            )
+
+
+        def turned_inv_var(k):
+            inv_var = pools["weights"].tile([P, PAIR, COMPONENTS * PACK], F32, name="turned_inv_var")
+            nc.scalar.activation(
+                out=turned_words(inv_var[:]),
+                in_=bank_values(w["lv", k, TURNED]),
+                func=ACT.Exp,
+                scale=-1.0,
+            )
+            w["turned_inv_var", k] = inv_var
+
+        def turned_operand(k):
+            nc.vector.tensor_tensor(
+                out=turned_words(w["grouped", k, TURNED][:, 1, :, :]),
+                in0=bank_values(w["mean", k, TURNED]),
+                in1=turned_words(w["turned_inv_var", k][:]),
+                op=ALU.mult,
+            )
+
+        def turned_squares(k):
+            mean_sq = pools["weights"].tile([P, PACK, PAIR * COMPONENTS], F32, name="mean_sq")
+            nc.scalar.activation(
+                out=mean_sq[:].rearrange("p (u e) m -> p u e m", u=WORDS),
+                in_=bank_values(w["mean", k, TURNED]).rearrange("p m u e -> p u e m"),
+                func=ACT.Square,
+            )
+            w["mean_sq", k] = mean_sq
+
+        def turned_c(k, pair, n):
+            g, t = divmod(n, PACK)
+            nc.tensor.matmul(
+                out=sums["diagonal"][:],
+                lhsT=w["mean_sq", k][:, t, g * COMPONENTS : (g + 1) * COMPONENTS],
+                rhs=w["turned_inv_var", k][:, g, t::PACK],
+                start=(k == 0 and n == 0),
+                stop=(k == CHUNKS - 1 and n == PAIR * PACK - 1),
+            )
+
+
+        def regroup(j):
+            plain[j] = pools["x"].tile([P, ROWS * PACK], BF16, name="x_grouped", align_bytes=64)
+            nc.vector.tensor_copy(
+                out=plain[j][:].rearrange("p (c i t) -> p c t i", i=RUN, t=PACK),
+                in_=raw[j][:].rearrange("p t (c i) -> p c t i", i=RUN),
+            )
+
+        def square(j, on_vector):
+            squares[j] = pools["x"].tile([P, ROWS * PACK], BF16, name="x2_grouped", align_bytes=64)
+            if on_vector:
+                nc.vector.tensor_tensor(
+                    out=squares[j][:], in0=plain[j][:], in1=plain[j][:], op=ALU.mult
+                )
+            else:
+                nc.scalar.activation(out=squares[j][:], in_=plain[j][:], func=ACT.Square)
+
+        def quantise_x(j, which, slot):
+            source = (squares, plain)[which][j]
+            codes = pools["x_codes"].tile([P, ROWS], U32, name="x_codes%d" % which, align_bytes=64)
+            scales = pools["x_codes"].tile([P, ROWS], U8, name="x_scales%d" % which, align_bytes=64)
+            nc.vector.quantize_mx(out=codes[:].bitcast(FP8X4), scales=scales[:], in_=source[:])
+            x_codes[j, which] = (codes, scales)
+            if which == 0:
+                quantised_at[j] = slot
+
+        def multiply(j):
+            k, g = divmod(j, PASSES_PER_CHUNK)
+            pair, g = divmod(g, PAIR)
+            w_codes, w_scales = weights[k, pair]
+            for which in (1, 0):
+                codes, scales = x_codes[j, which]
                 nc.tensor.matmul_mx(
-                    out=acc[pair][:],
-                    lhsT=w_codes[:, pair, g, :].bitcast(FP8X4),
-                    lhsT_scale=w_scales[:, pair, g, :],
-                    rhs=x_codes[:].bitcast(FP8X4),
-                    rhs_scale=x_scales[:],
-                    start=(i == 0),
-                    stop=(i == PASSES - 1),
+                    out=acc[which][:],
+                    lhsT=w_codes[:, which, g, :].bitcast(FP8X4),
+                    lhsT_scale=w_scales[:, which, g, :],
+                    rhs=codes[:].bitcast(FP8X4),
+                    rhs_scale=scales[:],
+                    start=(j == 0),
+                    stop=(j == PASSES - 1),
                 )
 
+
+        x_at = {x_slot(j): j for j in range(PASSES)}
+        lead = 4
+        load_weights(0)
+        load_x(0)
+        load_pair(0, NATURAL, 0)
+        load_x(1)
+        load_pair(0, NATURAL, 1)
+        load_pair(0, TURNED, 0)
+        load_pair(0, TURNED, 1)
+        for j in range(2, lead):
+            load_x(j)
+        nc.sync.dma_start(out=log_weight[:], in_=log_weights.rearrange("k (m o) -> (k m) o", o=1))
+        flip(0, NATURAL, 0, "lv")
+
+        multiplied = 0
+        last_slot = x_slot(PASSES - 1)
+        fill = []
+        for slot in range(last_slot + 4):
+            k, g = divmod(slot, PASSES_PER_CHUNK)
+            j = x_at.get(slot)
+            squared = x_at.get(slot - 1)
+            finished = x_at.get(slot - 3)
+            preparing = k < CHUNKS
+
+            if j is not None and j + lead < PASSES:
+                load_x(j + lead)
+            if g == 0 and k + 1 < CHUNKS:
+                load_weights(k + 1)
+                for pair in (NATURAL, TURNED):
+                    for which in range(2):
+                        load_pair(k + 1, pair, which)
+
+            if preparing and g == 2:
+                for pass_of_pair in range(PAIR):
+                    natural_flip(k, pass_of_pair)
+            for step in range(2):
+                of = (multiplied // PASSES_PER_CHUNK, multiplied % PASSES_PER_CHUNK // PAIR)
+                if (
+                    multiplied < PASSES
+                    and quantised_at.get(multiplied, slot) < slot
+                    and weights_at.get(of, slot) < slot
+                ):
+                    multiply(multiplied)
+                    multiplied += 1
+
+            if j is not None:
+                regroup(j)
+
+            on_vector = slot not in x_at or slot > last_slot
+            scalar_square = squared is not None and not on_vector
+            if preparing and g == 0:
+                group_tile(k, NATURAL)
+                natural_inv_var(k)
+                inv_var_operand(k, NATURAL)
+                log_var_copy(k, NATURAL)
+            elif preparing and g == 1:
+                natural_mean_iv(k)
+            elif preparing and g == 2:
+                group_tile(k, TURNED)
+                inv_var_operand(k, TURNED)
+                log_var_copy(k, TURNED)
+                natural_c(k)
+            elif preparing and g == 3:
+                turned_operand(k)
+                turned_squares(k)
+            if scalar_square:
+                square(squared, False)
+            if preparing and g == 1:
+                turned_inv_var(k)
+            elif preparing and g == 2:
+                for pass_of_pair in range(PAIR):
+                    natural_operand(k, pass_of_pair)
+                fill += [(log_det_sums, k, NATURAL, n) for n in range(PAIR * PACK)]
+            elif preparing and g == 3:
+                if k + 1 < CHUNKS:
+                    flip(k + 1, NATURAL, 0, "lv")
+                for n in range(PAIR * PACK):
+                    fill += [(log_det_sums, k, TURNED, n), (turned_c, k, None, n)]
+            if g == 0 and 0 < k <= CHUNKS:
+                quantise_weights(k - 1, NATURAL, slot)
+            elif g == 1 and 0 < k <= CHUNKS:
+                quantise_weights(k - 1, TURNED, slot)
+            if squared is not None and on_vector:
+                square(squared, True)
+
+            if slot == SLOTS + 3:
+                halves = centred_sums(nc, pools, consts, sums)
+            if slot == SLOTS + 5:
+                bias = component_bias(nc, pools, consts, *halves)
+            if squared is not None:
+                quantise_x(squared, 1, slot)
+            if finished is not None:
+                quantise_x(finished, 0, slot)
+            due = fill[:FILL if slot < SLOTS - 1 else len(fill)]
+            fill = fill[len(due):]
+            for make, of_chunk, pair, n in due[:FILL // 2]:
+                make(of_chunk, pair, n)
+            if preparing and g == 0:
+                flip(k, TURNED, 0, "lv")
+                flip(k, TURNED, 1, "mean")
+            for make, of_chunk, pair, n in due[FILL // 2:]:
+                make(of_chunk, pair, n)
+
+        while multiplied < PASSES:
+            multiply(multiplied)
+            multiplied += 1
         anomaly_scores(nc, pools, consts, p_acc, q_acc, bias, out)

@@ -25,11 +25,10 @@ PER_CLASS = 8
 COMPONENTS = CLASSES * PER_CLASS
 ROW_TILES = ROWS // P
 
-PASSES_PER_CHUNK = 4
-CHUNK = PASSES_PER_CHUNK * K_PASS
-CHUNKS = CHANNELS // CHUNK
 PASSES = CHANNELS // K_PASS
 PAIR = 2
+SPAN = PAIR * K_PASS
+PAIRS = PASSES // PAIR
 HALVES = 2
 WORDS = PACK // HALVES
 
@@ -37,10 +36,12 @@ SLABS = PASSES * PACK
 RUN = 4
 
 
-NATURAL, TURNED = 0, 1
+NATURAL_EVERY = 3
 SLOTS = PASSES
-X_OF_SLOTS = 7
-FILL = 6
+X_OF_SLOTS = 15
+VECTOR_SQUARES = 5
+BEFORE = 2
+FILL = 7
 
 FLOPS = 2 * 2 * ROWS * COMPONENTS * CHANNELS
 
@@ -55,6 +56,14 @@ def bank_values(bank):
     )
 
 
+def natural_pair(q):
+    return q % NATURAL_EVERY == 0
+
+
+def vector_squares(j):
+    return j % VECTOR_SQUARES == VECTOR_SQUARES // 2 or j == PASSES - 1
+
+
 def x_slot(j):
     spread = SLOTS // (X_OF_SLOTS + 1) * X_OF_SLOTS
     return j + j // X_OF_SLOTS if j < spread else SLOTS + j - spread
@@ -65,51 +74,63 @@ def anomaly_scores(nc, pools, consts, p_acc, q_acc, bias, out):
     q_plus_bias = const.tile([P, ROWS], F32, name="q_plus_bias")
     nc.scalar.activation(out=q_plus_bias[:], in_=q_acc[:], func=ACT.Identity, bias=bias[:, 0:1])
     z_by_component = const.tile([P, ROWS], F32, name="z_by_component")
-    nc.vector.scalar_tensor_tensor(
-        out=z_by_component[:],
-        in0=p_acc[:],
-        scalar=-0.5,
-        in1=q_plus_bias[:],
-        op0=ALU.mult,
-        op1=ALU.add,
-    )
-    z = pools["bank"].tile([P, ROW_TILES, COMPONENTS], F32, name="z", tag="bank")
-    for j in range(ROW_TILES):
-        nc.tensor.transpose(z[:, j, :], z_by_component[:, j * P : (j + 1) * P], consts["ident"][:])
-
-    minus_top = const.tile([P, ROW_TILES], F32, name="minus_top")
-    nc.vector.tensor_reduce(out=minus_top[:], in_=z[:], axis=AXIS_X, op=ALU.max, negate=True)
+    half = ROWS // 2
+    tiles = ROW_TILES // 2
+    z, minus_top = [], []
+    for h in range(2):
+        rows = slice(h * half, (h + 1) * half)
+        nc.vector.scalar_tensor_tensor(
+            out=z_by_component[:, rows],
+            in0=p_acc[:, rows],
+            scalar=-0.5,
+            in1=q_plus_bias[:, rows],
+            op0=ALU.mult,
+            op1=ALU.add,
+        )
+        z.append(pools["bank"].tile([P, tiles, COMPONENTS], F32, name="z", tag="bank"))
+        for j in range(tiles):
+            first = h * half + j * P
+            nc.tensor.transpose(
+                z[h][:, j, :], z_by_component[:, first : first + P], consts["ident"][:]
+            )
     weight = const.tile([P, ROW_TILES, COMPONENTS], F32, name="weight")
     total = const.tile([P, ROW_TILES], F32, name="total")
-    for j in range(ROW_TILES):
-        nc.scalar.activation(
-            out=weight[:, j, :],
-            in_=z[:, j, :],
-            func=ACT.Exp,
-            bias=minus_top[:, j : j + 1],
-            accum_out=total[:, j : j + 1],
+    for h in range(2):
+        minus_top.append(const.tile([P, tiles], F32, name="minus_top%d" % h))
+        nc.vector.tensor_reduce(
+            out=minus_top[h][:], in_=z[h][:], axis=AXIS_X, op=ALU.max, negate=True
+        )
+        for j in range(tiles):
+            nc.scalar.activation(
+                out=weight[:, h * tiles + j, :],
+                in_=z[h][:, j, :],
+                func=ACT.Exp,
+                bias=minus_top[h][:, j : j + 1],
+                accum_out=total[:, h * tiles + j : h * tiles + j + 1],
+            )
+    class_sum = const.tile([P, ROW_TILES, CLASSES], F32, name="class_sum")
+    for h in range(2):
+        rows = slice(h * tiles, (h + 1) * tiles)
+        nc.vector.tensor_reduce(
+            out=class_sum[:, rows, :].rearrange("p j k -> p (j k)"),
+            in_=weight[:, rows, :].rearrange("p j (k m) -> p (j k) m", m=PER_CLASS),
+            axis=AXIS_X,
+            op=ALU.add,
         )
     inv_total = const.tile([P, ROW_TILES], F32, name="inv_total")
     nc.vector.reciprocal(out=inv_total[:], in_=total[:])
-    class_sum = const.tile([P, ROW_TILES, CLASSES], F32, name="class_sum")
-    nc.vector.tensor_reduce(
-        out=class_sum[:].rearrange("p j k -> p (j k)"),
-        in_=weight[:].rearrange("p j (k m) -> p (j k) m", m=PER_CLASS),
-        axis=AXIS_X,
-        op=ALU.add,
-    )
     largest = const.tile([P, ROW_TILES], F32, name="largest")
     nc.vector.tensor_reduce(out=largest[:], in_=class_sum[:], axis=AXIS_X, op=ALU.max)
-    others = const.tile([P, ROW_TILES], F32, name="others")
-    nc.vector.tensor_tensor(out=others[:], in0=total[:], in1=largest[:], op=ALU.subtract)
-    score = consts["score"]
+    top = consts["score"]
     nc.vector.tensor_tensor(
-        out=score[:, 0:ROW_TILES], in0=others[:], in1=inv_total[:], op=ALU.mult
+        out=top[:, 0:ROW_TILES], in0=largest[:], in1=inv_total[:], op=ALU.mult
     )
-    score_bank = pools["bank"].tile([P, PACK, P], F32, name="score_bank", tag="bank")
-    nc.tensor.transpose(score_bank[:, 0, :], score[:], consts["ident"][:])
+    top_bank = pools["bank"].tile([P, P], F32, name="top_bank", tag="bank")
+    nc.tensor.transpose(top_bank[:], top[:], consts["ident"][:])
     score_rows = const.tile([P, P], F32, name="score_rows")
-    nc.vector.tensor_copy(out=score_rows[:], in_=score_bank[:, 0, :])
+    nc.vector.tensor_scalar(
+        out=score_rows[:], in0=top_bank[:], scalar1=-1.0, scalar2=1.0, op0=ALU.mult, op1=ALU.add
+    )
     nc.sync.dma_start(
         out=out.rearrange("b (a h) w -> (b a) (h w)", a=ROW_TILES // BATCH),
         in_=score_rows[0:ROW_TILES, :],
@@ -120,7 +141,7 @@ def centred_sums(nc, pools, consts, sums):
     const = pools["const"]
     columns = sums["columns_sb"]
     nc.vector.tensor_copy(out=columns[:, 0:SLABS], in_=sums["columns"][:])
-    shifted = pools["bank"].tile([P, SLABS + CHUNKS], F32, name="shifted", tag="bank")
+    shifted = pools["bank"].tile([P, SLABS + PAIRS], F32, name="shifted", tag="bank")
     nc.tensor.matmul(
         out=shifted[:], lhsT=consts["minus_first"][:], rhs=columns[:], start=True, stop=True
     )
@@ -165,9 +186,10 @@ def tile_gmmoutlierdetector_k_kernel(tc, feats, means, log_vars, log_weights, ou
     with ExitStack() as stack:
         pools = {
             "const": stack.enter_context(tc.tile_pool(name="const", bufs=1)),
-            "load": stack.enter_context(tc.tile_pool(name="load", bufs=2)),
+            "load": stack.enter_context(tc.tile_pool(name="load", bufs=4)),
             "raw": stack.enter_context(tc.tile_pool(name="raw", bufs=6)),
-            "weights": stack.enter_context(tc.tile_pool(name="weights", bufs=2)),
+            "weights": stack.enter_context(tc.tile_pool(name="weights", bufs=3)),
+            "turned": stack.enter_context(tc.tile_pool(name="turned", bufs=3)),
             "scratch": stack.enter_context(tc.tile_pool(name="scratch", bufs=1)),
             "w_codes": stack.enter_context(tc.tile_pool(name="w_codes", bufs=3)),
             "x": stack.enter_context(tc.tile_pool(name="x", bufs=5)),
@@ -202,31 +224,24 @@ def tile_gmmoutlierdetector_k_kernel(tc, feats, means, log_vars, log_weights, ou
         sums = {
             "diagonal": pools["acc"].tile([P, COMPONENTS], F32, name="c_diagonal"),
             "columns": pools["acc"].tile([P, SLABS], F32, name="columns"),
-            "columns_sb": const.tile([P, SLABS + CHUNKS], F32, name="columns_sb"),
+            "columns_sb": const.tile([P, SLABS + PAIRS], F32, name="columns_sb"),
         }
+
+        nc.vector.memset(sums["columns_sb"][:, SLABS:], 0.0)
 
         stack.enter_context(tc.manual_schedule())
 
         loaded = {}
         w = {}
         weights = {}
-        raw, plain, squares = {}, {}, {}
-        x_codes = {}
+        raw, grouped, x_codes = {}, {}, {}
         quantised_at, weights_at = {}, {}
 
-        def load_weights(k):
-            loaded[k] = (
-                pools["load"].tile([P, CHUNK], BF16, name="log_var"),
-                pools["load"].tile([P, CHUNK], BF16, name="mean"),
-            )
-
-        def load_pair(k, pair, which):
-            rows = (log_var_rows, mean_rows)[which]
-            span = PAIR * K_PASS
-            nc.sync.dma_start(
-                out=loaded[k][which][:, pair * span : (pair + 1) * span],
-                in_=rows[:, k * CHUNK + pair * span : k * CHUNK + (pair + 1) * span],
-            )
+        def load_weights(q, which):
+            rows, name = ((log_var_rows, "log_var"), (mean_rows, "mean"))[which]
+            natural = pools["load"].tile([P, SPAN], BF16, name=name)
+            nc.sync.dma_start(out=natural[:], in_=rows[:, q * SPAN : (q + 1) * SPAN])
+            loaded[q, which] = natural
 
         def load_x(j):
             raw[j] = pools["raw"].tile([P, PACK, ROWS], BF16, name="raw")
@@ -238,39 +253,37 @@ def tile_gmmoutlierdetector_k_kernel(tc, feats, means, log_vars, log_weights, ou
                     )
 
 
-        def flip(k, pair, which, pool):
-            words = loaded[k][which][:].bitcast(F32)
+        def flip(q, which, pool):
+            words = loaded[q, which][:].bitcast(F32)
             bank = pools[pool].tile([P, WORDS, PAIR, COMPONENTS], F32, name=pool + "_bank")
             for g in range(PAIR):
                 for u in range(WORDS):
-                    first = ((pair * PAIR + g) * WORDS + u) * P
+                    first = (g * WORDS + u) * P
                     nc.tensor.transpose(bank[:, u, g, :], words[:, first : first + P], ident[:])
-            w[pool, k, pair] = bank
+            w[pool, q] = bank
 
-        def group_tile(k, pair):
-            w["grouped", k, pair] = pools["weights"].tile(
-                [P, 2, PAIR, COMPONENTS * PACK], BF16, name="w_grouped%d" % pair, align_bytes=64
+        def inv_var_operand(q):
+            w["grouped", q] = pools["weights"].tile(
+                [P, 2, PAIR, COMPONENTS * PACK], BF16, name="w_grouped", align_bytes=64
             )
-
-        def inv_var_operand(k, pair):
             nc.scalar.activation(
-                out=turned_words(w["grouped", k, pair][:, 0, :, :]),
-                in_=bank_values(w["lv", k, pair]),
+                out=turned_words(w["grouped", q][:, 0, :, :]),
+                in_=bank_values(w["lv", q]),
                 func=ACT.Exp,
                 scale=-1.0,
             )
 
-        def log_var_copy(k, pair):
+        def log_var_copy(q):
             by_channel = pools["weights"].tile(
-                [P, WORDS, PAIR, COMPONENTS], F32, name="by_channel%d" % pair
+                [P, WORDS, PAIR, COMPONENTS], F32, name="by_channel"
             )
-            nc.scalar.copy(out=by_channel[:], in_=w["lv", k, pair][:])
-            w["by_channel", k, pair] = by_channel
+            nc.scalar.copy(out=by_channel[:], in_=w["lv", q][:])
+            w["by_channel", q] = by_channel
 
-        def log_det_sums(k, pair, n):
-            values = w["by_channel", k, pair][:].bitcast(BF16)
+        def log_det_sum(q, n):
+            values = w["by_channel", q][:].bitcast(BF16)
             g, t = divmod(n, PACK)
-            slab = (k * PASSES_PER_CHUNK + pair * PAIR + g) * PACK + t
+            slab = (q * PAIR + g) * PACK + t
             nc.tensor.matmul(
                 out=sums["columns"][:, slab : slab + 1],
                 lhsT=values[:, t // HALVES, g, t % HALVES :: HALVES],
@@ -279,147 +292,147 @@ def tile_gmmoutlierdetector_k_kernel(tc, feats, means, log_vars, log_weights, ou
                 stop=True,
             )
 
-        def quantise_weights(k, pair, slot):
+        def quantise_weights(q, slot):
             codes = pools["w_codes"].tile(
-                [P, 2, PAIR, COMPONENTS], U32, name="w_codes%d" % pair, align_bytes=64
+                [P, 2, PAIR, COMPONENTS], U32, name="w_codes", align_bytes=64
             )
             scales = pools["w_codes"].tile(
-                [P, 2, PAIR, COMPONENTS], U8, name="w_scales%d" % pair, align_bytes=64
+                [P, 2, PAIR, COMPONENTS], U8, name="w_scales", align_bytes=64
             )
             nc.vector.quantize_mx(
                 out=codes[:].rearrange("p a g m -> p (a g m)").bitcast(FP8X4),
                 scales=scales[:].rearrange("p a g m -> p (a g m)"),
-                in_=w["grouped", k, pair][:].rearrange("p a g v -> p (a g v)"),
+                in_=w["grouped", q][:].rearrange("p a g v -> p (a g v)"),
             )
-            weights[k, pair] = (codes, scales)
-            weights_at[k, pair] = slot
+            weights[q] = (codes, scales)
+            weights_at[q] = slot
 
 
-        span_natural = slice(NATURAL * PAIR * K_PASS, (NATURAL + 1) * PAIR * K_PASS)
-
-        def natural_inv_var(k):
-            inv_var = pools["weights"].tile([P, PAIR * K_PASS], F32, name="natural_inv_var")
+        def natural_inv_var(q):
+            w["inv_var", q] = pools["weights"].tile([P, SPAN], F32, name="natural_inv_var")
             nc.scalar.activation(
-                out=inv_var[:], in_=loaded[k][0][:, span_natural], func=ACT.Exp, scale=-1.0
+                out=w["inv_var", q][:], in_=loaded[q, 0][:], func=ACT.Exp, scale=-1.0
             )
-            w["natural_inv_var", k] = inv_var
 
-        def natural_mean_iv(k):
-            mean_iv = pools["weights"].tile([P, PAIR * K_PASS], F32, name="natural_mean_iv")
+        def natural_mean_iv(q):
+            w["mean_iv", q] = pools["weights"].tile([P, SPAN], F32, name="natural_mean_iv")
             nc.vector.tensor_tensor(
-                out=mean_iv[:],
-                in0=loaded[k][1][:, span_natural],
-                in1=w["natural_inv_var", k][:],
-                op=ALU.mult,
+                out=w["mean_iv", q][:], in0=loaded[q, 1][:], in1=w["inv_var", q][:], op=ALU.mult
             )
-            w["natural_mean_iv", k] = mean_iv
 
-        def natural_c(k):
-            products = pools["scratch"].tile([P, PAIR * K_PASS], F32, name="products")
+        def natural_c(q):
+            products = pools["scratch"].tile([P, SPAN], F32, name="products")
             nc.vector.scalar_tensor_tensor(
                 out=products[:],
-                in0=loaded[k][1][:, span_natural],
+                in0=loaded[q, 1][:],
                 scalar=1.0,
-                in1=w["natural_mean_iv", k][:],
+                in1=w["mean_iv", q][:],
                 op0=ALU.mult,
                 op1=ALU.mult,
-                accum_out=sums["columns_sb"][:, SLABS + k : SLABS + k + 1],
+                accum_out=sums["columns_sb"][:, SLABS + q : SLABS + q + 1],
             )
 
-        def natural_flip(k, g):
+        def natural_flip(q, g):
             bank = pools["bank"].tile([P, PACK, COMPONENTS], F32, name="mean_iv_bank", tag="bank")
             for t in range(PACK):
                 u, e = divmod(t, HALVES)
                 first = (g * WORDS + u) * HALVES * P
                 nc.tensor.transpose(
                     bank[:, t, :],
-                    w["natural_mean_iv", k][:, first + e : first + HALVES * P : HALVES],
+                    w["mean_iv", q][:, first + e : first + HALVES * P : HALVES],
                     ident[:],
                 )
-            w["mean_iv_bank", k, g] = bank
+            w["mean_iv_bank", q, g] = bank
 
-        def natural_operand(k, g):
+        def natural_operand(q, g):
             nc.scalar.copy(
-                out=w["grouped", k, NATURAL][:, 1, g, :].rearrange("p (m t) -> p m t", t=PACK),
-                in_=w["mean_iv_bank", k, g][:].rearrange("p t m -> p m t"),
+                out=w["grouped", q][:, 1, g, :].rearrange("p (m t) -> p m t", t=PACK),
+                in_=w["mean_iv_bank", q, g][:].rearrange("p t m -> p m t"),
             )
 
 
-        def turned_inv_var(k):
-            inv_var = pools["weights"].tile([P, PAIR, COMPONENTS * PACK], F32, name="turned_inv_var")
+        def turned_inv_var(q):
+            w["inv_var", q] = pools["turned"].tile(
+                [P, PAIR, COMPONENTS * PACK], F32, name="turned_inv_var"
+            )
             nc.scalar.activation(
-                out=turned_words(inv_var[:]),
-                in_=bank_values(w["lv", k, TURNED]),
+                out=turned_words(w["inv_var", q][:]),
+                in_=bank_values(w["lv", q]),
                 func=ACT.Exp,
                 scale=-1.0,
             )
-            w["turned_inv_var", k] = inv_var
 
-        def turned_operand(k):
+        def turned_operand(q):
             nc.vector.tensor_tensor(
-                out=turned_words(w["grouped", k, TURNED][:, 1, :, :]),
-                in0=bank_values(w["mean", k, TURNED]),
-                in1=turned_words(w["turned_inv_var", k][:]),
+                out=turned_words(w["grouped", q][:, 1, :, :]),
+                in0=bank_values(w["mean", q]),
+                in1=turned_words(w["inv_var", q][:]),
                 op=ALU.mult,
             )
 
-        def turned_squares(k):
-            mean_sq = pools["weights"].tile([P, PACK, PAIR * COMPONENTS], F32, name="mean_sq")
+        def turned_squares(q):
+            w["mean_sq", q] = pools["turned"].tile(
+                [P, PACK, PAIR * COMPONENTS], F32, name="mean_sq"
+            )
             nc.scalar.activation(
-                out=mean_sq[:].rearrange("p (u e) m -> p u e m", u=WORDS),
-                in_=bank_values(w["mean", k, TURNED]).rearrange("p m u e -> p u e m"),
+                out=w["mean_sq", q][:].rearrange("p (u e) m -> p u e m", u=WORDS),
+                in_=bank_values(w["mean", q]).rearrange("p m u e -> p u e m"),
                 func=ACT.Square,
             )
-            w["mean_sq", k] = mean_sq
 
-        def turned_c(k, pair, n):
+        turned_pairs = [q for q in range(PAIRS) if not natural_pair(q)]
+
+        def turned_c(q, n):
             g, t = divmod(n, PACK)
             nc.tensor.matmul(
                 out=sums["diagonal"][:],
-                lhsT=w["mean_sq", k][:, t, g * COMPONENTS : (g + 1) * COMPONENTS],
-                rhs=w["turned_inv_var", k][:, g, t::PACK],
-                start=(k == 0 and n == 0),
-                stop=(k == CHUNKS - 1 and n == PAIR * PACK - 1),
+                lhsT=w["mean_sq", q][:, t, g * COMPONENTS : (g + 1) * COMPONENTS],
+                rhs=w["inv_var", q][:, g, t::PACK],
+                start=(q == turned_pairs[0] and n == 0),
+                stop=(q == turned_pairs[-1] and n == PAIR * PACK - 1),
             )
 
 
         def regroup(j):
-            plain[j] = pools["x"].tile([P, ROWS * PACK], BF16, name="x_grouped", align_bytes=64)
+            grouped[j] = pools["x"].tile(
+                [P, 2, ROWS * PACK], BF16, name="x_grouped", align_bytes=64
+            )
             nc.vector.tensor_copy(
-                out=plain[j][:].rearrange("p (c i t) -> p c t i", i=RUN, t=PACK),
+                out=grouped[j][:, 1, :].rearrange("p (c i t) -> p c t i", i=RUN, t=PACK),
                 in_=raw[j][:].rearrange("p t (c i) -> p c t i", i=RUN),
             )
 
         def square(j, on_vector):
-            squares[j] = pools["x"].tile([P, ROWS * PACK], BF16, name="x2_grouped", align_bytes=64)
+            plain = grouped[j][:, 1, :]
             if on_vector:
                 nc.vector.tensor_tensor(
-                    out=squares[j][:], in0=plain[j][:], in1=plain[j][:], op=ALU.mult
+                    out=grouped[j][:, 0, :], in0=plain, in1=plain, op=ALU.mult
                 )
             else:
-                nc.scalar.activation(out=squares[j][:], in_=plain[j][:], func=ACT.Square)
+                nc.scalar.activation(out=grouped[j][:, 0, :], in_=plain, func=ACT.Square)
 
-        def quantise_x(j, which, slot):
-            source = (squares, plain)[which][j]
-            codes = pools["x_codes"].tile([P, ROWS], U32, name="x_codes%d" % which, align_bytes=64)
-            scales = pools["x_codes"].tile([P, ROWS], U8, name="x_scales%d" % which, align_bytes=64)
-            nc.vector.quantize_mx(out=codes[:].bitcast(FP8X4), scales=scales[:], in_=source[:])
-            x_codes[j, which] = (codes, scales)
-            if which == 0:
-                quantised_at[j] = slot
+        def quantise_x(j, slot):
+            codes = pools["x_codes"].tile([P, 2, ROWS], U32, name="x_codes", align_bytes=64)
+            scales = pools["x_codes"].tile([P, 2, ROWS], U8, name="x_scales", align_bytes=64)
+            nc.vector.quantize_mx(
+                out=codes[:].rearrange("p a r -> p (a r)").bitcast(FP8X4),
+                scales=scales[:].rearrange("p a r -> p (a r)"),
+                in_=grouped[j][:].rearrange("p a v -> p (a v)"),
+            )
+            x_codes[j] = (codes, scales)
+            quantised_at[j] = slot
 
         def multiply(j):
-            k, g = divmod(j, PASSES_PER_CHUNK)
-            pair, g = divmod(g, PAIR)
-            w_codes, w_scales = weights[k, pair]
+            q, g = divmod(j, PAIR)
+            w_codes, w_scales = weights[q]
+            codes, scales = x_codes[j]
             for which in (1, 0):
-                codes, scales = x_codes[j, which]
                 nc.tensor.matmul_mx(
                     out=acc[which][:],
                     lhsT=w_codes[:, which, g, :].bitcast(FP8X4),
                     lhsT_scale=w_scales[:, which, g, :],
-                    rhs=codes[:].bitcast(FP8X4),
-                    rhs_scale=scales[:],
+                    rhs=codes[:, which, :].bitcast(FP8X4),
+                    rhs_scale=scales[:, which, :],
                     start=(j == 0),
                     stop=(j == PASSES - 1),
                 )
@@ -427,45 +440,43 @@ def tile_gmmoutlierdetector_k_kernel(tc, feats, means, log_vars, log_weights, ou
 
         x_at = {x_slot(j): j for j in range(PASSES)}
         lead = 4
-        load_weights(0)
         load_x(0)
-        load_pair(0, NATURAL, 0)
+        load_weights(0, 0)
         load_x(1)
-        load_pair(0, NATURAL, 1)
-        load_pair(0, TURNED, 0)
-        load_pair(0, TURNED, 1)
-        for j in range(2, lead):
-            load_x(j)
+        load_weights(0, 1)
+        load_x(2)
+        load_weights(1, 0)
+        load_weights(1, 1)
+        load_x(3)
         nc.sync.dma_start(out=log_weight[:], in_=log_weights.rearrange("k (m o) -> (k m) o", o=1))
-        flip(0, NATURAL, 0, "lv")
+        flip(0, 0, "lv")
 
         multiplied = 0
         last_slot = x_slot(PASSES - 1)
         fill = []
         for slot in range(last_slot + 4):
-            k, g = divmod(slot, PASSES_PER_CHUNK)
+            q, second = divmod(slot, PAIR)
+            made = []
             j = x_at.get(slot)
             squared = x_at.get(slot - 1)
             finished = x_at.get(slot - 3)
-            preparing = k < CHUNKS
+            preparing = q < PAIRS
 
             if j is not None and j + lead < PASSES:
                 load_x(j + lead)
-            if g == 0 and k + 1 < CHUNKS:
-                load_weights(k + 1)
-                for pair in (NATURAL, TURNED):
-                    for which in range(2):
-                        load_pair(k + 1, pair, which)
+            if not second and q + 2 < PAIRS:
+                for which in range(2):
+                    load_weights(q + 2, which)
 
-            if preparing and g == 2:
-                for pass_of_pair in range(PAIR):
-                    natural_flip(k, pass_of_pair)
+            before = q - 1
+            if not second and 0 <= before < PAIRS and natural_pair(before):
+                for g in range(PAIR):
+                    natural_flip(before, g)
             for step in range(2):
-                of = (multiplied // PASSES_PER_CHUNK, multiplied % PASSES_PER_CHUNK // PAIR)
                 if (
                     multiplied < PASSES
                     and quantised_at.get(multiplied, slot) < slot
-                    and weights_at.get(of, slot) < slot
+                    and weights_at.get(multiplied // PAIR, slot) < slot
                 ):
                     multiply(multiplied)
                     multiplied += 1
@@ -473,60 +484,55 @@ def tile_gmmoutlierdetector_k_kernel(tc, feats, means, log_vars, log_weights, ou
             if j is not None:
                 regroup(j)
 
-            on_vector = slot not in x_at or slot > last_slot
+            on_vector = squared is not None and vector_squares(squared)
             scalar_square = squared is not None and not on_vector
-            if preparing and g == 0:
-                group_tile(k, NATURAL)
-                natural_inv_var(k)
-                inv_var_operand(k, NATURAL)
-                log_var_copy(k, NATURAL)
-            elif preparing and g == 1:
-                natural_mean_iv(k)
-            elif preparing and g == 2:
-                group_tile(k, TURNED)
-                inv_var_operand(k, TURNED)
-                log_var_copy(k, TURNED)
-                natural_c(k)
-            elif preparing and g == 3:
-                turned_operand(k)
-                turned_squares(k)
+            if preparing and not second:
+                if natural_pair(q):
+                    natural_inv_var(q)
+                else:
+                    turned_inv_var(q)
+                inv_var_operand(q)
+                log_var_copy(q)
+                made += [(log_det_sum, q, n) for n in range(PAIR * PACK)]
+            elif preparing:
+                if natural_pair(q):
+                    natural_mean_iv(q)
+                else:
+                    turned_squares(q)
+                    turned_operand(q)
+                    made += [(turned_c, q, n) for n in range(PAIR * PACK)]
             if scalar_square:
                 square(squared, False)
-            if preparing and g == 1:
-                turned_inv_var(k)
-            elif preparing and g == 2:
-                for pass_of_pair in range(PAIR):
-                    natural_operand(k, pass_of_pair)
-                fill += [(log_det_sums, k, NATURAL, n) for n in range(PAIR * PACK)]
-            elif preparing and g == 3:
-                if k + 1 < CHUNKS:
-                    flip(k + 1, NATURAL, 0, "lv")
-                for n in range(PAIR * PACK):
-                    fill += [(log_det_sums, k, TURNED, n), (turned_c, k, None, n)]
-            if g == 0 and 0 < k <= CHUNKS:
-                quantise_weights(k - 1, NATURAL, slot)
-            elif g == 1 and 0 < k <= CHUNKS:
-                quantise_weights(k - 1, TURNED, slot)
+            if second and 0 <= before < PAIRS and natural_pair(before):
+                for g in range(PAIR):
+                    natural_operand(before, g)
+            if not second and 0 <= before < PAIRS:
+                if natural_pair(before):
+                    natural_c(before)
+                else:
+                    quantise_weights(before, slot)
+            if second and 0 <= before - 1 < PAIRS and natural_pair(before - 1):
+                quantise_weights(before - 1, slot)
             if squared is not None and on_vector:
                 square(squared, True)
 
-            if slot == SLOTS + 3:
+            if slot == last_slot:
                 halves = centred_sums(nc, pools, consts, sums)
-            if slot == SLOTS + 5:
+            if slot == last_slot + 2:
                 bias = component_bias(nc, pools, consts, *halves)
-            if squared is not None:
-                quantise_x(squared, 1, slot)
             if finished is not None:
-                quantise_x(finished, 0, slot)
-            due = fill[:FILL if slot < SLOTS - 1 else len(fill)]
+                quantise_x(finished, slot)
+            due = fill[:FILL if slot < SLOTS else len(fill)]
             fill = fill[len(due):]
-            for make, of_chunk, pair, n in due[:FILL // 2]:
-                make(of_chunk, pair, n)
-            if preparing and g == 0:
-                flip(k, TURNED, 0, "lv")
-                flip(k, TURNED, 1, "mean")
-            for make, of_chunk, pair, n in due[FILL // 2:]:
-                make(of_chunk, pair, n)
+            for make, of_pair, n in due[:BEFORE]:
+                make(of_pair, n)
+            if second and q + 1 < PAIRS:
+                flip(q + 1, 0, "lv")
+            if preparing and not second and not natural_pair(q):
+                flip(q, 1, "mean")
+            for make, of_pair, n in due[BEFORE:]:
+                make(of_pair, n)
+            fill += made
 
         while multiplied < PASSES:
             multiply(multiplied)

@@ -36,7 +36,7 @@ SLABS = PASSES * PACK
 RUN = 4
 
 
-NATURAL_EVERY = 3
+NATURAL_EVERY = 2
 SLOTS = PASSES
 X_OF_SLOTS = 15
 VECTOR_SQUARES = 5
@@ -61,7 +61,7 @@ def natural_pair(q):
 
 
 def vector_squares(j):
-    return j % VECTOR_SQUARES == VECTOR_SQUARES // 2 or j == PASSES - 1
+    return j % VECTOR_SQUARES == VECTOR_SQUARES // 2
 
 
 def x_slot(j):
@@ -411,15 +411,19 @@ def tile_gmmoutlierdetector_k_kernel(tc, feats, means, log_vars, log_weights, ou
             else:
                 nc.scalar.activation(out=grouped[j][:, 0, :], in_=plain, func=ACT.Square)
 
-        def quantise_x(j, slot):
-            codes = pools["x_codes"].tile([P, 2, ROWS], U32, name="x_codes", align_bytes=64)
-            scales = pools["x_codes"].tile([P, 2, ROWS], U8, name="x_scales", align_bytes=64)
+        def quantise_x(j, slot, first=0, count=2):
+            if j not in x_codes:
+                x_codes[j] = (
+                    pools["x_codes"].tile([P, 2, ROWS], U32, name="x_codes", align_bytes=64),
+                    pools["x_codes"].tile([P, 2, ROWS], U8, name="x_scales", align_bytes=64),
+                )
+            codes, scales = x_codes[j]
+            which = slice(first, first + count)
             nc.vector.quantize_mx(
-                out=codes[:].rearrange("p a r -> p (a r)").bitcast(FP8X4),
-                scales=scales[:].rearrange("p a r -> p (a r)"),
-                in_=grouped[j][:].rearrange("p a v -> p (a v)"),
+                out=codes[:, which, :].rearrange("p a r -> p (a r)").bitcast(FP8X4),
+                scales=scales[:, which, :].rearrange("p a r -> p (a r)"),
+                in_=grouped[j][:, which, :].rearrange("p a v -> p (a v)"),
             )
-            x_codes[j] = (codes, scales)
             quantised_at[j] = slot
 
         def multiply(j):
@@ -516,11 +520,12 @@ def tile_gmmoutlierdetector_k_kernel(tc, feats, means, log_vars, log_weights, ou
             if squared is not None and on_vector:
                 square(squared, True)
 
-            if slot == last_slot:
+            if finished == PASSES - 1:
+                quantise_x(finished, slot, 1, 1)
                 halves = centred_sums(nc, pools, consts, sums)
-            if slot == last_slot + 2:
+                quantise_x(finished, slot, 0, 1)
                 bias = component_bias(nc, pools, consts, *halves)
-            if finished is not None:
+            elif finished is not None:
                 quantise_x(finished, slot)
             due = fill[:FILL if slot < SLOTS else len(fill)]
             fill = fill[len(due):]

@@ -50,6 +50,10 @@ def turned_words(values):
     return values.rearrange("p g (m u e) -> p (g m) u e", u=WORDS, e=HALVES)
 
 
+def by_slab(tile_in):
+    return tile_in[:].rearrange("p (u e) m -> p u e m", u=WORDS)
+
+
 def bank_values(bank):
     return bank[:].rearrange("p u g m -> p u (g m)").bitcast(BF16).rearrange(
         "p u (m e) -> p m u e", e=HALVES
@@ -308,25 +312,34 @@ def tile_gmmoutlierdetector_k_kernel(tc, feats, means, log_vars, log_weights, ou
             weights_at[q] = slot
 
 
+        def parted(tile_in):
+            return tile_in[:].rearrange("c (m e) -> c e m", e=HALVES)
+
+        def even_odd(tile_out):
+            return tile_out[:].rearrange("c (e m) -> c e m", e=HALVES)
+
         def natural_inv_var(q):
             w["inv_var", q] = pools["weights"].tile([P, SPAN], F32, name="natural_inv_var")
             nc.scalar.activation(
-                out=w["inv_var", q][:], in_=loaded[q, 0][:], func=ACT.Exp, scale=-1.0
+                out=even_odd(w["inv_var", q]), in_=parted(loaded[q, 0]), func=ACT.Exp, scale=-1.0
             )
 
         def natural_mean_iv(q):
             w["mean_iv", q] = pools["weights"].tile([P, SPAN], F32, name="natural_mean_iv")
             nc.vector.tensor_tensor(
-                out=w["mean_iv", q][:], in0=loaded[q, 1][:], in1=w["inv_var", q][:], op=ALU.mult
+                out=even_odd(w["mean_iv", q]),
+                in0=parted(loaded[q, 1]),
+                in1=even_odd(w["inv_var", q]),
+                op=ALU.mult,
             )
 
         def natural_c(q):
             products = pools["scratch"].tile([P, SPAN], F32, name="products")
             nc.vector.scalar_tensor_tensor(
-                out=products[:],
-                in0=loaded[q, 1][:],
+                out=even_odd(products),
+                in0=parted(loaded[q, 1]),
                 scalar=1.0,
-                in1=w["mean_iv", q][:],
+                in1=even_odd(w["mean_iv", q]),
                 op0=ALU.mult,
                 op1=ALU.mult,
                 accum_out=sums["columns_sb"][:, SLABS + q : SLABS + q + 1],
@@ -336,11 +349,9 @@ def tile_gmmoutlierdetector_k_kernel(tc, feats, means, log_vars, log_weights, ou
             bank = pools["bank"].tile([P, PACK, COMPONENTS], F32, name="mean_iv_bank", tag="bank")
             for t in range(PACK):
                 u, e = divmod(t, HALVES)
-                first = (g * WORDS + u) * HALVES * P
+                first = ((e * PAIR + g) * WORDS + u) * P
                 nc.tensor.transpose(
-                    bank[:, t, :],
-                    w["mean_iv", q][:, first + e : first + HALVES * P : HALVES],
-                    ident[:],
+                    bank[:, t, :], w["mean_iv", q][:, first : first + P], ident[:]
                 )
             w["mean_iv_bank", q, g] = bank
 
@@ -353,11 +364,11 @@ def tile_gmmoutlierdetector_k_kernel(tc, feats, means, log_vars, log_weights, ou
 
         def turned_inv_var(q):
             w["inv_var", q] = pools["turned"].tile(
-                [P, PAIR, COMPONENTS * PACK], F32, name="turned_inv_var"
+                [P, PACK, PAIR * COMPONENTS], F32, name="turned_inv_var"
             )
             nc.scalar.activation(
-                out=turned_words(w["inv_var", q][:]),
-                in_=bank_values(w["lv", q]),
+                out=by_slab(w["inv_var", q]),
+                in_=bank_values(w["lv", q]).rearrange("p m u e -> p u e m"),
                 func=ACT.Exp,
                 scale=-1.0,
             )
@@ -366,7 +377,7 @@ def tile_gmmoutlierdetector_k_kernel(tc, feats, means, log_vars, log_weights, ou
             nc.vector.tensor_tensor(
                 out=turned_words(w["grouped", q][:, 1, :, :]),
                 in0=bank_values(w["mean", q]),
-                in1=turned_words(w["inv_var", q][:]),
+                in1=by_slab(w["inv_var", q]).rearrange("p u e m -> p m u e"),
                 op=ALU.mult,
             )
 
@@ -375,7 +386,7 @@ def tile_gmmoutlierdetector_k_kernel(tc, feats, means, log_vars, log_weights, ou
                 [P, PACK, PAIR * COMPONENTS], F32, name="mean_sq"
             )
             nc.scalar.activation(
-                out=w["mean_sq", q][:].rearrange("p (u e) m -> p u e m", u=WORDS),
+                out=by_slab(w["mean_sq", q]),
                 in_=bank_values(w["mean", q]).rearrange("p m u e -> p u e m"),
                 func=ACT.Square,
             )
@@ -384,10 +395,11 @@ def tile_gmmoutlierdetector_k_kernel(tc, feats, means, log_vars, log_weights, ou
 
         def turned_c(q, n):
             g, t = divmod(n, PACK)
+            columns = slice(g * COMPONENTS, (g + 1) * COMPONENTS)
             nc.tensor.matmul(
                 out=sums["diagonal"][:],
-                lhsT=w["mean_sq", q][:, t, g * COMPONENTS : (g + 1) * COMPONENTS],
-                rhs=w["inv_var", q][:, g, t::PACK],
+                lhsT=w["mean_sq", q][:, t, columns],
+                rhs=w["inv_var", q][:, t, columns],
                 start=(q == turned_pairs[0] and n == 0),
                 stop=(q == turned_pairs[-1] and n == PAIR * PACK - 1),
             )

@@ -39,8 +39,9 @@ RUN = 4
 NATURAL_EVERY = 2
 SLOTS = PASSES
 X_OF_SLOTS = 15
-VECTOR_SQUARES = 5
+VECTOR_SQUARES = 6
 BEFORE = 2
+LD_WIDTH = 32
 FILL = 7
 
 FLOPS = 2 * 2 * ROWS * COMPONENTS * CHANNELS
@@ -65,7 +66,7 @@ def natural_pair(q):
 
 
 def vector_squares(j):
-    return j % VECTOR_SQUARES == VECTOR_SQUARES // 2
+    return j % VECTOR_SQUARES == 0
 
 
 def x_slot(j):
@@ -144,7 +145,7 @@ def anomaly_scores(nc, pools, consts, p_acc, q_acc, bias, out):
 def centred_sums(nc, pools, consts, sums):
     const = pools["const"]
     columns = sums["columns_sb"]
-    nc.vector.tensor_copy(out=columns[:, 0:SLABS], in_=sums["columns"][:])
+    nc.vector.tensor_copy(out=columns[:, 0:SLABS], in_=sums["columns"][:, 0:SLABS])
     shifted = pools["bank"].tile([P, SLABS + PAIRS], F32, name="shifted", tag="bank")
     nc.tensor.matmul(
         out=shifted[:], lhsT=consts["minus_first"][:], rhs=columns[:], start=True, stop=True
@@ -210,8 +211,9 @@ def tile_gmmoutlierdetector_k_kernel(tc, feats, means, log_vars, log_weights, ou
         minus_first = const.tile([P, P], F32, name="minus_first")
         nc.vector.tensor_copy(out=minus_first[:], in_=ident[:])
         nc.vector.tensor_scalar_sub(out=minus_first[0:1, :], in0=ident[0:1, :], scalar1=1.0)
-        ones_bf = const.tile([P, 1], BF16, name="ones_bf")
-        nc.vector.memset(ones_bf[:], 1.0)
+        ones_bf = const.tile([P, LD_WIDTH], BF16, name="ones_bf")
+        nc.vector.memset(ones_bf[:], 0.0)
+        nc.vector.memset(ones_bf[:, 0:1], 1.0)
         score = const.tile([P, P], F32, name="score")
         nc.vector.memset(score[:], 0.0)
         log_weight = const.tile([P, 1], BF16, name="log_weight")
@@ -227,7 +229,7 @@ def tile_gmmoutlierdetector_k_kernel(tc, feats, means, log_vars, log_weights, ou
         acc = [p_acc, q_acc]
         sums = {
             "diagonal": pools["acc"].tile([P, COMPONENTS], F32, name="c_diagonal"),
-            "columns": pools["acc"].tile([P, SLABS], F32, name="columns"),
+            "columns": pools["acc"].tile([P, SLABS + LD_WIDTH], F32, name="columns"),
             "columns_sb": const.tile([P, SLABS + PAIRS], F32, name="columns_sb"),
         }
 
@@ -247,9 +249,10 @@ def tile_gmmoutlierdetector_k_kernel(tc, feats, means, log_vars, log_weights, ou
             nc.sync.dma_start(out=natural[:], in_=rows[:, q * SPAN : (q + 1) * SPAN])
             loaded[q, which] = natural
 
-        def load_x(j):
-            raw[j] = pools["raw"].tile([P, PACK, ROWS], BF16, name="raw")
-            for b in range(BATCH):
+        def load_x(j, only=None):
+            if j not in raw:
+                raw[j] = pools["raw"].tile([P, PACK, ROWS], BF16, name="raw")
+            for b in range(BATCH) if only is None else [only]:
                 for u in range(WORDS):
                     nc.sync.dma_start(
                         out=raw[j][:, u * HALVES : (u + 1) * HALVES, b * PIXELS : (b + 1) * PIXELS],
@@ -289,7 +292,7 @@ def tile_gmmoutlierdetector_k_kernel(tc, feats, means, log_vars, log_weights, ou
             g, t = divmod(n, PACK)
             slab = (q * PAIR + g) * PACK + t
             nc.tensor.matmul(
-                out=sums["columns"][:, slab : slab + 1],
+                out=sums["columns"][:, slab : slab + LD_WIDTH],
                 lhsT=values[:, t // HALVES, g, t % HALVES :: HALVES],
                 rhs=ones_bf[:],
                 start=True,
@@ -405,14 +408,15 @@ def tile_gmmoutlierdetector_k_kernel(tc, feats, means, log_vars, log_weights, ou
             )
 
 
-        def regroup(j):
+        def regroup(j, parts=1):
             grouped[j] = pools["x"].tile(
                 [P, 2, ROWS * PACK], BF16, name="x_grouped", align_bytes=64
             )
-            nc.vector.tensor_copy(
-                out=grouped[j][:, 1, :].rearrange("p (c i t) -> p c t i", i=RUN, t=PACK),
-                in_=raw[j][:].rearrange("p t (c i) -> p c t i", i=RUN),
-            )
+            out = grouped[j][:, 1, :].rearrange("p (c i t) -> p c t i", i=RUN, t=PACK)
+            source = raw[j][:].rearrange("p t (c i) -> p c t i", i=RUN)
+            for n in range(parts):
+                some = slice(n * ROWS // RUN // parts, (n + 1) * ROWS // RUN // parts)
+                nc.vector.tensor_copy(out=out[:, some, :, :], in_=source[:, some, :, :])
 
         def square(j, on_vector):
             plain = grouped[j][:, 1, :]
@@ -456,12 +460,13 @@ def tile_gmmoutlierdetector_k_kernel(tc, feats, means, log_vars, log_weights, ou
 
         x_at = {x_slot(j): j for j in range(PASSES)}
         lead = 4
-        load_x(0)
+        load_x(0, 0)
         load_weights(0, 0)
+        load_x(0, 1)
         load_x(1)
         load_weights(0, 1)
-        load_x(2)
         load_weights(1, 0)
+        load_x(2)
         load_weights(1, 1)
         load_x(3)
         nc.sync.dma_start(out=log_weight[:], in_=log_weights.rearrange("k (m o) -> (k m) o", o=1))
@@ -497,10 +502,12 @@ def tile_gmmoutlierdetector_k_kernel(tc, feats, means, log_vars, log_weights, ou
                     multiply(multiplied)
                     multiplied += 1
 
-            if j is not None:
-                regroup(j)
-
             on_vector = squared is not None and vector_squares(squared)
+            if on_vector:
+                square(squared, True)
+            if j is not None:
+                regroup(j, BATCH if j == 0 else 1)
+
             scalar_square = squared is not None and not on_vector
             if preparing and not second:
                 if natural_pair(q):
@@ -529,9 +536,6 @@ def tile_gmmoutlierdetector_k_kernel(tc, feats, means, log_vars, log_weights, ou
                     quantise_weights(before, slot)
             if second and 0 <= before - 1 < PAIRS and natural_pair(before - 1):
                 quantise_weights(before - 1, slot)
-            if squared is not None and on_vector:
-                square(squared, True)
-
             if finished == PASSES - 1:
                 quantise_x(finished, slot, 1, 1)
                 halves = centred_sums(nc, pools, consts, sums)

@@ -36,12 +36,11 @@ SLABS = PASSES * PACK
 RUN = 4
 
 
-NATURAL_EVERY = 2
+TURNED_EVERY = 4
 SLOTS = PASSES
 X_OF_SLOTS = 15
-VECTOR_SQUARES = 6
+VECTOR_SQUARES = 5
 BEFORE = 2
-LD_WIDTH = 32
 FILL = 7
 
 FLOPS = 2 * 2 * ROWS * COMPONENTS * CHANNELS
@@ -62,7 +61,7 @@ def bank_values(bank):
 
 
 def natural_pair(q):
-    return q % NATURAL_EVERY == 0
+    return q % TURNED_EVERY != TURNED_EVERY // 2
 
 
 def vector_squares(j):
@@ -145,7 +144,7 @@ def anomaly_scores(nc, pools, consts, p_acc, q_acc, bias, out):
 def centred_sums(nc, pools, consts, sums):
     const = pools["const"]
     columns = sums["columns_sb"]
-    nc.vector.tensor_copy(out=columns[:, 0:SLABS], in_=sums["columns"][:, 0:SLABS])
+    nc.vector.tensor_copy(out=columns[:, 0:SLABS], in_=sums["columns"][:])
     shifted = pools["bank"].tile([P, SLABS + PAIRS], F32, name="shifted", tag="bank")
     nc.tensor.matmul(
         out=shifted[:], lhsT=consts["minus_first"][:], rhs=columns[:], start=True, stop=True
@@ -211,9 +210,8 @@ def tile_gmmoutlierdetector_k_kernel(tc, feats, means, log_vars, log_weights, ou
         minus_first = const.tile([P, P], F32, name="minus_first")
         nc.vector.tensor_copy(out=minus_first[:], in_=ident[:])
         nc.vector.tensor_scalar_sub(out=minus_first[0:1, :], in0=ident[0:1, :], scalar1=1.0)
-        ones_bf = const.tile([P, LD_WIDTH], BF16, name="ones_bf")
-        nc.vector.memset(ones_bf[:], 0.0)
-        nc.vector.memset(ones_bf[:, 0:1], 1.0)
+        ones_bf = const.tile([P, 1], BF16, name="ones_bf")
+        nc.vector.memset(ones_bf[:], 1.0)
         score = const.tile([P, P], F32, name="score")
         nc.vector.memset(score[:], 0.0)
         log_weight = const.tile([P, 1], BF16, name="log_weight")
@@ -229,7 +227,7 @@ def tile_gmmoutlierdetector_k_kernel(tc, feats, means, log_vars, log_weights, ou
         acc = [p_acc, q_acc]
         sums = {
             "diagonal": pools["acc"].tile([P, COMPONENTS], F32, name="c_diagonal"),
-            "columns": pools["acc"].tile([P, SLABS + LD_WIDTH], F32, name="columns"),
+            "columns": pools["acc"].tile([P, SLABS], F32, name="columns"),
             "columns_sb": const.tile([P, SLABS + PAIRS], F32, name="columns_sb"),
         }
 
@@ -292,7 +290,7 @@ def tile_gmmoutlierdetector_k_kernel(tc, feats, means, log_vars, log_weights, ou
             g, t = divmod(n, PACK)
             slab = (q * PAIR + g) * PACK + t
             nc.tensor.matmul(
-                out=sums["columns"][:, slab : slab + LD_WIDTH],
+                out=sums["columns"][:, slab : slab + 1],
                 lhsT=values[:, t // HALVES, g, t % HALVES :: HALVES],
                 rhs=ones_bf[:],
                 start=True,

@@ -32,26 +32,23 @@ PAIRS = PASSES // PAIR
 HALVES = 2
 WORDS = PACK // HALVES
 
-SLABS = PASSES * PACK
-RUN = 4
+SLABS_OF_PAIR = PAIR * PACK
+LD_COLUMNS = PAIRS // 2 * SLABS_OF_PAIR
+RUN = 2
 
 
 TURNED_EVERY = 4
 SLOTS = PASSES
 X_OF_SLOTS = 15
-VECTOR_SQUARES = 5
+VECTOR_SQUARES = 12
 BEFORE = 2
-FILL = 7
+FILL = 6
 
 FLOPS = 2 * 2 * ROWS * COMPONENTS * CHANNELS
 
 
 def turned_words(values):
     return values.rearrange("p g (m u e) -> p (g m) u e", u=WORDS, e=HALVES)
-
-
-def by_slab(tile_in):
-    return tile_in[:].rearrange("p (u e) m -> p u e m", u=WORDS)
 
 
 def bank_values(bank):
@@ -62,6 +59,10 @@ def bank_values(bank):
 
 def natural_pair(q):
     return q % TURNED_EVERY != TURNED_EVERY // 2
+
+
+def copied_pair(q):
+    return q % 2 == 0
 
 
 def vector_squares(j):
@@ -144,35 +145,38 @@ def anomaly_scores(nc, pools, consts, p_acc, q_acc, bias, out):
 def centred_sums(nc, pools, consts, sums):
     const = pools["const"]
     columns = sums["columns_sb"]
-    nc.vector.tensor_copy(out=columns[:, 0:SLABS], in_=sums["columns"][:])
-    shifted = pools["bank"].tile([P, SLABS + PAIRS], F32, name="shifted", tag="bank")
+    nc.vector.tensor_copy(out=columns[:, 0:LD_COLUMNS], in_=sums["columns"][:])
+    slabs = const.tile([P, COMPONENTS], F32, name="slabs_sb")
+    nc.vector.tensor_scalar_sub(
+        out=slabs[:], in0=sums["slabs"][:], scalar1=sums["slabs"][:, 0:1]
+    )
+    width = LD_COLUMNS + PAIRS
+    shifted = pools["bank"].tile([P, width + 1], F32, name="shifted", tag="bank")
     nc.tensor.matmul(
-        out=shifted[:], lhsT=consts["minus_first"][:], rhs=columns[:], start=True, stop=True
+        out=shifted[:, 0:width],
+        lhsT=consts["minus_first"][:],
+        rhs=columns[:],
+        start=True,
+        stop=True,
     )
-    on_diagonal = const.tile([P, COMPONENTS], F32, name="on_diagonal")
-    diagonal = const.tile([P, 1], F32, name="diagonal_sum")
-    nc.vector.scalar_tensor_tensor(
-        out=on_diagonal[:],
-        in0=sums["diagonal"][:],
-        scalar=1.0,
-        in1=consts["ident"][:],
-        op0=ALU.mult,
-        op1=ALU.mult,
-        accum_out=diagonal[:],
+    nc.tensor.matmul(
+        out=shifted[:, width : width + 1],
+        lhsT=slabs[:],
+        rhs=consts["ones"][:],
+        start=True,
+        stop=True,
     )
-    return shifted, diagonal
+    return shifted
 
 
-def component_bias(nc, pools, consts, shifted, diagonal):
+def component_bias(nc, pools, consts, shifted):
     const = pools["const"]
     total = const.tile([P, 1], F32, name="bias_total")
     nc.vector.tensor_reduce(out=total[:], in_=shifted[:], axis=AXIS_X, op=ALU.add)
-    both = const.tile([P, 1], F32, name="bias_both")
-    nc.vector.tensor_tensor(out=both[:], in0=total[:], in1=diagonal[:], op=ALU.add)
     bias = const.tile([P, 1], F32, name="bias")
     nc.vector.scalar_tensor_tensor(
         out=bias[:],
-        in0=both[:],
+        in0=total[:],
         scalar=-0.5,
         in1=consts["log_weight"][:],
         op0=ALU.mult,
@@ -210,6 +214,10 @@ def tile_gmmoutlierdetector_k_kernel(tc, feats, means, log_vars, log_weights, ou
         minus_first = const.tile([P, P], F32, name="minus_first")
         nc.vector.tensor_copy(out=minus_first[:], in_=ident[:])
         nc.vector.tensor_scalar_sub(out=minus_first[0:1, :], in0=ident[0:1, :], scalar1=1.0)
+        ident_bf = const.tile([P, P], BF16, name="ident_bf")
+        make_identity(nc, ident_bf[:])
+        ones = const.tile([P, 1], F32, name="ones")
+        nc.vector.memset(ones[:], 1.0)
         ones_bf = const.tile([P, 1], BF16, name="ones_bf")
         nc.vector.memset(ones_bf[:], 1.0)
         score = const.tile([P, P], F32, name="score")
@@ -218,6 +226,7 @@ def tile_gmmoutlierdetector_k_kernel(tc, feats, means, log_vars, log_weights, ou
         consts = {
             "ident": ident,
             "minus_first": minus_first,
+            "ones": ones,
             "score": score,
             "log_weight": log_weight,
         }
@@ -226,12 +235,11 @@ def tile_gmmoutlierdetector_k_kernel(tc, feats, means, log_vars, log_weights, ou
         q_acc = pools["acc"].tile([P, ROWS], F32, name="q_acc")
         acc = [p_acc, q_acc]
         sums = {
-            "diagonal": pools["acc"].tile([P, COMPONENTS], F32, name="c_diagonal"),
-            "columns": pools["acc"].tile([P, SLABS], F32, name="columns"),
-            "columns_sb": const.tile([P, SLABS + PAIRS], F32, name="columns_sb"),
+            "columns": pools["acc"].tile([P, LD_COLUMNS], F32, name="columns"),
+            "slabs": pools["acc"].tile([P, COMPONENTS], F32, name="slabs"),
+            "columns_sb": const.tile([P, LD_COLUMNS + PAIRS], F32, name="columns_sb"),
         }
 
-        nc.vector.memset(sums["columns_sb"][:, SLABS:], 0.0)
 
         stack.enter_context(tc.manual_schedule())
 
@@ -285,17 +293,31 @@ def tile_gmmoutlierdetector_k_kernel(tc, feats, means, log_vars, log_weights, ou
             nc.scalar.copy(out=by_channel[:], in_=w["lv", q][:])
             w["by_channel", q] = by_channel
 
-        def log_det_sum(q, n):
+
+        def log_det_copied(q, n):
             values = w["by_channel", q][:].bitcast(BF16)
             g, t = divmod(n, PACK)
-            slab = (q * PAIR + g) * PACK + t
+            column = q // 2 * SLABS_OF_PAIR + n
             nc.tensor.matmul(
-                out=sums["columns"][:, slab : slab + 1],
+                out=sums["columns"][:, column : column + 1],
                 lhsT=values[:, t // HALVES, g, t % HALVES :: HALVES],
                 rhs=ones_bf[:],
                 start=True,
                 stop=True,
             )
+
+        def log_det_turned(q, n):
+            nc.tensor.matmul(
+                out=sums["slabs"][:],
+                lhsT=loaded[q, 0][:, n * P : (n + 1) * P],
+                rhs=ident_bf[:],
+                start=(q == 1 and n == 0),
+                stop=(q == PAIRS - 1 and n == SLABS_OF_PAIR - 1),
+            )
+
+        def c_column(q):
+            column = LD_COLUMNS + q
+            return sums["columns_sb"][:, column : column + 1]
 
         def quantise_weights(q, slot):
             codes = pools["w_codes"].tile(
@@ -313,46 +335,42 @@ def tile_gmmoutlierdetector_k_kernel(tc, feats, means, log_vars, log_weights, ou
             weights_at[q] = slot
 
 
-        def parted(tile_in):
-            return tile_in[:].rearrange("c (m e) -> c e m", e=HALVES)
-
-        def even_odd(tile_out):
-            return tile_out[:].rearrange("c (e m) -> c e m", e=HALVES)
-
         def natural_inv_var(q):
             w["inv_var", q] = pools["weights"].tile([P, SPAN], F32, name="natural_inv_var")
             nc.scalar.activation(
-                out=even_odd(w["inv_var", q]), in_=parted(loaded[q, 0]), func=ACT.Exp, scale=-1.0
+                out=w["inv_var", q][:], in_=loaded[q, 0][:], func=ACT.Exp, scale=-1.0
             )
 
         def natural_mean_iv(q):
             w["mean_iv", q] = pools["weights"].tile([P, SPAN], F32, name="natural_mean_iv")
             nc.vector.tensor_tensor(
-                out=even_odd(w["mean_iv", q]),
-                in0=parted(loaded[q, 1]),
-                in1=even_odd(w["inv_var", q]),
+                out=w["mean_iv", q][:],
+                in0=loaded[q, 1][:],
+                in1=w["inv_var", q][:],
                 op=ALU.mult,
             )
 
         def natural_c(q):
             products = pools["scratch"].tile([P, SPAN], F32, name="products")
             nc.vector.scalar_tensor_tensor(
-                out=even_odd(products),
-                in0=parted(loaded[q, 1]),
+                out=products[:],
+                in0=loaded[q, 1][:],
                 scalar=1.0,
-                in1=even_odd(w["mean_iv", q]),
+                in1=w["mean_iv", q][:],
                 op0=ALU.mult,
                 op1=ALU.mult,
-                accum_out=sums["columns_sb"][:, SLABS + q : SLABS + q + 1],
+                accum_out=c_column(q),
             )
 
         def natural_flip(q, g):
             bank = pools["bank"].tile([P, PACK, COMPONENTS], F32, name="mean_iv_bank", tag="bank")
             for t in range(PACK):
                 u, e = divmod(t, HALVES)
-                first = ((e * PAIR + g) * WORDS + u) * P
+                first = (g * WORDS + u) * HALVES * P
                 nc.tensor.transpose(
-                    bank[:, t, :], w["mean_iv", q][:, first : first + P], ident[:]
+                    bank[:, t, :],
+                    w["mean_iv", q][:, first + e : first + HALVES * P : HALVES],
+                    ident[:],
                 )
             w["mean_iv_bank", q, g] = bank
 
@@ -365,11 +383,11 @@ def tile_gmmoutlierdetector_k_kernel(tc, feats, means, log_vars, log_weights, ou
 
         def turned_inv_var(q):
             w["inv_var", q] = pools["turned"].tile(
-                [P, PACK, PAIR * COMPONENTS], F32, name="turned_inv_var"
+                [P, PAIR, COMPONENTS * PACK], F32, name="turned_inv_var"
             )
             nc.scalar.activation(
-                out=by_slab(w["inv_var", q]),
-                in_=bank_values(w["lv", q]).rearrange("p m u e -> p u e m"),
+                out=turned_words(w["inv_var", q][:]),
+                in_=bank_values(w["lv", q]),
                 func=ACT.Exp,
                 scale=-1.0,
             )
@@ -378,7 +396,7 @@ def tile_gmmoutlierdetector_k_kernel(tc, feats, means, log_vars, log_weights, ou
             nc.vector.tensor_tensor(
                 out=turned_words(w["grouped", q][:, 1, :, :]),
                 in0=bank_values(w["mean", q]),
-                in1=by_slab(w["inv_var", q]).rearrange("p u e m -> p m u e"),
+                in1=turned_words(w["inv_var", q][:]),
                 op=ALU.mult,
             )
 
@@ -387,22 +405,36 @@ def tile_gmmoutlierdetector_k_kernel(tc, feats, means, log_vars, log_weights, ou
                 [P, PACK, PAIR * COMPONENTS], F32, name="mean_sq"
             )
             nc.scalar.activation(
-                out=by_slab(w["mean_sq", q]),
+                out=w["mean_sq", q][:].rearrange("p (u e) m -> p u e m", u=WORDS),
                 in_=bank_values(w["mean", q]).rearrange("p m u e -> p u e m"),
                 func=ACT.Square,
             )
 
-        turned_pairs = [q for q in range(PAIRS) if not natural_pair(q)]
-
         def turned_c(q, n):
+            if n == 0:
+                w["diagonal", q] = pools["mean"].tile(
+                    [P, COMPONENTS], F32, name="diagonal", tag="mean_bank"
+                )
             g, t = divmod(n, PACK)
             columns = slice(g * COMPONENTS, (g + 1) * COMPONENTS)
             nc.tensor.matmul(
-                out=sums["diagonal"][:],
+                out=w["diagonal", q][:],
                 lhsT=w["mean_sq", q][:, t, columns],
-                rhs=w["inv_var", q][:, t, columns],
-                start=(q == turned_pairs[0] and n == 0),
-                stop=(q == turned_pairs[-1] and n == PAIR * PACK - 1),
+                rhs=w["inv_var", q][:, g, t::PACK],
+                start=(n == 0),
+                stop=(n == SLABS_OF_PAIR - 1),
+            )
+
+        def turned_c_out(q):
+            on_diagonal = pools["scratch"].tile([P, COMPONENTS], F32, name="on_diagonal")
+            nc.vector.scalar_tensor_tensor(
+                out=on_diagonal[:],
+                in0=w["diagonal", q][:],
+                scalar=1.0,
+                in1=ident[:],
+                op0=ALU.mult,
+                op1=ALU.mult,
+                accum_out=c_column(q),
             )
 
 
@@ -513,15 +545,17 @@ def tile_gmmoutlierdetector_k_kernel(tc, feats, means, log_vars, log_weights, ou
                 else:
                     turned_inv_var(q)
                 inv_var_operand(q)
-                log_var_copy(q)
-                made += [(log_det_sum, q, n) for n in range(PAIR * PACK)]
+                if copied_pair(q):
+                    log_var_copy(q)
+                log_det = log_det_copied if copied_pair(q) else log_det_turned
+                made += [(log_det, q, n) for n in range(SLABS_OF_PAIR)]
             elif preparing:
                 if natural_pair(q):
                     natural_mean_iv(q)
                 else:
                     turned_squares(q)
                     turned_operand(q)
-                    made += [(turned_c, q, n) for n in range(PAIR * PACK)]
+                    made += [(turned_c, q, n) for n in range(SLABS_OF_PAIR)]
             if scalar_square:
                 square(squared, False)
             if second and 0 <= before < PAIRS and natural_pair(before):
@@ -534,11 +568,13 @@ def tile_gmmoutlierdetector_k_kernel(tc, feats, means, log_vars, log_weights, ou
                     quantise_weights(before, slot)
             if second and 0 <= before - 1 < PAIRS and natural_pair(before - 1):
                 quantise_weights(before - 1, slot)
+            if not second and 0 <= q - 3 < PAIRS and not natural_pair(q - 3):
+                turned_c_out(q - 3)
             if finished == PASSES - 1:
                 quantise_x(finished, slot, 1, 1)
-                halves = centred_sums(nc, pools, consts, sums)
+                shifted = centred_sums(nc, pools, consts, sums)
                 quantise_x(finished, slot, 0, 1)
-                bias = component_bias(nc, pools, consts, *halves)
+                bias = component_bias(nc, pools, consts, shifted)
             elif finished is not None:
                 quantise_x(finished, slot)
             due = fill[:FILL if slot < SLOTS else len(fill)]

@@ -249,10 +249,16 @@ def tile_gmmoutlierdetector_k_kernel(tc, feats, means, log_vars, log_weights, ou
         raw, grouped, x_codes = {}, {}, {}
         quantised_at, weights_at = {}, {}
 
-        def load_weights(q, which):
+        def load_weights(q, which, parts=1):
             rows, name = ((log_var_rows, "log_var"), (mean_rows, "mean"))[which]
             natural = pools["load"].tile([P, SPAN], BF16, name=name)
-            nc.sync.dma_start(out=natural[:], in_=rows[:, q * SPAN : (q + 1) * SPAN])
+            width = SPAN // parts
+            for n in range(parts):
+                first = q * SPAN + n * width
+                nc.sync.dma_start(
+                    out=natural[:, n * width : (n + 1) * width],
+                    in_=rows[:, first : first + width],
+                )
             loaded[q, which] = natural
 
         def load_x(j, only=None):
@@ -335,11 +341,17 @@ def tile_gmmoutlierdetector_k_kernel(tc, feats, means, log_vars, log_weights, ou
             weights_at[q] = slot
 
 
-        def natural_inv_var(q):
+        def natural_inv_var(q, parts=1):
             w["inv_var", q] = pools["weights"].tile([P, SPAN], F32, name="natural_inv_var")
-            nc.scalar.activation(
-                out=w["inv_var", q][:], in_=loaded[q, 0][:], func=ACT.Exp, scale=-1.0
-            )
+            width = SPAN // parts
+            for n in range(parts):
+                some = slice(n * width, (n + 1) * width)
+                nc.scalar.activation(
+                    out=w["inv_var", q][:, some],
+                    in_=loaded[q, 0][:, some],
+                    func=ACT.Exp,
+                    scale=-1.0,
+                )
 
         def natural_mean_iv(q):
             w["mean_iv", q] = pools["weights"].tile([P, SPAN], F32, name="natural_mean_iv")
@@ -491,11 +503,11 @@ def tile_gmmoutlierdetector_k_kernel(tc, feats, means, log_vars, log_weights, ou
         x_at = {x_slot(j): j for j in range(PASSES)}
         lead = 4
         load_x(0, 0)
-        load_weights(0, 0)
+        load_weights(0, 0, 2)
         load_x(0, 1)
+        load_weights(1, 0)
         load_x(1)
         load_weights(0, 1)
-        load_weights(1, 0)
         load_x(2)
         load_weights(1, 1)
         load_x(3)
@@ -541,7 +553,7 @@ def tile_gmmoutlierdetector_k_kernel(tc, feats, means, log_vars, log_weights, ou
             scalar_square = squared is not None and not on_vector
             if preparing and not second:
                 if natural_pair(q):
-                    natural_inv_var(q)
+                    natural_inv_var(q, 2 if q == 0 else 1)
                 else:
                     turned_inv_var(q)
                 inv_var_operand(q)
@@ -572,8 +584,10 @@ def tile_gmmoutlierdetector_k_kernel(tc, feats, means, log_vars, log_weights, ou
                 turned_c_out(q - 3)
             if finished == PASSES - 1:
                 quantise_x(finished, slot, 1, 1)
-                shifted = centred_sums(nc, pools, consts, sums)
                 quantise_x(finished, slot, 0, 1)
+            elif finished == PASSES - 2:
+                shifted = centred_sums(nc, pools, consts, sums)
+                quantise_x(finished, slot)
                 bias = component_bias(nc, pools, consts, shifted)
             elif finished is not None:
                 quantise_x(finished, slot)

from contextlib import ExitStack

import concourse.mybir as mybir
from concourse.masks import make_identity

F32 = mybir.dt.float32
BF16 = mybir.dt.bfloat16
U32 = mybir.dt.uint32
U8 = mybir.dt.uint8
FP8X4 = mybir.dt.float8_e4m3fn_x4
ALU = mybir.AluOpType
ACT = mybir.ActivationFunctionType
AXIS_X = mybir.AxisListType.X

P = 128
PACK = 4
K_PASS = P * PACK

BATCH = 2
CHANNELS = 16384
PIXELS = 256
ROWS = BATCH * PIXELS
CLASSES = 16
PER_CLASS = 8
COMPONENTS = CLASSES * PER_CLASS
ROW_TILES = ROWS // P

PASSES = CHANNELS // K_PASS
PAIR = 2
SPAN = PAIR * K_PASS
PAIRS = PASSES // PAIR
HALVES = 2
WORDS = PACK // HALVES

SLABS_OF_PAIR = PAIR * PACK
LD_COLUMNS = PAIRS // 2 * SLABS_OF_PAIR
RUN = 2


TURNED_EVERY = 4
SLOTS = PASSES
X_OF_SLOTS = 15
VECTOR_SQUARES = 12
BEFORE = 2
FILL = 6

FLOPS = 2 * 2 * ROWS * COMPONENTS * CHANNELS


def turned_words(values):
    return values.rearrange("p g (m u e) -> p (g m) u e", u=WORDS, e=HALVES)


def bank_values(bank):
    return bank[:].rearrange("p u g m -> p u (g m)").bitcast(BF16).rearrange(
        "p u (m e) -> p m u e", e=HALVES
    )


def natural_pair(q):
    return q % TURNED_EVERY != TURNED_EVERY // 2


def copied_pair(q):
    return q % 2 == 0


def vector_squares(j):
    return j % VECTOR_SQUARES == 0


def x_slot(j):
    spread = SLOTS // (X_OF_SLOTS + 1) * X_OF_SLOTS
    return j + j // X_OF_SLOTS if j < spread else SLOTS + j - spread


def anomaly_scores(nc, pools, consts, p_acc, q_acc, bias, out):
    const = pools["const"]
    q_plus_bias = const.tile([P, ROWS], F32, name="q_plus_bias")
    nc.scalar.activation(out=q_plus_bias[:], in_=q_acc[:], func=ACT.Identity, bias=bias[:, 0:1])
    z_by_component = const.tile([P, ROWS], F32, name="z_by_component")
    half = ROWS // 2
    tiles = ROW_TILES // 2
    z, minus_top = [], []
    for h in range(2):
        rows = slice(h * half, (h + 1) * half)
        nc.vector.scalar_tensor_tensor(
            out=z_by_component[:, rows],
            in0=p_acc[:, rows],
            scalar=-0.5,
            in1=q_plus_bias[:, rows],
            op0=ALU.mult,
            op1=ALU.add,
        )
        z.append(pools["bank"].tile([P, tiles, COMPONENTS], F32, name="z", tag="bank"))
        for j in range(tiles):
            first = h * half + j * P
            nc.tensor.transpose(
                z[h][:, j, :], z_by_component[:, first : first + P], consts["ident"][:]
            )
    weight = const.tile([P, ROW_TILES, COMPONENTS], F32, name="weight")
    total = const.tile([P, ROW_TILES], F32, name="total")
    for h in range(2):
        minus_top.append(const.tile([P, tiles], F32, name="minus_top%d" % h))
        nc.vector.tensor_reduce(
            out=minus_top[h][:], in_=z[h][:], axis=AXIS_X, op=ALU.max, negate=True
        )
        for j in range(tiles):
            nc.scalar.activation(
                out=weight[:, h * tiles + j, :],
                in_=z[h][:, j, :],
                func=ACT.Exp,
                bias=minus_top[h][:, j : j + 1],
                accum_out=total[:, h * tiles + j : h * tiles + j + 1],
            )
    class_sum = const.tile([P, ROW_TILES, CLASSES], F32, name="class_sum")
    for h in range(2):
        rows = slice(h * tiles, (h + 1) * tiles)
        nc.vector.tensor_reduce(
            out=class_sum[:, rows, :].rearrange("p j k -> p (j k)"),
            in_=weight[:, rows, :].rearrange("p j (k m) -> p (j k) m", m=PER_CLASS),
            axis=AXIS_X,
            op=ALU.add,
        )
    inv_total = const.tile([P, ROW_TILES], F32, name="inv_total")
    nc.vector.reciprocal(out=inv_total[:], in_=total[:])
    largest = const.tile([P, ROW_TILES], F32, name="largest")
    nc.vector.tensor_reduce(out=largest[:], in_=class_sum[:], axis=AXIS_X, op=ALU.max)
    top = consts["score"]
    nc.vector.tensor_tensor(
        out=top[:, 0:ROW_TILES], in0=largest[:], in1=inv_total[:], op=ALU.mult
    )
    top_bank = pools["bank"].tile([P, P], F32, name="top_bank", tag="bank")
    nc.tensor.transpose(top_bank[:], top[:], consts["ident"][:])
    score_rows = const.tile([P, P], F32, name="score_rows")
    nc.vector.tensor_scalar(
        out=score_rows[:], in0=top_bank[:], scalar1=-1.0, scalar2=1.0, op0=ALU.mult, op1=ALU.add
    )
    nc.sync.dma_start(
        out=out.rearrange("b (a h) w -> (b a) (h w)", a=ROW_TILES // BATCH),
        in_=score_rows[0:ROW_TILES, :],
    )


def centred_sums(nc, pools, consts, sums):
    const = pools["const"]
    columns = sums["columns_sb"]
    nc.vector.tensor_copy(out=columns[:, 0:LD_COLUMNS], in_=sums["columns"][:])
    slabs = const.tile([P, COMPONENTS], F32, name="slabs_sb")
    nc.vector.tensor_scalar_sub(
        out=slabs[:], in0=sums["slabs"][:], scalar1=sums["slabs"][:, 0:1]
    )
    width = LD_COLUMNS + PAIRS
    shifted = pools["bank"].tile([P, width + 1], F32, name="shifted", tag="bank")
    nc.tensor.matmul(
        out=shifted[:, 0:width],
        lhsT=consts["minus_first"][:],
        rhs=columns[:],
        start=True,
        stop=True,
    )
    nc.tensor.matmul(
        out=shifted[:, width : width + 1],
        lhsT=slabs[:],
        rhs=consts["ones"][:],
        start=True,
        stop=True,
    )
    return shifted


def component_bias(nc, pools, consts, shifted):
    const = pools["const"]
    total = const.tile([P, 1], F32, name="bias_total")
    nc.vector.tensor_reduce(out=total[:], in_=shifted[:], axis=AXIS_X, op=ALU.add)
    bias = const.tile([P, 1], F32, name="bias")
    nc.vector.scalar_tensor_tensor(
        out=bias[:],
        in0=total[:],
        scalar=-0.5,
        in1=consts["log_weight"][:],
        op0=ALU.mult,
        op1=ALU.add,
    )
    return bias


def tile_gmmoutlierdetector_k_kernel(tc, feats, means, log_vars, log_weights, out):
    nc = tc.nc
    x_passes = feats.rearrange("b (g u p e) h w -> b g u p e (h w)", u=WORDS, p=P, e=HALVES)
    mean_rows = means.rearrange("k m d -> (k m) d")
    log_var_rows = log_vars.rearrange("k m d -> (k m) d")

    with ExitStack() as stack:
        pools = {
            "const": stack.enter_context(tc.tile_pool(name="const", bufs=1)),
            "load": stack.enter_context(tc.tile_pool(name="load", bufs=4)),
            "raw": stack.enter_context(tc.tile_pool(name="raw", bufs=6)),
            "weights": stack.enter_context(tc.tile_pool(name="weights", bufs=3)),
            "turned": stack.enter_context(tc.tile_pool(name="turned", bufs=3)),
            "scratch": stack.enter_context(tc.tile_pool(name="scratch", bufs=1)),
            "w_codes": stack.enter_context(tc.tile_pool(name="w_codes", bufs=3)),
            "x": stack.enter_context(tc.tile_pool(name="x", bufs=5)),
            "x_codes": stack.enter_context(tc.tile_pool(name="x_codes", bufs=8)),
            "acc": stack.enter_context(tc.psum_pool(name="acc", bufs=1)),
            "lv": stack.enter_context(tc.psum_pool(name="lv", bufs=1)),
            "mean": stack.enter_context(tc.psum_pool(name="mean", bufs=1)),
            "bank": stack.enter_context(tc.psum_pool(name="bank", bufs=2)),
        }
        const = pools["const"]

        ident = const.tile([P, P], F32, name="ident")
        make_identity(nc, ident[:])
        minus_first = const.tile([P, P], F32, name="minus_first")
        nc.vector.tensor_copy(out=minus_first[:], in_=ident[:])
        nc.vector.tensor_scalar_sub(out=minus_first[0:1, :], in0=ident[0:1, :], scalar1=1.0)
        ident_bf = const.tile([P, P], BF16, name="ident_bf")
        make_identity(nc, ident_bf[:])
        ones = const.tile([P, 1], F32, name="ones")
        nc.vector.memset(ones[:], 1.0)
        ones_bf = const.tile([P, 1], BF16, name="ones_bf")
        nc.vector.memset(ones_bf[:], 1.0)
        score = const.tile([P, P], F32, name="score")
        nc.vector.memset(score[:], 0.0)
        log_weight = const.tile([P, 1], BF16, name="log_weight")
        consts = {
            "ident": ident,
            "minus_first": minus_first,
            "ones": ones,
            "score": score,
            "log_weight": log_weight,
        }

        p_acc = pools["acc"].tile([P, ROWS], F32, name="p_acc")
        q_acc = pools["acc"].tile([P, ROWS], F32, name="q_acc")
        acc = [p_acc, q_acc]
        sums = {
            "columns": pools["acc"].tile([P, LD_COLUMNS], F32, name="columns"),
            "slabs": pools["acc"].tile([P, COMPONENTS], F32, name="slabs"),
            "columns_sb": const.tile([P, LD_COLUMNS + PAIRS], F32, name="columns_sb"),
        }


        stack.enter_context(tc.manual_schedule())

        loaded = {}
        w = {}
        weights = {}
        raw, grouped, x_codes = {}, {}, {}
        quantised_at, weights_at = {}, {}

        def load_weights(q, which, parts=1):
            rows, name = ((log_var_rows, "log_var"), (mean_rows, "mean"))[which]
            natural = pools["load"].tile([P, SPAN], BF16, name=name)
            width = SPAN // parts
            for n in range(parts):
                first = q * SPAN + n * width
                nc.sync.dma_start(
                    out=natural[:, n * width : (n + 1) * width],
                    in_=rows[:, first : first + width],
                )
            loaded[q, which] = natural

        def load_x(j, only=None):
            if j not in raw:
                raw[j] = pools["raw"].tile([P, PACK, ROWS], BF16, name="raw")
            for b in range(BATCH) if only is None else [only]:
                for u in range(WORDS):
                    nc.sync.dma_start(
                        out=raw[j][:, u * HALVES : (u + 1) * HALVES, b * PIXELS : (b + 1) * PIXELS],
                        in_=x_passes[b, j, u, :, :, :],
                    )


        def flip(q, which, pool):
            words = loaded[q, which][:].bitcast(F32)
            bank = pools[pool].tile([P, WORDS, PAIR, COMPONENTS], F32, name=pool + "_bank")
            for g in range(PAIR):
                for u in range(WORDS):
                    first = (g * WORDS + u) * P
                    nc.tensor.transpose(bank[:, u, g, :], words[:, first : first + P], ident[:])
            w[pool, q] = bank

        def inv_var_operand(q):
            w["grouped", q] = pools["weights"].tile(
                [P, 2, PAIR, COMPONENTS * PACK], BF16, name="w_grouped", align_bytes=64
            )
            nc.scalar.activation(
                out=turned_words(w["grouped", q][:, 0, :, :]),
                in_=bank_values(w["lv", q]),
                func=ACT.Exp,
                scale=-1.0,
            )

        def log_var_copy(q):
            by_channel = pools["weights"].tile(
                [P, WORDS, PAIR, COMPONENTS], F32, name="by_channel"
            )
            nc.scalar.copy(out=by_channel[:], in_=w["lv", q][:])
            w["by_channel", q] = by_channel


        def log_det_copied(q, n):
            values = w["by_channel", q][:].bitcast(BF16)
            g, t = divmod(n, PACK)
            column = q // 2 * SLABS_OF_PAIR + n
            nc.tensor.matmul(
                out=sums["columns"][:, column : column + 1],
                lhsT=values[:, t // HALVES, g, t % HALVES :: HALVES],
                rhs=ones_bf[:],
                start=True,
                stop=True,
            )

        def log_det_turned(q, n):
            nc.tensor.matmul(
                out=sums["slabs"][:],
                lhsT=loaded[q, 0][:, n * P : (n + 1) * P],
                rhs=ident_bf[:],
                start=(q == 1 and n == 0),
                stop=(q == PAIRS - 1 and n == SLABS_OF_PAIR - 1),
            )

        def c_column(q):
            column = LD_COLUMNS + q
            return sums["columns_sb"][:, column : column + 1]

        def quantise_weights(q, slot):
            codes = pools["w_codes"].tile(
                [P, 2, PAIR, COMPONENTS], U32, name="w_codes", align_bytes=64
            )
            scales = pools["w_codes"].tile(
                [P, 2, PAIR, COMPONENTS], U8, name="w_scales", align_bytes=64
            )
            nc.vector.quantize_mx(
                out=codes[:].rearrange("p a g m -> p (a g m)").bitcast(FP8X4),
                scales=scales[:].rearrange("p a g m -> p (a g m)"),
                in_=w["grouped", q][:].rearrange("p a g v -> p (a g v)"),
            )
            weights[q] = (codes, scales)
            weights_at[q] = slot


        def natural_inv_var(q, parts=1):
            w["inv_var", q] = pools["weights"].tile([P, SPAN], F32, name="natural_inv_var")
            width = SPAN // parts
            for n in range(parts):
                some = slice(n * width, (n + 1) * width)
                nc.scalar.activation(
                    out=w["inv_var", q][:, some],
                    in_=loaded[q, 0][:, some],
                    func=ACT.Exp,
                    scale=-1.0,
                )

        def natural_mean_iv(q):
            w["mean_iv", q] = pools["weights"].tile([P, SPAN], F32, name="natural_mean_iv")
            nc.vector.tensor_tensor(
                out=w["mean_iv", q][:],
                in0=loaded[q, 1][:],
                in1=w["inv_var", q][:],
                op=ALU.mult,
            )

        def natural_c(q):
            products = pools["scratch"].tile([P, SPAN], F32, name="products")
            nc.vector.scalar_tensor_tensor(
                out=products[:],
                in0=loaded[q, 1][:],
                scalar=1.0,
                in1=w["mean_iv", q][:],
                op0=ALU.mult,
                op1=ALU.mult,
                accum_out=c_column(q),
            )

        def natural_flip(q, g):
            bank = pools["bank"].tile([P, PACK, COMPONENTS], F32, name="mean_iv_bank", tag="bank")
            for t in range(PACK):
                u, e = divmod(t, HALVES)
                first = (g * WORDS + u) * HALVES * P
                nc.tensor.transpose(
                    bank[:, t, :],
                    w["mean_iv", q][:, first + e : first + HALVES * P : HALVES],
                    ident[:],
                )
            w["mean_iv_bank", q, g] = bank

        def natural_operand(q, g):
            nc.scalar.copy(
                out=w["grouped", q][:, 1, g, :].rearrange("p (m t) -> p m t", t=PACK),
                in_=w["mean_iv_bank", q, g][:].rearrange("p t m -> p m t"),
            )


        def turned_inv_var(q):
            w["inv_var", q] = pools["turned"].tile(
                [P, PAIR, COMPONENTS * PACK], F32, name="turned_inv_var"
            )
            nc.scalar.activation(
                out=turned_words(w["inv_var", q][:]),
                in_=bank_values(w["lv", q]),
                func=ACT.Exp,
                scale=-1.0,
            )

        def turned_operand(q):
            nc.vector.tensor_tensor(
                out=turned_words(w["grouped", q][:, 1, :, :]),
                in0=bank_values(w["mean", q]),
                in1=turned_words(w["inv_var", q][:]),
                op=ALU.mult,
            )

        def turned_squares(q):
            w["mean_sq", q] = pools["turned"].tile(
                [P, PACK, PAIR * COMPONENTS], F32, name="mean_sq"
            )
            nc.scalar.activation(
                out=w["mean_sq", q][:].rearrange("p (u e) m -> p u e m", u=WORDS),
                in_=bank_values(w["mean", q]).rearrange("p m u e -> p u e m"),
                func=ACT.Square,
            )

        def turned_c(q, n):
            if n == 0:
                w["diagonal", q] = pools["mean"].tile(
                    [P, COMPONENTS], F32, name="diagonal", tag="mean_bank"
                )
            g, t = divmod(n, PACK)
            columns = slice(g * COMPONENTS, (g + 1) * COMPONENTS)
            nc.tensor.matmul(
                out=w["diagonal", q][:],
                lhsT=w["mean_sq", q][:, t, columns],
                rhs=w["inv_var", q][:, g, t::PACK],
                start=(n == 0),
                stop=(n == SLABS_OF_PAIR - 1),
            )

        def turned_c_out(q):
            on_diagonal = pools["scratch"].tile([P, COMPONENTS], F32, name="on_diagonal")
            nc.vector.scalar_tensor_tensor(
                out=on_diagonal[:],
                in0=w["diagonal", q][:],
                scalar=1.0,
                in1=ident[:],
                op0=ALU.mult,
                op1=ALU.mult,
                accum_out=c_column(q),
            )


        def regroup(j, parts=1):
            grouped[j] = pools["x"].tile(
                [P, 2, ROWS * PACK], BF16, name="x_grouped", align_bytes=64
            )
            out = grouped[j][:, 1, :].rearrange("p (c i t) -> p c t i", i=RUN, t=PACK)
            source = raw[j][:].rearrange("p t (c i) -> p c t i", i=RUN)
            for n in range(parts):
                some = slice(n * ROWS // RUN // parts, (n + 1) * ROWS // RUN // parts)
                nc.vector.tensor_copy(out=out[:, some, :, :], in_=source[:, some, :, :])

        def square(j, on_vector):
            plain = grouped[j][:, 1, :]
            if on_vector:
                nc.vector.tensor_tensor(
                    out=grouped[j][:, 0, :], in0=plain, in1=plain, op=ALU.mult
                )
            else:
                nc.scalar.activation(out=grouped[j][:, 0, :], in_=plain, func=ACT.Square)

        def quantise_x(j, slot, first=0, count=2):
            if j not in x_codes:
                x_codes[j] = (
                    pools["x_codes"].tile([P, 2, ROWS], U32, name="x_codes", align_bytes=64),
                    pools["x_codes"].tile([P, 2, ROWS], U8, name="x_scales", align_bytes=64),
                )
            codes, scales = x_codes[j]
            which = slice(first, first + count)
            nc.vector.quantize_mx(
                out=codes[:, which, :].rearrange("p a r -> p (a r)").bitcast(FP8X4),
                scales=scales[:, which, :].rearrange("p a r -> p (a r)"),
                in_=grouped[j][:, which, :].rearrange("p a v -> p (a v)"),
            )
            quantised_at[j] = slot

        def multiply(j):
            q, g = divmod(j, PAIR)
            w_codes, w_scales = weights[q]
            codes, scales = x_codes[j]
            for which in (1, 0):
                nc.tensor.matmul_mx(
                    out=acc[which][:],
                    lhsT=w_codes[:, which, g, :].bitcast(FP8X4),
                    lhsT_scale=w_scales[:, which, g, :],
                    rhs=codes[:, which, :].bitcast(FP8X4),
                    rhs_scale=scales[:, which, :],
                    start=(j == 0),
                    stop=(j == PASSES - 1),
                )


        x_at = {x_slot(j): j for j in range(PASSES)}
        lead = 4
        load_x(0, 0)
        load_weights(0, 0, 2)
        load_x(0, 1)
        load_weights(1, 0)
        load_x(1)
        load_weights(0, 1)
        load_x(2)
        load_weights(1, 1)
        load_x(3)
        nc.sync.dma_start(out=log_weight[:], in_=log_weights.rearrange("k (m o) -> (k m) o", o=1))
        flip(0, 0, "lv")

        multiplied = 0
        last_slot = x_slot(PASSES - 1)
        fill = []
        for slot in range(last_slot + 4):
            q, second = divmod(slot, PAIR)
            made = []
            j = x_at.get(slot)
            squared = x_at.get(slot - 1)
            finished = x_at.get(slot - 3)
            preparing = q < PAIRS

            if j is not None and j + lead < PASSES:
                load_x(j + lead)
            if not second and q + 2 < PAIRS:
                for which in range(2):
                    load_weights(q + 2, which)

            before = q - 1
            if not second and 0 <= before < PAIRS and natural_pair(before):
                for g in range(PAIR):
                    natural_flip(before, g)
            for step in range(2):
                if (
                    multiplied < PASSES
                    and quantised_at.get(multiplied, slot) < slot
                    and weights_at.get(multiplied // PAIR, slot) < slot
                ):
                    multiply(multiplied)
                    multiplied += 1

            on_vector = squared is not None and vector_squares(squared)
            if on_vector:
                square(squared, True)
            if j is not None:
                regroup(j, BATCH if j == 0 else 1)

            scalar_square = squared is not None and not on_vector
            if preparing and not second:
                if natural_pair(q):
                    natural_inv_var(q, 2 if q == 0 else 1)
                else:
                    turned_inv_var(q)
                inv_var_operand(q)
                if copied_pair(q):
                    log_var_copy(q)
                log_det = log_det_copied if copied_pair(q) else log_det_turned
                made += [(log_det, q, n) for n in range(SLABS_OF_PAIR)]
            elif preparing:
                if natural_pair(q):
                    natural_mean_iv(q)
                else:
                    turned_squares(q)
                    turned_operand(q)
                    made += [(turned_c, q, n) for n in range(SLABS_OF_PAIR)]
            if scalar_square:
                square(squared, False)
            if second and 0 <= before < PAIRS and natural_pair(before):
                for g in range(PAIR):
                    natural_operand(before, g)
            if not second and 0 <= before < PAIRS:
                if natural_pair(before):
                    natural_c(before)
                else:
                    quantise_weights(before, slot)
            if second and 0 <= before - 1 < PAIRS and natural_pair(before - 1):
                quantise_weights(before - 1, slot)
            if not second and 0 <= q - 3 < PAIRS and not natural_pair(q - 3):
                turned_c_out(q - 3)
            if finished == PASSES - 1:
                quantise_x(finished, slot, 1, 1)
                quantise_x(finished, slot, 0, 1)
            elif finished == PASSES - 2:
                shifted = centred_sums(nc, pools, consts, sums)
                quantise_x(finished, slot)
                bias = component_bias(nc, pools, consts, shifted)
            elif finished is not None:
                quantise_x(finished, slot)
            due = fill[:FILL if slot < SLOTS else len(fill)]
            fill = fill[len(due):]
            for make, of_pair, n in due[:BEFORE]:
                make(of_pair, n)
            if second and q + 1 < PAIRS:
                flip(q + 1, 0, "lv")
            if preparing and not second and not natural_pair(q):
                flip(q, 1, "mean")
            for make, of_pair, n in due[BEFORE:]:
                make(of_pair, n)
            fill += made

        while multiplied < PASSES:
            multiply(multiplied)
            multiplied += 1
        anomaly_scores(nc, pools, consts, p_acc, q_acc, bias, out)
